import numpy as np
import ml_dtypes


def mxq(x, axis, fmt="e4m3"):
    dtype, down = {"e4m3": (ml_dtypes.float8_e4m3fn, 7), "e5m2": (ml_dtypes.float8_e5m2, 14)}[fmt]
    v = np.moveaxis(np.asarray(x, np.float32).astype(ml_dtypes.bfloat16).astype(np.float64), axis, -1)
    blocks = v.reshape(v.shape[:-1] + (-1, 32))
    amax = np.abs(blocks).max(-1, keepdims=True)
    byte = np.maximum(np.where(amax > 0, np.frexp(amax)[1] - 1 + 127, 0) - down, 1)
    scale = np.exp2(byte - 127.0)
    codes = (blocks / scale).astype(np.float32).astype(dtype).astype(np.float64)
    return np.moveaxis((codes * scale).reshape(v.shape), -1, axis)


WIDE = False


def mx_kscale(k):
    if not WIDE:
        return np.ones(k)
    levels = np.array([10, -10, 5, -5, 0])
    a = np.random.permutation(np.resize(levels, k // 512 * 4)).reshape(k // 512, 4)
    idx = np.arange(k)
    return np.exp2(a[idx // 512, idx % 128 // 32])


BF16 = ml_dtypes.bfloat16


def bf(x):
    return np.asarray(x, np.float32).astype(BF16)


def f64(x):
    return np.asarray(x).astype(np.float64)


B, C, H, W = 2, 512, 64, 64
OFFSETS = [(-1, 0), (1, 0), (0, -1), (0, 1), (-1, -1), (-1, 1), (1, -1), (1, 1)]


def _neighbor_mean(x):
    p = np.pad(x, ((0, 0), (0, 0), (1, 1), (1, 1)), mode="edge")
    h, w = x.shape[2], x.shape[3]
    s = None
    for dy, dx in OFFSETS:
        sl = p[:, :, 1 + dy:1 + dy + h, 1 + dx:1 + dx + w]
        s = sl if s is None else s + sl
    return s / 8.0


def setup_inputs():
    s = mx_kscale(C)
    s = s / s.max()
    return {"x": bf(np.random.standard_normal((B, C, H, W)) * s[None, :, None, None]),
            "Wp": bf(np.random.standard_normal((C, 2 * C)) / np.sqrt(C) / np.concatenate([s, s])[None, :]),
            "b": bf(np.random.standard_normal(C) * 0.3)}


def reference(x, Wp, b):
    x, Wp, b = f64(x), f64(Wp), f64(b)
    n, c, h, w = x.shape
    mean = _neighbor_mean(x)
    xq = mxq(x, 1, "e4m3").reshape(n, c, h * w)
    mq = mxq(mean, 1, "e4m3").reshape(n, c, h * w)
    out = ((mxq(Wp[:, :c], 1, "e4m3") @ xq)
           + (mxq(Wp[:, c:], 1, "e4m3") @ mq)).reshape(n, c, h, w) + b[None, :, None, None]
    return np.maximum(out, 0.0) + x

@@ -1,0 +1,235 @@
+from contextlib import ExitStack
+
+import concourse.bass as bass
+import concourse.mybir as mybir
+import concourse.tile as tile
+from concourse.masks import make_identity
+
+F32 = mybir.dt.float32
+BF16 = mybir.dt.bfloat16
+U32 = mybir.dt.uint32
+U8 = mybir.dt.uint8
+FP8X4 = mybir.dt.float8_e4m3fn_x4
+ADD = mybir.AluOpType.add
+SUB = mybir.AluOpType.subtract
+ACT = mybir.ActivationFunctionType
+
+P = 128
+PACK = 4
+ROWS = 8
+W_IMG = 64
+H_IMG = 64
+PIX = ROWS * W_IMG
+RL = W_IMG * PACK
+CL = PIX * PACK
+CPI = H_IMG // ROWS
+NCH = 2 * CPI
+
+FLOPS = 2 * 512 * 1024 * 8192
+
+
+def tile_staticgraphmodule_t_kernel(tc, x, Wp, b, out):
+    nc = tc.nc
+    xv = x.rearrange("n (p j) h w -> n p j (h w)", j=PACK)
+    ov = out.rearrange("n (p j) h w -> n p j (h w)", j=PACK)
+
+    with ExitStack() as ctx:
+        const = ctx.enter_context(tc.tile_pool(name="const", bufs=1))
+        xpool = ctx.enter_context(tc.tile_pool(name="xpool", bufs=1))
+        tmp = ctx.enter_context(tc.tile_pool(name="tmp", bufs=1))
+        dbl = ctx.enter_context(tc.tile_pool(name="dbl", bufs=2))
+        tri = ctx.enter_context(tc.tile_pool(name="tri", bufs=3))
+        psum = ctx.enter_context(tc.psum_pool(name="psum", bufs=8))
+        ctx.enter_context(tc.manual_schedule())
+
+        xt = []
+        for c in range(NCH):
+            xt.append(xpool.tile([P, PACK, PIX], BF16, name="xt%d" % c))
+        w_sb = const.tile([P, PACK * 1024], BF16, name="w_sb")
+        b16 = const.tile([P, PACK], BF16, name="b16")
+
+        def load_x(c):
+            n, cc = divmod(c, CPI)
+            nc.sync.dma_start(out=xt[c][:], in_=xv[n, :, :, cc * PIX:(cc + 1) * PIX])
+
+        load_x(0)
+        load_x(1)
+        load_x(2)
+        nc.sync.dma_start(out=w_sb[:], in_=Wp.rearrange("(m j) k -> m (j k)", j=PACK))
+        nc.sync.dma_start(out=b16[:], in_=b.rearrange("(p j) -> p j", j=PACK))
+        for c in range(3, NCH):
+            load_x(c)
+
+        ident = const.tile([P, P], F32, name="ident")
+        make_identity(nc, ident[:])
+
+        x8 = const.tile([P, (H_IMG + 2) * RL], BF16, name="x8")
+        b32 = const.tile([P, PACK], F32, name="b32")
+        wg = const.tile([P, 8 * P * PACK], BF16, name="wg", align_bytes=64)
+        wcodes = const.tile([P, 8 * P], U32, name="wcodes", align_bytes=64)
+        wscales = const.tile([P, 8 * P], U8, name="wscales", align_bytes=64)
+
+        def grouped_view(flat):
+            return flat.rearrange("p (c i t) -> p c t i", i=4, t=PACK)
+
+        def planar_view(pl):
+            return pl.rearrange("p t (c i) -> p c t i", i=4)
+
+        def s_x8(c):
+            cc = c % CPI
+            r0 = 1 + cc * ROWS
+            nc.scalar.mul(grouped_view(x8[:, r0 * RL:(r0 + ROWS) * RL]), planar_view(xt[c][:]), 0.125)
+            if cc == 0:
+                nc.scalar.mul(grouped_view(x8[:, 0:RL]), planar_view(xt[c][:, :, 0:W_IMG]), 0.125)
+            if cc == CPI - 1:
+                nc.scalar.mul(grouped_view(x8[:, (H_IMG + 1) * RL:(H_IMG + 2) * RL]),
+                              planar_view(xt[c][:, :, PIX - W_IMG:PIX]), 0.125)
+
+        xg = {}
+        cv = {}
+        mean = {}
+        xc = {}
+        xs = {}
+        mc = {}
+        ms = {}
+        acc = {}
+        tt = {}
+        scratch = {}
+
+        def s_xg(c):
+            xg[c] = dbl.tile([P, CL], BF16, name="xg", align_bytes=64)
+            nc.scalar.copy(grouped_view(xg[c][:]), planar_view(xt[c][:]))
+
+        def rows2(c, first):
+            r0 = (c % CPI) * ROWS + first
+            return x8[:, r0 * RL:(r0 + ROWS) * RL].rearrange("p (k t c) -> p k t c", t=2, c=RL)
+
+        def v_pv(c):
+            pv = tmp.tile([P, ROWS // 2, RL], F32, name="pv")
+            scratch["pv"] = pv
+            mid = rows2(c, 1)
+            nc.vector.tensor_tensor(out=pv[:], in0=mid[:, :, 0, :], in1=mid[:, :, 1, :], op=ADD)
+
+        def v_cv(c, par):
+            if par == 0:
+                cv[c] = dbl.tile([P, CL], F32, name="cv")
+            cvv = cv[c][:].rearrange("p (k t c) -> p k t c", t=2, c=RL)
+            other = rows2(c, 0)[:, :, 0, :] if par == 0 else rows2(c, 2)[:, :, 1, :]
+            nc.vector.tensor_tensor(out=cvv[:, :, par, :], in0=scratch["pv"][:], in1=other, op=ADD)
+
+        def c4(flat):
+            return flat.rearrange("p (r i t j) -> p r i t j", i=W_IMG // 2, t=2, j=PACK)
+
+        def v_ph(c):
+            ph = tmp.tile([P, ROWS, W_IMG // 2, PACK], F32, name="ph")
+            scratch["ph"] = ph
+            cc4 = c4(cv[c][:])
+            nc.vector.tensor_tensor(out=ph[:], in0=cc4[:, :, :, 0, :], in1=cc4[:, :, :, 1, :], op=ADD)
+
+        def v_box(c, par):
+            if par == 0:
+                scratch["box"] = tmp.tile([P, CL], F32, name="box")
+            b4 = c4(scratch["box"][:])
+            cc4 = c4(cv[c][:])
+            ph = scratch["ph"]
+            h = W_IMG // 2
+            if par == 0:
+                nc.vector.tensor_tensor(out=b4[:, :, 1:h, 0, :], in0=cc4[:, :, 0:h - 1, 1, :],
+                                        in1=ph[:, :, 1:h, :], op=ADD)
+            else:
+                nc.vector.tensor_tensor(out=b4[:, :, 0:h - 1, 1, :], in0=ph[:, :, 0:h - 1, :],
+                                        in1=cc4[:, :, 1:h, 0, :], op=ADD)
+
+        def v_edge(c):
+            bw = scratch["box"][:].rearrange("p (r w j) -> p r w j", w=W_IMG, j=PACK)
+            cw = cv[c][:].rearrange("p (r w j) -> p r w j", w=W_IMG, j=PACK)
+            ph = scratch["ph"]
+            nc.vector.tensor_tensor(out=bw[:, :, 0:W_IMG:W_IMG - 1, :], in0=cw[:, :, 0:W_IMG:W_IMG - 1, :],
+                                    in1=ph[:, :, 0:W_IMG // 2:W_IMG // 2 - 1, :], op=ADD)
+
+        def v_fin(c):
+            mean[c] = dbl.tile([P, CL], BF16, name="mean", align_bytes=64)
+            r0 = 1 + (c % CPI) * ROWS
+            nc.vector.tensor_tensor(out=mean[c][:], in0=scratch["box"][:],
+                                    in1=x8[:, r0 * RL:(r0 + ROWS) * RL], op=SUB)
+
+        def v_q(src, codes, scales, c, nm):
+            codes[c] = tri.tile([P, PIX], U32, name=nm + "c", align_bytes=64)
+            scales[c] = tri.tile([P, PIX], U8, name=nm + "s", align_bytes=64)
+            nc.vector.quantize_mx(out=codes[c][:].bitcast(FP8X4), scales=scales[c][:], in_=src[c][:])
+
+        def pe_mx(c, s):
+            codes, scales = (xc, xs) if s == 0 else (mc, ms)
+            for j in range(PACK):
+                if s == 0:
+                    acc[(c, j)] = psum.tile([P, PIX], F32, name="acc")
+                cols = slice((s * PACK + j) * P, (s * PACK + j + 1) * P)
+                nc.tensor.matmul_mx(out=acc[(c, j)][:],
+                                    lhsT=wcodes[:, cols].bitcast(FP8X4), lhsT_scale=wscales[:, cols],
+                                    rhs=codes[c][:].bitcast(FP8X4), rhs_scale=scales[c][:],
+                                    start=(s == 0), stop=(s == 1))
+
+        def s_relu(c):
+            tt[c] = tri.tile([P, PACK, PIX], F32, name="tt")
+            for j in range(PACK):
+                nc.scalar.activation(out=tt[c][:, j, :], in_=acc[(c, j)][:], func=ACT.Relu,
+                                     bias=b32[:, j:j + 1], scale=1.0)
+
+        def v_res(c):
+            nc.vector.tensor_tensor(out=tt[c][:], in0=tt[c][:], in1=xt[c][:], op=ADD)
+
+        def store(c):
+            n, cc = divmod(c, CPI)
+            nc.sync.dma_start(out=ov[n, :, :, cc * PIX:(cc + 1) * PIX], in_=tt[c][:])
+
+        def w_prep_pe_s():
+            wf = w_sb[:].bitcast(F32).rearrange("p (j s q u) -> p j s q u", j=PACK, s=2, u=2)
+            wgf = wg[:].bitcast(F32).rearrange("p (g m u) -> p g m u", m=P, u=2)
+            for half in range(4):
+                pw = psum.tile([P, 2, 2, P], F32, name="acc")
+                for gi in range(2):
+                    g = half * 2 + gi
+                    s, j = divmod(g, PACK)
+                    for u in range(2):
+                        nc.tensor.transpose(pw[:, gi, u, :], wf[:, j, s, :, u], ident[:])
+                nc.scalar.copy(wgf[:, half * 2:half * 2 + 2, :, :], pw[:].rearrange("p g u m -> p g m u"))
+
+        def ok(c):
+            return 0 <= c < NCH
+
+        s_x8(0)
+        s_x8(1)
+        for s in range(NCH + 3):
+            if ok(s + 2):
+                s_x8(s + 2)
+            if ok(s):
+                s_xg(s)
+            if s == 0:
+                w_prep_pe_s()
+            if ok(s):
+                v_pv(s)
+            if ok(s - 1):
+                v_ph(s - 1)
+            if ok(s):
+                v_cv(s, 0)
+            if ok(s - 1):
+                v_box(s - 1, 0)
+            if ok(s):
+                v_cv(s, 1)
+            if ok(s - 1):
+                v_box(s - 1, 1)
+                v_edge(s - 1)
+                v_q(xg, xc, xs, s - 1, "x")
+                v_fin(s - 1)
+            if s == 1:
+                nc.vector.tensor_copy(out=b32[:], in_=b16[:])
+                nc.vector.quantize_mx(out=wcodes[:].bitcast(FP8X4), scales=wscales[:], in_=wg[:])
+            if ok(s - 1):
+                pe_mx(s - 1, 0)
+            if ok(s - 2):
+                s_relu(s - 2)
+                v_res(s - 2)
+                store(s - 2)
+            if ok(s - 1):
+                v_q(mean, mc, ms, s - 1, "m")
+                pe_mx(s - 1, 1)

@@ -1,8 +1,6 @@
 from contextlib import ExitStack
 
-import concourse.bass as bass
 import concourse.mybir as mybir
-import concourse.tile as tile
 from concourse.masks import make_identity
 
 F32 = mybir.dt.float32
@@ -12,6 +10,7 @@ U8 = mybir.dt.uint8
 FP8X4 = mybir.dt.float8_e4m3fn_x4
 ADD = mybir.AluOpType.add
 SUB = mybir.AluOpType.subtract
+MAX = mybir.AluOpType.max
 ACT = mybir.ActivationFunctionType
 
 P = 128
@@ -22,8 +21,13 @@ H_IMG = 64
 PIX = ROWS * W_IMG
 RL = W_IMG * PACK
 CL = PIX * PACK
+HL = CL // 2
 CPI = H_IMG // ROWS
 NCH = 2 * CPI
+
+PE_FROM = 4
+GP = 8
+GF = 4
 
 FLOPS = 2 * 512 * 1024 * 8192
 
@@ -39,7 +43,8 @@ def tile_staticgraphmodule_t_kernel(tc, x, Wp, b, out):
         tmp = ctx.enter_context(tc.tile_pool(name="tmp", bufs=1))
         dbl = ctx.enter_context(tc.tile_pool(name="dbl", bufs=2))
         tri = ctx.enter_context(tc.tile_pool(name="tri", bufs=3))
-        psum = ctx.enter_context(tc.psum_pool(name="psum", bufs=8))
+        qua = ctx.enter_context(tc.tile_pool(name="qua", bufs=4))
+        psum = ctx.enter_context(tc.psum_pool(name="psum", bufs=4))
         ctx.enter_context(tc.manual_schedule())
 
         xt = []
@@ -54,17 +59,20 @@ def tile_staticgraphmodule_t_kernel(tc, x, Wp, b, out):
 
         load_x(0)
         load_x(1)
+        nc.sync.dma_start(out=b16[:], in_=b.rearrange("(p j) -> p j", j=PACK))
         load_x(2)
         nc.sync.dma_start(out=w_sb[:], in_=Wp.rearrange("(m j) k -> m (j k)", j=PACK))
-        nc.sync.dma_start(out=b16[:], in_=b.rearrange("(p j) -> p j", j=PACK))
         for c in range(3, NCH):
             load_x(c)
 
         ident = const.tile([P, P], F32, name="ident")
         make_identity(nc, ident[:])
+        identb = const.tile([P, P], BF16, name="identb")
+        make_identity(nc, identb[:])
 
         x8 = const.tile([P, (H_IMG + 2) * RL], BF16, name="x8")
         b32 = const.tile([P, PACK], F32, name="b32")
+        nb32 = const.tile([P, PACK], F32, name="nb32")
         wg = const.tile([P, 8 * P * PACK], BF16, name="wg", align_bytes=64)
         wcodes = const.tile([P, 8 * P], U32, name="wcodes", align_bytes=64)
         wscales = const.tile([P, 8 * P], U8, name="wscales", align_bytes=64)
@@ -87,6 +95,7 @@ def tile_staticgraphmodule_t_kernel(tc, x, Wp, b, out):
 
         xg = {}
         cv = {}
+        hb = {}
         mean = {}
         xc = {}
         xs = {}
@@ -94,102 +103,111 @@ def tile_staticgraphmodule_t_kernel(tc, x, Wp, b, out):
         ms = {}
         acc = {}
         tt = {}
-        scratch = {}
+        pvb = {}
 
         def s_xg(c):
             xg[c] = dbl.tile([P, CL], BF16, name="xg", align_bytes=64)
             nc.scalar.copy(grouped_view(xg[c][:]), planar_view(xt[c][:]))
 
+        def s_xb(c):
+            tt[c] = qua.tile([P, PACK, PIX], F32, name="tt")
+            for j in range(PACK):
+                nc.scalar.activation(out=tt[c][:, j, :], in_=xt[c][:, j, :], func=ACT.Identity,
+                                     bias=b32[:, j:j + 1], scale=1.0)
+
         def rows2(c, first):
             r0 = (c % CPI) * ROWS + first
             return x8[:, r0 * RL:(r0 + ROWS) * RL].rearrange("p (k t c) -> p k t c", t=2, c=RL)
 
-        def v_pv(c):
-            pv = tmp.tile([P, ROWS // 2, RL], F32, name="pv")
-            scratch["pv"] = pv
-            mid = rows2(c, 1)
-            nc.vector.tensor_tensor(out=pv[:], in0=mid[:, :, 0, :], in1=mid[:, :, 1, :], op=ADD)
+        def on_pe(c):
+            return PE_FROM <= c < NCH
 
-        def v_cv(c, par):
-            if par == 0:
-                cv[c] = dbl.tile([P, CL], F32, name="cv")
+        def pe_pv(c):
+            mid = rows2(c, 1)
+            for h in range(2):
+                pvb[(c, h)] = psum.tile([P, 2, RL], F32, name="pvb")
+                for t in range(2):
+                    nc.tensor.matmul(out=pvb[(c, h)][:], lhsT=identb[:], rhs=mid[:, 2 * h:2 * h + 2, t, :],
+                                     start=(t == 0), stop=(t == 1))
+
+        def v_cv(c):
+            cv[c] = dbl.tile([P, CL], F32, name="cv")
             cvv = cv[c][:].rearrange("p (k t c) -> p k t c", t=2, c=RL)
-            other = rows2(c, 0)[:, :, 0, :] if par == 0 else rows2(c, 2)[:, :, 1, :]
-            nc.vector.tensor_tensor(out=cvv[:, :, par, :], in0=scratch["pv"][:], in1=other, op=ADD)
+            others = (rows2(c, 0)[:, :, 0, :], rows2(c, 2)[:, :, 1, :])
+            if on_pe(c):
+                for h in range(2):
+                    for par in range(2):
+                        nc.vector.tensor_tensor(out=cvv[:, 2 * h:2 * h + 2, par, :], in0=pvb[(c, h)][:],
+                                                in1=others[par][:, 2 * h:2 * h + 2, :], op=ADD)
+            else:
+                pv = tmp.tile([P, ROWS // 2, RL], F32, name="pv")
+                mid = rows2(c, 1)
+                nc.vector.tensor_tensor(out=pv[:], in0=mid[:, :, 0, :], in1=mid[:, :, 1, :], op=ADD)
+                for par in range(2):
+                    nc.vector.tensor_tensor(out=cvv[:, :, par, :], in0=pv[:], in1=others[par], op=ADD)
 
         def c4(flat):
             return flat.rearrange("p (r i t j) -> p r i t j", i=W_IMG // 2, t=2, j=PACK)
 
-        def v_ph(c):
-            ph = tmp.tile([P, ROWS, W_IMG // 2, PACK], F32, name="ph")
-            scratch["ph"] = ph
-            cc4 = c4(cv[c][:])
-            nc.vector.tensor_tensor(out=ph[:], in0=cc4[:, :, :, 0, :], in1=cc4[:, :, :, 1, :], op=ADD)
+        def ph_of(c):
+            return hb[c][:, 0:HL].rearrange("p (r i j) -> p r i j", i=W_IMG // 2, j=PACK)
 
-        def v_box(c, par):
-            if par == 0:
-                scratch["box"] = tmp.tile([P, CL], F32, name="box")
-            b4 = c4(scratch["box"][:])
+        def ph_rows(eng, c, r0, r1):
+            if r1 > r0:
+                cc4 = c4(cv[c][:])
+                eng.tensor_tensor(out=ph_of(c)[:, r0:r1, :, :], in0=cc4[:, r0:r1, :, 0, :],
+                                  in1=cc4[:, r0:r1, :, 1, :], op=ADD)
+
+        def v_box(c):
+            box = hb[c][:, HL:HL + CL]
+            b4 = c4(box)
             cc4 = c4(cv[c][:])
-            ph = scratch["ph"]
+            ph = ph_of(c)
             h = W_IMG // 2
-            if par == 0:
-                nc.vector.tensor_tensor(out=b4[:, :, 1:h, 0, :], in0=cc4[:, :, 0:h - 1, 1, :],
-                                        in1=ph[:, :, 1:h, :], op=ADD)
-            else:
-                nc.vector.tensor_tensor(out=b4[:, :, 0:h - 1, 1, :], in0=ph[:, :, 0:h - 1, :],
-                                        in1=cc4[:, :, 1:h, 0, :], op=ADD)
-
-        def v_edge(c):
-            bw = scratch["box"][:].rearrange("p (r w j) -> p r w j", w=W_IMG, j=PACK)
+            nc.vector.tensor_tensor(out=b4[:, :, 1:h, 0, :], in0=cc4[:, :, 0:h - 1, 1, :],
+                                    in1=ph[:, :, 1:h, :], op=ADD)
+            nc.vector.tensor_tensor(out=b4[:, :, 0:h - 1, 1, :], in0=ph[:, :, 0:h - 1, :],
+                                    in1=cc4[:, :, 1:h, 0, :], op=ADD)
+            bw = box.rearrange("p (r w j) -> p r w j", w=W_IMG, j=PACK)
             cw = cv[c][:].rearrange("p (r w j) -> p r w j", w=W_IMG, j=PACK)
-            ph = scratch["ph"]
             nc.vector.tensor_tensor(out=bw[:, :, 0:W_IMG:W_IMG - 1, :], in0=cw[:, :, 0:W_IMG:W_IMG - 1, :],
-                                    in1=ph[:, :, 0:W_IMG // 2:W_IMG // 2 - 1, :], op=ADD)
+                                    in1=ph[:, :, 0:h:h - 1, :], op=ADD)
 
-        def v_fin(c):
-            mean[c] = dbl.tile([P, CL], BF16, name="mean", align_bytes=64)
-            r0 = 1 + (c % CPI) * ROWS
-            nc.vector.tensor_tensor(out=mean[c][:], in0=scratch["box"][:],
-                                    in1=x8[:, r0 * RL:(r0 + ROWS) * RL], op=SUB)
+        def fin_rows(eng, c, r0, r1):
+            if r1 > r0:
+                base = (1 + (c % CPI) * ROWS) * RL
+                eng.tensor_tensor(out=mean[c][:, r0 * RL:r1 * RL], in0=hb[c][:, HL + r0 * RL:HL + r1 * RL],
+                                  in1=x8[:, base + r0 * RL:base + r1 * RL], op=SUB)
 
         def v_q(src, codes, scales, c, nm):
             codes[c] = tri.tile([P, PIX], U32, name=nm + "c", align_bytes=64)
             scales[c] = tri.tile([P, PIX], U8, name=nm + "s", align_bytes=64)
             nc.vector.quantize_mx(out=codes[c][:].bitcast(FP8X4), scales=scales[c][:], in_=src[c][:])
 
-        def pe_mx(c, s):
-            codes, scales = (xc, xs) if s == 0 else (mc, ms)
+        def pe_mx(c):
             for j in range(PACK):
-                if s == 0:
-                    acc[(c, j)] = psum.tile([P, PIX], F32, name="acc")
-                cols = slice((s * PACK + j) * P, (s * PACK + j + 1) * P)
-                nc.tensor.matmul_mx(out=acc[(c, j)][:],
-                                    lhsT=wcodes[:, cols].bitcast(FP8X4), lhsT_scale=wscales[:, cols],
-                                    rhs=codes[c][:].bitcast(FP8X4), rhs_scale=scales[c][:],
-                                    start=(s == 0), stop=(s == 1))
+                acc[(c, j)] = psum.tile([P, PIX], F32, name="acc")
+                for s, codes, scales in ((0, xc, xs), (1, mc, ms)):
+                    cols = slice((s * PACK + j) * P, (s * PACK + j + 1) * P)
+                    nc.tensor.matmul_mx(out=acc[(c, j)][:],
+                                        lhsT=wcodes[:, cols].bitcast(FP8X4), lhsT_scale=wscales[:, cols],
+                                        rhs=codes[c][:].bitcast(FP8X4), rhs_scale=scales[c][:],
+                                        start=(s == 0), stop=(s == 1))
 
-        def s_relu(c):
-            tt[c] = tri.tile([P, PACK, PIX], F32, name="tt")
-            for j in range(PACK):
-                nc.scalar.activation(out=tt[c][:, j, :], in_=acc[(c, j)][:], func=ACT.Relu,
-                                     bias=b32[:, j:j + 1], scale=1.0)
-
-        def v_res(c):
-            nc.vector.tensor_tensor(out=tt[c][:], in0=tt[c][:], in1=xt[c][:], op=ADD)
-
-        def store(c):
+        def v_res_store(c):
             n, cc = divmod(c, CPI)
+            for j in range(PACK):
+                nc.vector.scalar_tensor_tensor(out=tt[c][:, j, :], in0=acc[(c, j)][:], scalar=nb32[:, j:j + 1],
+                                               in1=tt[c][:, j, :], op0=MAX, op1=ADD)
             nc.sync.dma_start(out=ov[n, :, :, cc * PIX:(cc + 1) * PIX], in_=tt[c][:])
 
-        def w_prep_pe_s():
+        def w_transposes():
             wf = w_sb[:].bitcast(F32).rearrange("p (j s q u) -> p j s q u", j=PACK, s=2, u=2)
             wgf = wg[:].bitcast(F32).rearrange("p (g m u) -> p g m u", m=P, u=2)
             for half in range(4):
                 pw = psum.tile([P, 2, 2, P], F32, name="acc")
                 for gi in range(2):
-                    g = half * 2 + gi
-                    s, j = divmod(g, PACK)
+                    s, j = divmod(half * 2 + gi, PACK)
                     for u in range(2):
                         nc.tensor.transpose(pw[:, gi, u, :], wf[:, j, s, :, u], ident[:])
                 nc.scalar.copy(wgf[:, half * 2:half * 2 + 2, :, :], pw[:].rearrange("p g u m -> p g m u"))
@@ -197,39 +215,41 @@ def tile_staticgraphmodule_t_kernel(tc, x, Wp, b, out):
         def ok(c):
             return 0 <= c < NCH
 
+        nc.vector.tensor_copy(out=b32[:], in_=b16[:])
+        nc.vector.tensor_scalar_mul(nb32[:], b16[:], -1.0)
         s_x8(0)
         s_x8(1)
-        for s in range(NCH + 3):
+        for s in range(NCH + 4):
             if ok(s + 2):
                 s_x8(s + 2)
             if ok(s):
                 s_xg(s)
-            if s == 0:
-                w_prep_pe_s()
-            if ok(s):
-                v_pv(s)
-            if ok(s - 1):
-                v_ph(s - 1)
-            if ok(s):
-                v_cv(s, 0)
-            if ok(s - 1):
-                v_box(s - 1, 0)
-            if ok(s):
-                v_cv(s, 1)
-            if ok(s - 1):
-                v_box(s - 1, 1)
-                v_edge(s - 1)
-                v_q(xg, xc, xs, s - 1, "x")
-                v_fin(s - 1)
             if s == 1:
-                nc.vector.tensor_copy(out=b32[:], in_=b16[:])
+                w_transposes()
+            if ok(s - 1):
+                s_xb(s - 1)
+            if on_pe(s + 1):
+                pe_pv(s + 1)
+            if ok(s):
+                v_cv(s)
+            c = s - 1
+            if ok(c):
+                hb[c] = tmp.tile([P, HL + CL], F32, name="hb")
+                gp = GP if on_pe(s) else 0
+                ph_rows(nc.gpsimd, c, 0, gp)
+                v_q(xg, xc, xs, c, "x")
+                ph_rows(nc.vector, c, gp, ROWS)
+                v_box(c)
+            if s == 2:
                 nc.vector.quantize_mx(out=wcodes[:].bitcast(FP8X4), scales=wscales[:], in_=wg[:])
-            if ok(s - 1):
-                pe_mx(s - 1, 0)
             if ok(s - 2):
-                s_relu(s - 2)
-                v_res(s - 2)
-                store(s - 2)
-            if ok(s - 1):
-                v_q(mean, mc, ms, s - 1, "m")
-                pe_mx(s - 1, 1)
+                v_q(mean, mc, ms, s - 2, "m")
+                pe_mx(s - 2)
+            if ok(c):
+                mean[c] = tri.tile([P, CL], BF16, name="mean", align_bytes=64)
+                gf = GF if ok(s - 3) else 0
+                fin_rows(nc.gpsimd, c, 0, gf)
+            if ok(s - 3):
+                v_res_store(s - 3)
+            if ok(c):
+                fin_rows(nc.vector, c, gf, ROWS)

@@ -199,7 +199,10 @@ def tile_staticgraphmodule_t_kernel(tc, x, Wp, b, out):
             for j in range(PACK):
                 nc.vector.scalar_tensor_tensor(out=tt[c][:, j, :], in0=acc[(c, j)][:], scalar=nb32[:, j:j + 1],
                                                in1=tt[c][:, j, :], op0=MAX, op1=ADD)
-            nc.sync.dma_start(out=ov[n, :, :, cc * PIX:(cc + 1) * PIX], in_=tt[c][:])
+                if c == NCH - 1:
+                    nc.sync.dma_start(out=ov[n, :, j, cc * PIX:(cc + 1) * PIX], in_=tt[c][:, j, :])
+            if c < NCH - 1:
+                nc.sync.dma_start(out=ov[n, :, :, cc * PIX:(cc + 1) * PIX], in_=tt[c][:])
 
         def w_transposes():
             wf = w_sb[:].bitcast(F32).rearrange("p (j s q u) -> p j s q u", j=PACK, s=2, u=2)
@@ -219,7 +222,8 @@ def tile_staticgraphmodule_t_kernel(tc, x, Wp, b, out):
         nc.vector.tensor_scalar_mul(nb32[:], b16[:], -1.0)
         s_x8(0)
         s_x8(1)
-        for s in range(NCH + 4):
+        gps = {}
+        for s in range(NCH + 2):
             if ok(s + 2):
                 s_x8(s + 2)
             if ok(s):
@@ -232,24 +236,23 @@ def tile_staticgraphmodule_t_kernel(tc, x, Wp, b, out):
                 pe_pv(s + 1)
             if ok(s):
                 v_cv(s)
-            c = s - 1
-            if ok(c):
-                hb[c] = tmp.tile([P, HL + CL], F32, name="hb")
-                gp = GP if on_pe(s) else 0
-                ph_rows(nc.gpsimd, c, 0, gp)
-                v_q(xg, xc, xs, c, "x")
-                ph_rows(nc.vector, c, gp, ROWS)
-                v_box(c)
             if s == 2:
                 nc.vector.quantize_mx(out=wcodes[:].bitcast(FP8X4), scales=wscales[:], in_=wg[:])
             if ok(s - 2):
                 v_q(mean, mc, ms, s - 2, "m")
                 pe_mx(s - 2)
+            c = s - 1
             if ok(c):
+                ph_rows(nc.vector, c, gps[c], ROWS)
+                v_box(c)
+                v_q(xg, xc, xs, c, "x")
                 mean[c] = tri.tile([P, CL], BF16, name="mean", align_bytes=64)
-                gf = GF if ok(s - 3) else 0
-                fin_rows(nc.gpsimd, c, 0, gf)
-            if ok(s - 3):
-                v_res_store(s - 3)
-            if ok(c):
+                gf = GF if ok(s - 2) else 0
                 fin_rows(nc.vector, c, gf, ROWS)
+                fin_rows(nc.gpsimd, c, 0, gf)
+            if ok(s - 2):
+                v_res_store(s - 2)
+            if ok(s):
+                hb[s] = tmp.tile([P, HL + CL], F32, name="hb")
+                gps[s] = GP if on_pe(s + 1) else 0
+                ph_rows(nc.gpsimd, s, 0, gps[s])

@@ -9,8 +9,8 @@ U32 = mybir.dt.uint32
 U8 = mybir.dt.uint8
 FP8X4 = mybir.dt.float8_e4m3fn_x4
 ADD = mybir.AluOpType.add
-SUB = mybir.AluOpType.subtract
 MAX = mybir.AluOpType.max
+MULT = mybir.AluOpType.mult
 ACT = mybir.ActivationFunctionType
 
 P = 128
@@ -22,12 +22,10 @@ PIX = ROWS * W_IMG
 RL = W_IMG * PACK
 CL = PIX * PACK
 HL = CL // 2
+PRL = (W_IMG + 2) * PACK
 CPI = H_IMG // ROWS
 NCH = 2 * CPI
-
 PE_FROM = 4
-GP = 8
-GF = 4
 
 FLOPS = 2 * 512 * 1024 * 8192
 
@@ -43,8 +41,9 @@ def tile_staticgraphmodule_t_kernel(tc, x, Wp, b, out):
         tmp = ctx.enter_context(tc.tile_pool(name="tmp", bufs=1))
         dbl = ctx.enter_context(tc.tile_pool(name="dbl", bufs=2))
         tri = ctx.enter_context(tc.tile_pool(name="tri", bufs=3))
-        qua = ctx.enter_context(tc.tile_pool(name="qua", bufs=4))
-        psum = ctx.enter_context(tc.psum_pool(name="psum", bufs=4))
+        ps1 = ctx.enter_context(tc.psum_pool(name="ps1", bufs=1))
+        ps2 = ctx.enter_context(tc.psum_pool(name="ps2", bufs=2))
+        ps3 = ctx.enter_context(tc.psum_pool(name="ps3", bufs=3))
         ctx.enter_context(tc.manual_schedule())
 
         xt = []
@@ -69,8 +68,9 @@ def tile_staticgraphmodule_t_kernel(tc, x, Wp, b, out):
         make_identity(nc, ident[:])
         identb = const.tile([P, P], BF16, name="identb")
         make_identity(nc, identb[:])
+        i8b = const.tile([P, P], BF16, name="i8b")
 
-        x8 = const.tile([P, (H_IMG + 2) * RL], BF16, name="x8")
+        xgi = const.tile([P, (H_IMG + 2) * RL], BF16, name="xgi", align_bytes=64)
         b32 = const.tile([P, PACK], F32, name="b32")
         nb32 = const.tile([P, PACK], F32, name="nb32")
         wg = const.tile([P, 8 * P * PACK], BF16, name="wg", align_bytes=64)
@@ -83,19 +83,9 @@ def tile_staticgraphmodule_t_kernel(tc, x, Wp, b, out):
         def planar_view(pl):
             return pl.rearrange("p t (c i) -> p c t i", i=4)
 
-        def s_x8(c):
-            cc = c % CPI
-            r0 = 1 + cc * ROWS
-            nc.scalar.mul(grouped_view(x8[:, r0 * RL:(r0 + ROWS) * RL]), planar_view(xt[c][:]), 0.125)
-            if cc == 0:
-                nc.scalar.mul(grouped_view(x8[:, 0:RL]), planar_view(xt[c][:, :, 0:W_IMG]), 0.125)
-            if cc == CPI - 1:
-                nc.scalar.mul(grouped_view(x8[:, (H_IMG + 1) * RL:(H_IMG + 2) * RL]),
-                              planar_view(xt[c][:, :, PIX - W_IMG:PIX]), 0.125)
-
-        xg = {}
         cv = {}
-        hb = {}
+        ph = {}
+        box = {}
         mean = {}
         xc = {}
         xs = {}
@@ -104,89 +94,63 @@ def tile_staticgraphmodule_t_kernel(tc, x, Wp, b, out):
         acc = {}
         tt = {}
         pvb = {}
+        xtr = {}
+        xps = {}
+
+        def ok(c):
+            return 0 <= c < NCH
+
+        def on_pe(c):
+            return PE_FROM <= c < NCH
+
+        def base_of(c):
+            return (1 + (c % CPI) * ROWS) * RL
 
         def s_xg(c):
-            xg[c] = dbl.tile([P, CL], BF16, name="xg", align_bytes=64)
-            nc.scalar.copy(grouped_view(xg[c][:]), planar_view(xt[c][:]))
+            cc = c % CPI
+            nc.scalar.copy(grouped_view(xgi[:, base_of(c):base_of(c) + CL]), planar_view(xt[c][:]))
+            if cc == 0:
+                nc.scalar.copy(grouped_view(xgi[:, 0:RL]), planar_view(xt[c][:, :, 0:W_IMG]))
+            if cc == CPI - 1:
+                nc.scalar.copy(grouped_view(xgi[:, (H_IMG + 1) * RL:(H_IMG + 2) * RL]),
+                               planar_view(xt[c][:, :, PIX - W_IMG:PIX]))
 
         def s_xb(c):
-            tt[c] = qua.tile([P, PACK, PIX], F32, name="tt")
+            tt[c] = tri.tile([P, PACK, PIX], F32, name="tt")
             for j in range(PACK):
                 nc.scalar.activation(out=tt[c][:, j, :], in_=xt[c][:, j, :], func=ACT.Identity,
                                      bias=b32[:, j:j + 1], scale=1.0)
 
         def rows2(c, first):
             r0 = (c % CPI) * ROWS + first
-            return x8[:, r0 * RL:(r0 + ROWS) * RL].rearrange("p (k t c) -> p k t c", t=2, c=RL)
-
-        def on_pe(c):
-            return PE_FROM <= c < NCH
+            return xgi[:, r0 * RL:(r0 + ROWS) * RL].rearrange("p (k t c) -> p k t c", t=2, c=RL)
 
         def pe_pv(c):
             mid = rows2(c, 1)
             for h in range(2):
-                pvb[(c, h)] = psum.tile([P, 2, RL], F32, name="pvb")
+                pvb[(c, h)] = ps2.tile([P, 2, RL], F32, name="pvb")
                 for t in range(2):
-                    nc.tensor.matmul(out=pvb[(c, h)][:], lhsT=identb[:], rhs=mid[:, 2 * h:2 * h + 2, t, :],
+                    nc.tensor.matmul(out=pvb[(c, h)][:], lhsT=i8b[:], rhs=mid[:, 2 * h:2 * h + 2, t, :],
                                      start=(t == 0), stop=(t == 1))
 
-        def v_cv(c):
-            cv[c] = dbl.tile([P, CL], F32, name="cv")
-            cvv = cv[c][:].rearrange("p (k t c) -> p k t c", t=2, c=RL)
-            others = (rows2(c, 0)[:, :, 0, :], rows2(c, 2)[:, :, 1, :])
-            if on_pe(c):
-                for h in range(2):
-                    for par in range(2):
-                        nc.vector.tensor_tensor(out=cvv[:, 2 * h:2 * h + 2, par, :], in0=pvb[(c, h)][:],
-                                                in1=others[par][:, 2 * h:2 * h + 2, :], op=ADD)
-            else:
-                pv = tmp.tile([P, ROWS // 2, RL], F32, name="pv")
-                mid = rows2(c, 1)
-                nc.vector.tensor_tensor(out=pv[:], in0=mid[:, :, 0, :], in1=mid[:, :, 1, :], op=ADD)
-                for par in range(2):
-                    nc.vector.tensor_tensor(out=cvv[:, :, par, :], in0=pv[:], in1=others[par], op=ADD)
+        def pe_t1_s_evac(c):
+            xw = xgi[:, base_of(c):base_of(c) + CL].bitcast(F32)
+            xtr[c] = dbl.tile([P, HL], F32, name="xtr")
+            for r in range(2):
+                t1 = ps1.tile([P, 4, P], F32, name="t1")
+                for q in range(4):
+                    nc.tensor.transpose(t1[:, q, :], xw[:, (4 * r + q) * P:(4 * r + q + 1) * P], ident[:])
+                nc.scalar.copy(xtr[c][:, r * 512:(r + 1) * 512], t1[:].rearrange("p q m -> p (q m)"))
 
-        def c4(flat):
-            return flat.rearrange("p (r i t j) -> p r i t j", i=W_IMG // 2, t=2, j=PACK)
-
-        def ph_of(c):
-            return hb[c][:, 0:HL].rearrange("p (r i j) -> p r i j", i=W_IMG // 2, j=PACK)
-
-        def ph_rows(eng, c, r0, r1):
-            if r1 > r0:
-                cc4 = c4(cv[c][:])
-                eng.tensor_tensor(out=ph_of(c)[:, r0:r1, :, :], in0=cc4[:, r0:r1, :, 0, :],
-                                  in1=cc4[:, r0:r1, :, 1, :], op=ADD)
-
-        def v_box(c):
-            box = hb[c][:, HL:HL + CL]
-            b4 = c4(box)
-            cc4 = c4(cv[c][:])
-            ph = ph_of(c)
-            h = W_IMG // 2
-            nc.vector.tensor_tensor(out=b4[:, :, 1:h, 0, :], in0=cc4[:, :, 0:h - 1, 1, :],
-                                    in1=ph[:, :, 1:h, :], op=ADD)
-            nc.vector.tensor_tensor(out=b4[:, :, 0:h - 1, 1, :], in0=ph[:, :, 0:h - 1, :],
-                                    in1=cc4[:, :, 1:h, 0, :], op=ADD)
-            bw = box.rearrange("p (r w j) -> p r w j", w=W_IMG, j=PACK)
-            cw = cv[c][:].rearrange("p (r w j) -> p r w j", w=W_IMG, j=PACK)
-            nc.vector.tensor_tensor(out=bw[:, :, 0:W_IMG:W_IMG - 1, :], in0=cw[:, :, 0:W_IMG:W_IMG - 1, :],
-                                    in1=ph[:, :, 0:h:h - 1, :], op=ADD)
-
-        def fin_rows(eng, c, r0, r1):
-            if r1 > r0:
-                base = (1 + (c % CPI) * ROWS) * RL
-                eng.tensor_tensor(out=mean[c][:, r0 * RL:r1 * RL], in0=hb[c][:, HL + r0 * RL:HL + r1 * RL],
-                                  in1=x8[:, base + r0 * RL:base + r1 * RL], op=SUB)
-
-        def v_q(src, codes, scales, c, nm):
-            codes[c] = tri.tile([P, PIX], U32, name=nm + "c", align_bytes=64)
-            scales[c] = tri.tile([P, PIX], U8, name=nm + "s", align_bytes=64)
-            nc.vector.quantize_mx(out=codes[c][:].bitcast(FP8X4), scales=scales[c][:], in_=src[c][:])
+        def pe_t2(c):
+            for r in range(2):
+                xps[(c, r)] = ps2.tile([P, 4, P], F32, name="xps")
+                for q in range(4):
+                    nc.tensor.transpose(xps[(c, r)][:, q, :], xtr[c][:, (4 * r + q) * P:(4 * r + q + 1) * P], ident[:])
 
         def pe_mx(c):
             for j in range(PACK):
-                acc[(c, j)] = psum.tile([P, PIX], F32, name="acc")
+                acc[(c, j)] = ps3.tile([P, PIX], F32, name="acc")
                 for s, codes, scales in ((0, xc, xs), (1, mc, ms)):
                     cols = slice((s * PACK + j) * P, (s * PACK + j + 1) * P)
                     nc.tensor.matmul_mx(out=acc[(c, j)][:],
@@ -194,65 +158,112 @@ def tile_staticgraphmodule_t_kernel(tc, x, Wp, b, out):
                                         rhs=codes[c][:].bitcast(FP8X4), rhs_scale=scales[c][:],
                                         start=(s == 0), stop=(s == 1))
 
-        def v_res_store(c):
-            n, cc = divmod(c, CPI)
-            for j in range(PACK):
-                nc.vector.scalar_tensor_tensor(out=tt[c][:, j, :], in0=acc[(c, j)][:], scalar=nb32[:, j:j + 1],
-                                               in1=tt[c][:, j, :], op0=MAX, op1=ADD)
-                if c == NCH - 1:
-                    nc.sync.dma_start(out=ov[n, :, j, cc * PIX:(cc + 1) * PIX], in_=tt[c][:, j, :])
-            if c < NCH - 1:
-                nc.sync.dma_start(out=ov[n, :, :, cc * PIX:(cc + 1) * PIX], in_=tt[c][:])
-
         def w_transposes():
             wf = w_sb[:].bitcast(F32).rearrange("p (j s q u) -> p j s q u", j=PACK, s=2, u=2)
             wgf = wg[:].bitcast(F32).rearrange("p (g m u) -> p g m u", m=P, u=2)
             for half in range(4):
-                pw = psum.tile([P, 2, 2, P], F32, name="acc")
+                pw = ps3.tile([P, 2, 2, P], F32, name="acc")
                 for gi in range(2):
                     s, j = divmod(half * 2 + gi, PACK)
                     for u in range(2):
                         nc.tensor.transpose(pw[:, gi, u, :], wf[:, j, s, :, u], ident[:])
                 nc.scalar.copy(wgf[:, half * 2:half * 2 + 2, :, :], pw[:].rearrange("p g u m -> p g m u"))
 
-        def ok(c):
-            return 0 <= c < NCH
+        def v_cv(c):
+            cv[c] = dbl.tile([P, ROWS, PRL], F32, name="cv")
+            cvk = cv[c][:].rearrange("p (k t) c -> p k t c", t=2)
+            others = (rows2(c, 0)[:, :, 0, :], rows2(c, 2)[:, :, 1, :])
+            if on_pe(c):
+                for h in range(2):
+                    for par in range(2):
+                        nc.vector.scalar_tensor_tensor(out=cvk[:, 2 * h:2 * h + 2, par, PACK:PACK + RL],
+                                                       in0=others[par][:, 2 * h:2 * h + 2, :], scalar=0.125,
+                                                       in1=pvb[(c, h)][:], op0=MULT, op1=ADD)
+            else:
+                hrow = tmp.tile([P, ROWS // 2, RL], BF16, name="hrow")
+                nc.vector.tensor_scalar_mul(hrow[:], rows2(c, 1)[:, :, 1, :], 0.125)
+                pv = tmp.tile([P, ROWS // 2, RL], F32, name="pv")
+                nc.vector.scalar_tensor_tensor(out=pv[:], in0=rows2(c, 1)[:, :, 0, :], scalar=0.125,
+                                               in1=hrow[:], op0=MULT, op1=ADD)
+                for par in range(2):
+                    nc.vector.scalar_tensor_tensor(out=cvk[:, :, par, PACK:PACK + RL], in0=others[par], scalar=0.125,
+                                                   in1=pv[:], op0=MULT, op1=ADD)
+
+        def v_pad(c):
+            cvw = cv[c][:].rearrange("p r (w j) -> p r w j", j=PACK)
+            nc.vector.tensor_copy(out=cvw[:, :, 0:W_IMG + 2:W_IMG + 1, :], in_=cvw[:, :, 1:W_IMG + 1:W_IMG - 1, :])
+
+        def pairs(c, first):
+            return cv[c][:, :, first * PACK:first * PACK + RL].rearrange("p r (i t j) -> p r i t j", t=2, j=PACK)
+
+        def ph_sums(eng, c):
+            ph[c] = tmp.tile([P, ROWS, W_IMG // 2, PACK], F32, name="ph")
+            eng.tensor_tensor(out=ph[c][:], in0=pairs(c, 1)[:, :, :, 0, :], in1=pairs(c, 1)[:, :, :, 1, :], op=ADD)
+
+        def box_sums(eng, c):
+            box[c] = dbl.tile([P, CL], F32, name="box")
+            b4 = box[c][:].rearrange("p (r i t j) -> p r i t j", i=W_IMG // 2, t=2, j=PACK)
+            eng.tensor_tensor(out=b4[:, :, :, 0, :], in0=pairs(c, 0)[:, :, :, 0, :], in1=ph[c][:], op=ADD)
+            eng.tensor_tensor(out=b4[:, :, :, 1, :], in0=ph[c][:], in1=pairs(c, 2)[:, :, :, 1, :], op=ADD)
+
+        def v_fin(c, r):
+            if ok(c):
+                if r == 0:
+                    mean[c] = dbl.tile([P, CL], BF16, name="mean", align_bytes=64)
+                nc.vector.scalar_tensor_tensor(out=mean[c][:, r * HL:(r + 1) * HL],
+                                               in0=xps[(c, r)][:].rearrange("p q m -> p (q m)").bitcast(BF16),
+                                               scalar=-0.125, in1=box[c][:, r * HL:(r + 1) * HL], op0=MULT, op1=ADD)
+
+        def v_q(src, codes, scales, c, nm):
+            codes[c] = tri.tile([P, PIX], U32, name=nm + "c", align_bytes=64)
+            scales[c] = tri.tile([P, PIX], U8, name=nm + "s", align_bytes=64)
+            nc.vector.quantize_mx(out=codes[c][:].bitcast(FP8X4), scales=scales[c][:], in_=src)
+
+        def v_res_store(c, js):
+            n, cc = divmod(c, CPI)
+            for j in js if ok(c) else ():
+                nc.vector.scalar_tensor_tensor(out=tt[c][:, j, :], in0=acc[(c, j)][:], scalar=nb32[:, j:j + 1],
+                                               in1=tt[c][:, j, :], op0=MAX, op1=ADD)
+                if c == NCH - 1:
+                    nc.sync.dma_start(out=ov[n, :, j, cc * PIX:(cc + 1) * PIX], in_=tt[c][:, j, :])
+            if ok(c) and c < NCH - 1 and PACK - 1 in js:
+                nc.sync.dma_start(out=ov[n, :, :, cc * PIX:(cc + 1) * PIX], in_=tt[c][:])
 
         nc.vector.tensor_copy(out=b32[:], in_=b16[:])
         nc.vector.tensor_scalar_mul(nb32[:], b16[:], -1.0)
-        s_x8(0)
-        s_x8(1)
-        gps = {}
-        for s in range(NCH + 2):
+        nc.vector.tensor_scalar_mul(i8b[:], identb[:], 0.125)
+        s_xg(0)
+        s_xg(1)
+        for s in range(NCH + 3):
             if ok(s + 2):
-                s_x8(s + 2)
-            if ok(s):
-                s_xg(s)
+                s_xg(s + 2)
             if s == 1:
                 w_transposes()
+            if ok(s - 2):
+                s_xb(s - 2)
+                pe_t2(s - 2)
             if ok(s - 1):
-                s_xb(s - 1)
-            if on_pe(s + 1):
-                pe_pv(s + 1)
-            if ok(s):
-                v_cv(s)
+                v_q(xgi[:, base_of(s - 1):base_of(s - 1) + CL], xc, xs, s - 1, "x")
             if s == 2:
                 nc.vector.quantize_mx(out=wcodes[:].bitcast(FP8X4), scales=wscales[:], in_=wg[:])
-            if ok(s - 2):
-                v_q(mean, mc, ms, s - 2, "m")
-                pe_mx(s - 2)
-            c = s - 1
-            if ok(c):
-                ph_rows(nc.vector, c, gps[c], ROWS)
-                v_box(c)
-                v_q(xg, xc, xs, c, "x")
-                mean[c] = tri.tile([P, CL], BF16, name="mean", align_bytes=64)
-                gf = GF if ok(s - 2) else 0
-                fin_rows(nc.vector, c, gf, ROWS)
-                fin_rows(nc.gpsimd, c, 0, gf)
-            if ok(s - 2):
-                v_res_store(s - 2)
+            if ok(s - 3):
+                v_q(mean[s - 3][:], mc, ms, s - 3, "m")
+                pe_mx(s - 3)
+            if ok(s - 1):
+                v_pad(s - 1)
+                if not on_pe(s):
+                    box_sums(nc.vector, s - 1)
             if ok(s):
-                hb[s] = tmp.tile([P, HL + CL], F32, name="hb")
-                gps[s] = GP if on_pe(s + 1) else 0
-                ph_rows(nc.gpsimd, s, 0, gps[s])
+                v_cv(s)
+            if ok(s - 1) and on_pe(s):
+                box_sums(nc.gpsimd, s - 1)
+            if on_pe(s + 1):
+                pe_pv(s + 1)
+            if ok(s - 1):
+                pe_t1_s_evac(s - 1)
+            v_fin(s - 2, 0)
+            v_res_store(s - 3, (0, 1))
+            v_fin(s - 2, 1)
+            v_res_store(s - 3, (2, 3))
+            if ok(s):
+                ph_sums(nc.gpsimd if s > 0 else nc.vector, s)

@@ -26,6 +26,7 @@ PRL = (W_IMG + 2) * PACK
 CPI = H_IMG // ROWS
 NCH = 2 * CPI
 PE_FROM = 4
+VB = 2
 
 FLOPS = 2 * 512 * 1024 * 8192
 
@@ -133,10 +134,11 @@ def tile_staticgraphmodule_t_kernel(tc, x, Wp, b, out):
                     nc.tensor.matmul(out=pvb[(c, h)][:], lhsT=i8b[:], rhs=mid[:, 2 * h:2 * h + 2, t, :],
                                      start=(t == 0), stop=(t == 1))
 
-        def pe_t1_s_evac(c):
+        def pe_t1_s_evac(c, r):
             xw = xgi[:, base_of(c):base_of(c) + CL].bitcast(F32)
-            xtr[c] = dbl.tile([P, HL], F32, name="xtr")
-            for r in range(2):
+            if r == 0:
+                xtr[c] = dbl.tile([P, HL], F32, name="xtr")
+            if r >= 0:
                 t1 = ps1.tile([P, 4, P], F32, name="t1")
                 for q in range(4):
                     nc.tensor.transpose(t1[:, q, :], xw[:, (4 * r + q) * P:(4 * r + q + 1) * P], ident[:])
@@ -148,8 +150,8 @@ def tile_staticgraphmodule_t_kernel(tc, x, Wp, b, out):
                 for q in range(4):
                     nc.tensor.transpose(xps[(c, r)][:, q, :], xtr[c][:, (4 * r + q) * P:(4 * r + q + 1) * P], ident[:])
 
-        def pe_mx(c):
-            for j in range(PACK):
+        def pe_mx(c, js):
+            for j in js:
                 acc[(c, j)] = ps3.tile([P, PIX], F32, name="acc")
                 for s, codes, scales in ((0, xc, xs), (1, mc, ms)):
                     cols = slice((s * PACK + j) * P, (s * PACK + j + 1) * P)
@@ -189,9 +191,9 @@ def tile_staticgraphmodule_t_kernel(tc, x, Wp, b, out):
                     nc.vector.scalar_tensor_tensor(out=cvk[:, :, par, PACK:PACK + RL], in0=others[par], scalar=0.125,
                                                    in1=pv[:], op0=MULT, op1=ADD)
 
-        def v_pad(c):
+        def v_pad(c, r0, r1):
             cvw = cv[c][:].rearrange("p r (w j) -> p r w j", j=PACK)
-            nc.vector.tensor_copy(out=cvw[:, :, 0:W_IMG + 2:W_IMG + 1, :], in_=cvw[:, :, 1:W_IMG + 1:W_IMG - 1, :])
+            nc.vector.tensor_copy(out=cvw[:, r0:r1, 0:W_IMG + 2:W_IMG + 1, :], in_=cvw[:, r0:r1, 1:W_IMG + 1:W_IMG - 1, :])
 
         def pairs(c, first):
             return cv[c][:, :, first * PACK:first * PACK + RL].rearrange("p r (i t j) -> p r i t j", t=2, j=PACK)
@@ -200,11 +202,10 @@ def tile_staticgraphmodule_t_kernel(tc, x, Wp, b, out):
             ph[c] = tmp.tile([P, ROWS, W_IMG // 2, PACK], F32, name="ph")
             eng.tensor_tensor(out=ph[c][:], in0=pairs(c, 1)[:, :, :, 0, :], in1=pairs(c, 1)[:, :, :, 1, :], op=ADD)
 
-        def box_sums(eng, c):
-            box[c] = dbl.tile([P, CL], F32, name="box")
+        def box_sums(eng, c, r0, r1):
             b4 = box[c][:].rearrange("p (r i t j) -> p r i t j", i=W_IMG // 2, t=2, j=PACK)
-            eng.tensor_tensor(out=b4[:, :, :, 0, :], in0=pairs(c, 0)[:, :, :, 0, :], in1=ph[c][:], op=ADD)
-            eng.tensor_tensor(out=b4[:, :, :, 1, :], in0=ph[c][:], in1=pairs(c, 2)[:, :, :, 1, :], op=ADD)
+            eng.tensor_tensor(out=b4[:, r0:r1, :, 0, :], in0=pairs(c, 0)[:, r0:r1, :, 0, :], in1=ph[c][:, r0:r1], op=ADD)
+            eng.tensor_tensor(out=b4[:, r0:r1, :, 1, :], in0=ph[c][:, r0:r1], in1=pairs(c, 2)[:, r0:r1, :, 1, :], op=ADD)
 
         def v_fin(c, r):
             if ok(c):
@@ -248,19 +249,26 @@ def tile_staticgraphmodule_t_kernel(tc, x, Wp, b, out):
                 nc.vector.quantize_mx(out=wcodes[:].bitcast(FP8X4), scales=wscales[:], in_=wg[:])
             if ok(s - 3):
                 v_q(mean[s - 3][:], mc, ms, s - 3, "m")
-                pe_mx(s - 3)
+                pe_mx(s - 3, (0, 1, 2))
             if ok(s - 1):
-                v_pad(s - 1)
-                if not on_pe(s):
-                    box_sums(nc.vector, s - 1)
+                box[s - 1] = dbl.tile([P, CL], F32, name="box")
+                gr = ROWS - VB if on_pe(s) else 0
+                v_pad(s - 1, gr, ROWS)
+                box_sums(nc.vector, s - 1, gr, ROWS)
+                if gr > 0:
+                    v_pad(s - 1, 0, gr)
             if ok(s):
                 v_cv(s)
             if ok(s - 1) and on_pe(s):
-                box_sums(nc.gpsimd, s - 1)
+                box_sums(nc.gpsimd, s - 1, 0, ROWS - VB)
+            if ok(s - 1):
+                pe_t1_s_evac(s - 1, 0)
             if on_pe(s + 1):
                 pe_pv(s + 1)
             if ok(s - 1):
-                pe_t1_s_evac(s - 1)
+                pe_t1_s_evac(s - 1, 1)
+            if ok(s - 3):
+                pe_mx(s - 3, (3,))
             v_fin(s - 2, 0)
             v_res_store(s - 3, (0, 1))
             v_fin(s - 2, 1)

@@ -27,6 +27,7 @@ CPI = H_IMG // ROWS
 NCH = 2 * CPI
 PE_FROM = 4
 VB = 2
+GROWS = {2: 2, 3: 5, 16: 5}
 
 FLOPS = 2 * 512 * 1024 * 8192
 
@@ -57,7 +58,9 @@ def tile_staticgraphmodule_t_kernel(tc, x, Wp, b, out):
             n, cc = divmod(c, CPI)
             nc.sync.dma_start(out=xt[c][:], in_=xv[n, :, :, cc * PIX:(cc + 1) * PIX])
 
-        load_x(0)
+        for half in range(2):
+            nc.sync.dma_start(out=xt[0][:, :, half * PIX // 2:(half + 1) * PIX // 2],
+                              in_=xv[0, :, :, half * PIX // 2:(half + 1) * PIX // 2])
         load_x(1)
         nc.sync.dma_start(out=b16[:], in_=b.rearrange("(p j) -> p j", j=PACK))
         load_x(2)
@@ -104,14 +107,22 @@ def tile_staticgraphmodule_t_kernel(tc, x, Wp, b, out):
         def on_pe(c):
             return PE_FROM <= c < NCH
 
+        def pe_halves(c):
+            if on_pe(c):
+                return (0, 1)
+            return (1,) if c == PE_FROM - 1 else ()
+
         def base_of(c):
             return (1 + (c % CPI) * ROWS) * RL
 
         def s_xg(c):
             cc = c % CPI
-            nc.scalar.copy(grouped_view(xgi[:, base_of(c):base_of(c) + CL]), planar_view(xt[c][:]))
-            if cc == 0:
-                nc.scalar.copy(grouped_view(xgi[:, 0:RL]), planar_view(xt[c][:, :, 0:W_IMG]))
+            parts = 2 if c == 0 else 1
+            for part in range(parts):
+                nc.scalar.copy(grouped_view(xgi[:, base_of(c) + part * CL // parts:base_of(c) + (part + 1) * CL // parts]),
+                               planar_view(xt[c][:, :, part * PIX // parts:(part + 1) * PIX // parts]))
+                if cc == 0 and part == 0:
+                    nc.scalar.copy(grouped_view(xgi[:, 0:RL]), planar_view(xt[c][:, :, 0:W_IMG]))
             if cc == CPI - 1:
                 nc.scalar.copy(grouped_view(xgi[:, (H_IMG + 1) * RL:(H_IMG + 2) * RL]),
                                planar_view(xt[c][:, :, PIX - W_IMG:PIX]))
@@ -128,7 +139,7 @@ def tile_staticgraphmodule_t_kernel(tc, x, Wp, b, out):
 
         def pe_pv(c):
             mid = rows2(c, 1)
-            for h in range(2):
+            for h in pe_halves(c):
                 pvb[(c, h)] = ps2.tile([P, 2, RL], F32, name="pvb")
                 for t in range(2):
                     nc.tensor.matmul(out=pvb[(c, h)][:], lhsT=i8b[:], rhs=mid[:, 2 * h:2 * h + 2, t, :],
@@ -175,21 +186,24 @@ def tile_staticgraphmodule_t_kernel(tc, x, Wp, b, out):
             cv[c] = dbl.tile([P, ROWS, PRL], F32, name="cv")
             cvk = cv[c][:].rearrange("p (k t) c -> p k t c", t=2)
             others = (rows2(c, 0)[:, :, 0, :], rows2(c, 2)[:, :, 1, :])
-            if on_pe(c):
-                for h in range(2):
-                    for par in range(2):
-                        nc.vector.scalar_tensor_tensor(out=cvk[:, 2 * h:2 * h + 2, par, PACK:PACK + RL],
-                                                       in0=others[par][:, 2 * h:2 * h + 2, :], scalar=0.125,
-                                                       in1=pvb[(c, h)][:], op0=MULT, op1=ADD)
-            else:
-                hrow = tmp.tile([P, ROWS // 2, RL], BF16, name="hrow")
-                nc.vector.tensor_scalar_mul(hrow[:], rows2(c, 1)[:, :, 1, :], 0.125)
-                pv = tmp.tile([P, ROWS // 2, RL], F32, name="pv")
-                nc.vector.scalar_tensor_tensor(out=pv[:], in0=rows2(c, 1)[:, :, 0, :], scalar=0.125,
-                                               in1=hrow[:], op0=MULT, op1=ADD)
+            for h in pe_halves(c):
                 for par in range(2):
-                    nc.vector.scalar_tensor_tensor(out=cvk[:, :, par, PACK:PACK + RL], in0=others[par], scalar=0.125,
-                                                   in1=pv[:], op0=MULT, op1=ADD)
+                    nc.vector.scalar_tensor_tensor(out=cvk[:, 2 * h:2 * h + 2, par, PACK:PACK + RL],
+                                                   in0=others[par][:, 2 * h:2 * h + 2, :], scalar=0.125,
+                                                   in1=pvb[(c, h)][:], op0=MULT, op1=ADD)
+            kn = ROWS // 2 - 2 * len(pe_halves(c))
+            if kn > 0:
+                hrow = tmp.tile([P, ROWS // 2, RL], BF16, name="hrow")
+                pv = tmp.tile([P, ROWS // 2, RL], F32, name="pv")
+            for k0, k1 in ((0, 2), (2, 4)) if c == 0 else ((0, kn),):
+                if k1 > k0:
+                    nc.vector.tensor_scalar_mul(hrow[:, k0:k1, :], rows2(c, 1)[:, k0:k1, 1, :], 0.125)
+                    nc.vector.scalar_tensor_tensor(out=pv[:, k0:k1, :], in0=rows2(c, 1)[:, k0:k1, 0, :], scalar=0.125,
+                                                   in1=hrow[:, k0:k1, :], op0=MULT, op1=ADD)
+                    for par in range(2):
+                        nc.vector.scalar_tensor_tensor(out=cvk[:, k0:k1, par, PACK:PACK + RL],
+                                                       in0=others[par][:, k0:k1, :], scalar=0.125,
+                                                       in1=pv[:, k0:k1, :], op0=MULT, op1=ADD)
 
         def v_pad(c, r0, r1):
             cvw = cv[c][:].rearrange("p r (w j) -> p r w j", j=PACK)
@@ -247,31 +261,38 @@ def tile_staticgraphmodule_t_kernel(tc, x, Wp, b, out):
                 v_q(xgi[:, base_of(s - 1):base_of(s - 1) + CL], xc, xs, s - 1, "x")
             if s == 2:
                 nc.vector.quantize_mx(out=wcodes[:].bitcast(FP8X4), scales=wscales[:], in_=wg[:])
-            if ok(s - 3):
+            if ok(s - 3) and s - 3 < NCH - 1:
                 v_q(mean[s - 3][:], mc, ms, s - 3, "m")
                 pe_mx(s - 3, (0, 1, 2))
             if ok(s - 1):
                 box[s - 1] = dbl.tile([P, CL], F32, name="box")
-                gr = ROWS - VB if on_pe(s) else 0
+                gr = ROWS - VB if on_pe(s) else GROWS.get(s, 0)
                 v_pad(s - 1, gr, ROWS)
                 box_sums(nc.vector, s - 1, gr, ROWS)
                 if gr > 0:
                     v_pad(s - 1, 0, gr)
             if ok(s):
                 v_cv(s)
-            if ok(s - 1) and on_pe(s):
-                box_sums(nc.gpsimd, s - 1, 0, ROWS - VB)
+            if ok(s - 1) and gr > 0:
+                box_sums(nc.gpsimd, s - 1, 0, gr)
             if ok(s - 1):
                 pe_t1_s_evac(s - 1, 0)
-            if on_pe(s + 1):
+            if ok(s + 1):
                 pe_pv(s + 1)
             if ok(s - 1):
                 pe_t1_s_evac(s - 1, 1)
             if ok(s - 3):
                 pe_mx(s - 3, (3,))
             v_fin(s - 2, 0)
-            v_res_store(s - 3, (0, 1))
-            v_fin(s - 2, 1)
-            v_res_store(s - 3, (2, 3))
+            if s - 2 == NCH - 1:
+                v_fin(s - 2, 1)
+                v_res_store(s - 3, (0,))
+                v_q(mean[s - 2][:], mc, ms, s - 2, "m")
+                pe_mx(s - 2, (0, 1, 2))
+                v_res_store(s - 3, (1, 2, 3))
+            else:
+                v_res_store(s - 3, (0, 1))
+                v_fin(s - 2, 1)
+                v_res_store(s - 3, (2, 3))
             if ok(s):
                 ph_sums(nc.gpsimd if s > 0 else nc.vector, s)

@@ -19,15 +19,14 @@ ROWS = 8
 W_IMG = 64
 H_IMG = 64
 PIX = ROWS * W_IMG
+IMG = H_IMG * W_IMG
 RL = W_IMG * PACK
 CL = PIX * PACK
-HL = CL // 2
 PRL = (W_IMG + 2) * PACK
 CPI = H_IMG // ROWS
 NCH = 2 * CPI
-PE_FROM = 4
-VB = 2
-GROWS = {2: 2, 3: 5, 16: 5}
+PE_CHUNKS = (1, 4, 7)
+KT = ROWS // 2 + 1
 
 FLOPS = 2 * 512 * 1024 * 8192
 
@@ -39,40 +38,55 @@ def tile_staticgraphmodule_t_kernel(tc, x, Wp, b, out):
 
     with ExitStack() as ctx:
         const = ctx.enter_context(tc.tile_pool(name="const", bufs=1))
-        xpool = ctx.enter_context(tc.tile_pool(name="xpool", bufs=1))
         tmp = ctx.enter_context(tc.tile_pool(name="tmp", bufs=1))
         dbl = ctx.enter_context(tc.tile_pool(name="dbl", bufs=2))
         tri = ctx.enter_context(tc.tile_pool(name="tri", bufs=3))
-        ps1 = ctx.enter_context(tc.psum_pool(name="ps1", bufs=1))
         ps2 = ctx.enter_context(tc.psum_pool(name="ps2", bufs=2))
-        ps3 = ctx.enter_context(tc.psum_pool(name="ps3", bufs=3))
+        ps4 = ctx.enter_context(tc.psum_pool(name="ps4", bufs=4))
         ctx.enter_context(tc.manual_schedule())
+
+        def ok(c):
+            return 0 <= c < NCH
+
+        def on_pe(c):
+            return ok(c) and (c % CPI) in PE_CHUNKS
+
+        def vg(c):
+            return ok(c) and not on_pe(c)
 
         xt = []
         for c in range(NCH):
-            xt.append(xpool.tile([P, PACK, PIX], BF16, name="xt%d" % c))
+            xt.append(const.tile([P, PACK, PIX + (2 * W_IMG if on_pe(c) else 0)], BF16, name="xt%d" % c))
         w_sb = const.tile([P, PACK * 1024], BF16, name="w_sb")
         b16 = const.tile([P, PACK], BF16, name="b16")
 
-        def load_x(c):
-            n, cc = divmod(c, CPI)
-            nc.sync.dma_start(out=xt[c][:], in_=xv[n, :, :, cc * PIX:(cc + 1) * PIX])
+        def planar(c, p0, p1):
+            halo = W_IMG if on_pe(c) else 0
+            return xt[c][:, :, halo + p0:halo + p1]
 
-        for half in range(2):
-            nc.sync.dma_start(out=xt[0][:, :, half * PIX // 2:(half + 1) * PIX // 2],
-                              in_=xv[0, :, :, half * PIX // 2:(half + 1) * PIX // 2])
-        load_x(1)
+        def load_x(c, p0, p1):
+            n, cc = divmod(c, CPI)
+            if on_pe(c):
+                p0 = p0 - W_IMG
+                if cc == CPI - 1:
+                    nc.sync.dma_start(out=planar(c, PIX, PIX + W_IMG), in_=xv[n, :, :, IMG - W_IMG:IMG])
+                else:
+                    p1 = p1 + W_IMG
+            nc.sync.dma_start(out=planar(c, p0, p1), in_=xv[n, :, :, cc * PIX + p0:cc * PIX + p1])
+
+        load_x(0, 0, PIX // 2)
+        load_x(0, PIX // 2, PIX)
+        load_x(1, 0, PIX)
         nc.sync.dma_start(out=b16[:], in_=b.rearrange("(p j) -> p j", j=PACK))
-        load_x(2)
+        load_x(2, 0, PIX)
         nc.sync.dma_start(out=w_sb[:], in_=Wp.rearrange("(m j) k -> m (j k)", j=PACK))
         for c in range(3, NCH):
-            load_x(c)
+            load_x(c, 0, PIX)
 
         ident = const.tile([P, P], F32, name="ident")
         make_identity(nc, ident[:])
         identb = const.tile([P, P], BF16, name="identb")
         make_identity(nc, identb[:])
-        i8b = const.tile([P, P], BF16, name="i8b")
 
         xgi = const.tile([P, (H_IMG + 2) * RL], BF16, name="xgi", align_bytes=64)
         b32 = const.tile([P, PACK], F32, name="b32")
@@ -80,6 +94,11 @@ def tile_staticgraphmodule_t_kernel(tc, x, Wp, b, out):
         wg = const.tile([P, 8 * P * PACK], BF16, name="wg", align_bytes=64)
         wcodes = const.tile([P, 8 * P], U32, name="wcodes", align_bytes=64)
         wscales = const.tile([P, 8 * P], U8, name="wscales", align_bytes=64)
+        jt = const.tile([P, 2, W_IMG + 2], BF16, name="jt")
+        h8 = const.tile([P, 2, W_IMG], BF16, name="h8")
+        h3 = const.tile([P, 2, W_IMG], BF16, name="h3")
+        sa = const.tile([P, 2, W_IMG], BF16, name="sa")
+        sb = const.tile([P, 2, W_IMG], BF16, name="sb")
 
         def grouped_view(flat):
             return flat.rearrange("p (c i t) -> p c t i", i=4, t=PACK)
@@ -97,20 +116,11 @@ def tile_staticgraphmodule_t_kernel(tc, x, Wp, b, out):
         ms = {}
         acc = {}
         tt = {}
-        pvb = {}
-        xtr = {}
-        xps = {}
-
-        def ok(c):
-            return 0 <= c < NCH
-
-        def on_pe(c):
-            return PE_FROM <= c < NCH
-
-        def pe_halves(c):
-            if on_pe(c):
-                return (0, 1)
-            return (1,) if c == PE_FROM - 1 else ()
+        hrow = {}
+        pv = {}
+        xtp = {}
+        xts = {}
+        mo = {}
 
         def base_of(c):
             return (1 + (c % CPI) * ROWS) * RL
@@ -120,50 +130,52 @@ def tile_staticgraphmodule_t_kernel(tc, x, Wp, b, out):
             parts = 2 if c == 0 else 1
             for part in range(parts):
                 nc.scalar.copy(grouped_view(xgi[:, base_of(c) + part * CL // parts:base_of(c) + (part + 1) * CL // parts]),
-                               planar_view(xt[c][:, :, part * PIX // parts:(part + 1) * PIX // parts]))
+                               planar_view(planar(c, part * PIX // parts, (part + 1) * PIX // parts)))
                 if cc == 0 and part == 0:
-                    nc.scalar.copy(grouped_view(xgi[:, 0:RL]), planar_view(xt[c][:, :, 0:W_IMG]))
+                    nc.scalar.copy(grouped_view(xgi[:, 0:RL]), planar_view(planar(c, 0, W_IMG)))
             if cc == CPI - 1:
                 nc.scalar.copy(grouped_view(xgi[:, (H_IMG + 1) * RL:(H_IMG + 2) * RL]),
-                               planar_view(xt[c][:, :, PIX - W_IMG:PIX]))
+                               planar_view(planar(c, PIX - W_IMG, PIX)))
 
         def s_xb(c):
             tt[c] = tri.tile([P, PACK, PIX], F32, name="tt")
             for j in range(PACK):
-                nc.scalar.activation(out=tt[c][:, j, :], in_=xt[c][:, j, :], func=ACT.Identity,
+                nc.scalar.activation(out=tt[c][:, j, :], in_=planar(c, 0, PIX)[:, j, :], func=ACT.Identity,
                                      bias=b32[:, j:j + 1], scale=1.0)
+
+        def s_xt(c, g):
+            q0, q1 = 2 * g, min(2 * g + 2, KT)
+            nc.scalar.copy(xts[c][:, q0:q1, :, :], xtp[(c, g)][:, 0:q1 - q0, :, :])
+
+        def s_mean(c, t):
+            nc.scalar.copy(mean[c][:, t * 2 * RL:(t + 1) * 2 * RL].rearrange("p (n j) -> p n j", j=PACK),
+                           mo[(c, t)][:].rearrange("p j n -> p n j"))
 
         def rows2(c, first):
             r0 = (c % CPI) * ROWS + first
             return xgi[:, r0 * RL:(r0 + ROWS) * RL].rearrange("p (k t c) -> p k t c", t=2, c=RL)
 
-        def pe_pv(c):
-            mid = rows2(c, 1)
-            for h in pe_halves(c):
-                pvb[(c, h)] = ps2.tile([P, 2, RL], F32, name="pvb")
-                for t in range(2):
-                    nc.tensor.matmul(out=pvb[(c, h)][:], lhsT=i8b[:], rhs=mid[:, 2 * h:2 * h + 2, t, :],
-                                     start=(t == 0), stop=(t == 1))
+        def pe_t1(c, g):
+            if g == 0:
+                xts[c] = dbl.tile([P, KT, PACK, P], BF16, name="xts")
+            xtp[(c, g)] = ps2.tile([P, 2, PACK, P], BF16, name="xtp")
+            for q in range(2 * g, min(2 * g + 2, KT)):
+                for j in range(PACK):
+                    nc.tensor.transpose(xtp[(c, g)][:, q - 2 * g, j, :], xt[c][:, j, q * P:(q + 1) * P], identb[:])
 
-        def pe_t1_s_evac(c, r):
-            xw = xgi[:, base_of(c):base_of(c) + CL].bitcast(F32)
-            if r == 0:
-                xtr[c] = dbl.tile([P, HL], F32, name="xtr")
-            if r >= 0:
-                t1 = ps1.tile([P, 4, P], F32, name="t1")
-                for q in range(4):
-                    nc.tensor.transpose(t1[:, q, :], xw[:, (4 * r + q) * P:(4 * r + q + 1) * P], ident[:])
-                nc.scalar.copy(xtr[c][:, r * 512:(r + 1) * 512], t1[:].rearrange("p q m -> p (q m)"))
-
-        def pe_t2(c):
-            for r in range(2):
-                xps[(c, r)] = ps2.tile([P, 4, P], F32, name="xps")
-                for q in range(4):
-                    nc.tensor.transpose(xps[(c, r)][:, q, :], xtr[c][:, (4 * r + q) * P:(4 * r + q + 1) * P], ident[:])
+        def pe_mm(c, t):
+            if t == 0:
+                mean[c] = tri.tile([P, CL], BF16, name="mean", align_bytes=64)
+            mo[(c, t)] = ps2.tile([P, PACK, P], F32, name="mo")
+            for j in range(PACK):
+                nc.tensor.matmul(out=mo[(c, t)][:, j, :], lhsT=xts[c][:, t, j, :],
+                                 rhs=sa[:].rearrange("p a w -> p (a w)"), start=True, stop=False)
+                nc.tensor.matmul(out=mo[(c, t)][:, j, :], lhsT=xts[c][:, t + 1, j, :],
+                                 rhs=sb[:].rearrange("p a w -> p (a w)"), start=False, stop=True)
 
         def pe_mx(c, js):
             for j in js:
-                acc[(c, j)] = ps3.tile([P, PIX], F32, name="acc")
+                acc[(c, j)] = ps4.tile([P, PIX], F32, name="acc")
                 for s, codes, scales in ((0, xc, xs), (1, mc, ms)):
                     cols = slice((s * PACK + j) * P, (s * PACK + j + 1) * P)
                     nc.tensor.matmul_mx(out=acc[(c, j)][:],
@@ -175,39 +187,33 @@ def tile_staticgraphmodule_t_kernel(tc, x, Wp, b, out):
             wf = w_sb[:].bitcast(F32).rearrange("p (j s q u) -> p j s q u", j=PACK, s=2, u=2)
             wgf = wg[:].bitcast(F32).rearrange("p (g m u) -> p g m u", m=P, u=2)
             for half in range(4):
-                pw = ps3.tile([P, 2, 2, P], F32, name="acc")
+                pw = ps4.tile([P, 2, 2, P], F32, name="acc")
                 for gi in range(2):
                     s, j = divmod(half * 2 + gi, PACK)
                     for u in range(2):
                         nc.tensor.transpose(pw[:, gi, u, :], wf[:, j, s, :, u], ident[:])
                 nc.scalar.copy(wgf[:, half * 2:half * 2 + 2, :, :], pw[:].rearrange("p g u m -> p g m u"))
 
+        def v_hrow(c):
+            hrow[c] = tmp.tile([P, ROWS // 2, RL], BF16, name="hrow")
+            nc.vector.tensor_scalar_mul(hrow[c][:], rows2(c, 1)[:, :, 1, :], 0.125)
+
+        def v_pv(c):
+            pv[c] = tmp.tile([P, ROWS // 2, RL], F32, name="pv")
+            nc.vector.scalar_tensor_tensor(out=pv[c][:], in0=rows2(c, 1)[:, :, 0, :], scalar=0.125,
+                                           in1=hrow[c][:], op0=MULT, op1=ADD)
+
         def v_cv(c):
             cv[c] = dbl.tile([P, ROWS, PRL], F32, name="cv")
             cvk = cv[c][:].rearrange("p (k t) c -> p k t c", t=2)
             others = (rows2(c, 0)[:, :, 0, :], rows2(c, 2)[:, :, 1, :])
-            for h in pe_halves(c):
-                for par in range(2):
-                    nc.vector.scalar_tensor_tensor(out=cvk[:, 2 * h:2 * h + 2, par, PACK:PACK + RL],
-                                                   in0=others[par][:, 2 * h:2 * h + 2, :], scalar=0.125,
-                                                   in1=pvb[(c, h)][:], op0=MULT, op1=ADD)
-            kn = ROWS // 2 - 2 * len(pe_halves(c))
-            if kn > 0:
-                hrow = tmp.tile([P, ROWS // 2, RL], BF16, name="hrow")
-                pv = tmp.tile([P, ROWS // 2, RL], F32, name="pv")
-            for k0, k1 in ((0, 2), (2, 4)) if c == 0 else ((0, kn),):
-                if k1 > k0:
-                    nc.vector.tensor_scalar_mul(hrow[:, k0:k1, :], rows2(c, 1)[:, k0:k1, 1, :], 0.125)
-                    nc.vector.scalar_tensor_tensor(out=pv[:, k0:k1, :], in0=rows2(c, 1)[:, k0:k1, 0, :], scalar=0.125,
-                                                   in1=hrow[:, k0:k1, :], op0=MULT, op1=ADD)
-                    for par in range(2):
-                        nc.vector.scalar_tensor_tensor(out=cvk[:, k0:k1, par, PACK:PACK + RL],
-                                                       in0=others[par][:, k0:k1, :], scalar=0.125,
-                                                       in1=pv[:, k0:k1, :], op0=MULT, op1=ADD)
+            for par in range(2):
+                nc.vector.scalar_tensor_tensor(out=cvk[:, :, par, PACK:PACK + RL], in0=others[par], scalar=0.125,
+                                               in1=pv[c][:], op0=MULT, op1=ADD)
 
-        def v_pad(c, r0, r1):
+        def v_pad(c):
             cvw = cv[c][:].rearrange("p r (w j) -> p r w j", j=PACK)
-            nc.vector.tensor_copy(out=cvw[:, r0:r1, 0:W_IMG + 2:W_IMG + 1, :], in_=cvw[:, r0:r1, 1:W_IMG + 1:W_IMG - 1, :])
+            nc.vector.tensor_copy(out=cvw[:, :, 0:W_IMG + 2:W_IMG + 1, :], in_=cvw[:, :, 1:W_IMG + 1:W_IMG - 1, :])
 
         def pairs(c, first):
             return cv[c][:, :, first * PACK:first * PACK + RL].rearrange("p r (i t j) -> p r i t j", t=2, j=PACK)
@@ -221,78 +227,87 @@ def tile_staticgraphmodule_t_kernel(tc, x, Wp, b, out):
             eng.tensor_tensor(out=b4[:, r0:r1, :, 0, :], in0=pairs(c, 0)[:, r0:r1, :, 0, :], in1=ph[c][:, r0:r1], op=ADD)
             eng.tensor_tensor(out=b4[:, r0:r1, :, 1, :], in0=ph[c][:, r0:r1], in1=pairs(c, 2)[:, r0:r1, :, 1, :], op=ADD)
 
-        def v_fin(c, r):
-            if ok(c):
-                if r == 0:
-                    mean[c] = dbl.tile([P, CL], BF16, name="mean", align_bytes=64)
-                nc.vector.scalar_tensor_tensor(out=mean[c][:, r * HL:(r + 1) * HL],
-                                               in0=xps[(c, r)][:].rearrange("p q m -> p (q m)").bitcast(BF16),
-                                               scalar=-0.125, in1=box[c][:, r * HL:(r + 1) * HL], op0=MULT, op1=ADD)
+        def v_fin(c):
+            mean[c] = tri.tile([P, CL], BF16, name="mean", align_bytes=64)
+            nc.vector.scalar_tensor_tensor(out=mean[c][:], in0=xgi[:, base_of(c):base_of(c) + CL],
+                                           scalar=-0.125, in1=box[c][:], op0=MULT, op1=ADD)
 
         def v_q(src, codes, scales, c, nm):
             codes[c] = tri.tile([P, PIX], U32, name=nm + "c", align_bytes=64)
             scales[c] = tri.tile([P, PIX], U8, name=nm + "s", align_bytes=64)
             nc.vector.quantize_mx(out=codes[c][:].bitcast(FP8X4), scales=scales[c][:], in_=src)
 
-        def v_res_store(c, js):
+        def v_res_store(c):
             n, cc = divmod(c, CPI)
-            for j in js if ok(c) else ():
+            for j in range(PACK):
                 nc.vector.scalar_tensor_tensor(out=tt[c][:, j, :], in0=acc[(c, j)][:], scalar=nb32[:, j:j + 1],
                                                in1=tt[c][:, j, :], op0=MAX, op1=ADD)
                 if c == NCH - 1:
                     nc.sync.dma_start(out=ov[n, :, j, cc * PIX:(cc + 1) * PIX], in_=tt[c][:, j, :])
-            if ok(c) and c < NCH - 1 and PACK - 1 in js:
+            if c < NCH - 1:
                 nc.sync.dma_start(out=ov[n, :, :, cc * PIX:(cc + 1) * PIX], in_=tt[c][:])
 
         nc.vector.tensor_copy(out=b32[:], in_=b16[:])
         nc.vector.tensor_scalar_mul(nb32[:], b16[:], -1.0)
-        nc.vector.tensor_scalar_mul(i8b[:], identb[:], 0.125)
+        nc.vector.tensor_scalar_mul(jt[:, :, 1:W_IMG + 1], identb[:].rearrange("p (a w) -> p a w", a=2), 0.125)
+        nc.vector.tensor_copy(out=jt[:, :, 0:W_IMG + 2:W_IMG + 1], in_=jt[:, :, 1:W_IMG + 1:W_IMG - 1])
+        nc.vector.tensor_tensor(out=h8[:], in0=jt[:, :, 0:W_IMG], in1=jt[:, :, 2:W_IMG + 2], op=ADD)
+        nc.vector.tensor_tensor(out=h3[:], in0=h8[:], in1=jt[:, :, 1:W_IMG + 1], op=ADD)
+        nc.vector.tensor_tensor(out=sa[:, 0, :], in0=h3[:, 0, :], in1=h8[:, 1, :], op=ADD)
+        nc.vector.tensor_copy(out=sa[:, 1, :], in_=h3[:, 1, :])
+        nc.vector.tensor_copy(out=sb[:, 0, :], in_=h3[:, 0, :])
+        nc.vector.tensor_tensor(out=sb[:, 1, :], in0=h8[:, 0, :], in1=h3[:, 1, :], op=ADD)
+
         s_xg(0)
         s_xg(1)
         for s in range(NCH + 3):
+            if on_pe(s):
+                pe_t1(s, 0)
             if ok(s + 2):
                 s_xg(s + 2)
             if s == 1:
                 w_transposes()
+            if on_pe(s - 1):
+                pe_mm(s - 1, 0)
+                pe_mm(s - 1, 1)
+            if on_pe(s):
+                s_xt(s, 0)
+                pe_t1(s, 1)
+            if on_pe(s - 1):
+                s_mean(s - 1, 0)
+                s_mean(s - 1, 1)
+                pe_mm(s - 1, 2)
+                pe_mm(s - 1, 3)
             if ok(s - 2):
                 s_xb(s - 2)
-                pe_t2(s - 2)
+            if on_pe(s):
+                s_xt(s, 1)
+                pe_t1(s, 2)
+            if on_pe(s - 1):
+                s_mean(s - 1, 2)
+                s_mean(s - 1, 3)
+            if on_pe(s):
+                s_xt(s, 2)
+
+            if vg(s):
+                v_hrow(s)
             if ok(s - 1):
                 v_q(xgi[:, base_of(s - 1):base_of(s - 1) + CL], xc, xs, s - 1, "x")
             if s == 2:
                 nc.vector.quantize_mx(out=wcodes[:].bitcast(FP8X4), scales=wscales[:], in_=wg[:])
-            if ok(s - 3) and s - 3 < NCH - 1:
-                v_q(mean[s - 3][:], mc, ms, s - 3, "m")
-                pe_mx(s - 3, (0, 1, 2))
-            if ok(s - 1):
-                box[s - 1] = dbl.tile([P, CL], F32, name="box")
-                gr = ROWS - VB if on_pe(s) else GROWS.get(s, 0)
-                v_pad(s - 1, gr, ROWS)
-                box_sums(nc.vector, s - 1, gr, ROWS)
-                if gr > 0:
-                    v_pad(s - 1, 0, gr)
-            if ok(s):
-                v_cv(s)
-            if ok(s - 1) and gr > 0:
-                box_sums(nc.gpsimd, s - 1, 0, gr)
-            if ok(s - 1):
-                pe_t1_s_evac(s - 1, 0)
-            if ok(s + 1):
-                pe_pv(s + 1)
-            if ok(s - 1):
-                pe_t1_s_evac(s - 1, 1)
+            if vg(s):
+                v_pv(s)
             if ok(s - 3):
-                pe_mx(s - 3, (3,))
-            v_fin(s - 2, 0)
-            if s - 2 == NCH - 1:
-                v_fin(s - 2, 1)
-                v_res_store(s - 3, (0,))
-                v_q(mean[s - 2][:], mc, ms, s - 2, "m")
-                pe_mx(s - 2, (0, 1, 2))
-                v_res_store(s - 3, (1, 2, 3))
-            else:
-                v_res_store(s - 3, (0, 1))
-                v_fin(s - 2, 1)
-                v_res_store(s - 3, (2, 3))
-            if ok(s):
-                ph_sums(nc.gpsimd if s > 0 else nc.vector, s)
+                v_q(mean[s - 3][:], mc, ms, s - 3, "m")
+                pe_mx(s - 3, (0, 1, 2, 3))
+            if vg(s - 1):
+                v_pad(s - 1)
+                box[s - 1] = dbl.tile([P, CL], F32, name="box")
+                box_sums(nc.gpsimd, s - 1, 0, ROWS)
+            if vg(s):
+                v_cv(s)
+                ph_sums(nc.gpsimd, s)
+            if vg(s - 2):
+                v_fin(s - 2)
+            if ok(s - 3):
+                v_res_store(s - 3)

@@ -22,11 +22,13 @@ PIX = ROWS * W_IMG
 IMG = H_IMG * W_IMG
 RL = W_IMG * PACK
 CL = PIX * PACK
+HL = CL // 2
 PRL = (W_IMG + 2) * PACK
 CPI = H_IMG // ROWS
 NCH = 2 * CPI
 PE_CHUNKS = (1, 4, 7)
 KT = ROWS // 2 + 1
+NB = ROWS + 2
 
 FLOPS = 2 * 512 * 1024 * 8192
 
@@ -42,7 +44,7 @@ def tile_staticgraphmodule_t_kernel(tc, x, Wp, b, out):
         dbl = ctx.enter_context(tc.tile_pool(name="dbl", bufs=2))
         tri = ctx.enter_context(tc.tile_pool(name="tri", bufs=3))
         ps2 = ctx.enter_context(tc.psum_pool(name="ps2", bufs=2))
-        ps4 = ctx.enter_context(tc.psum_pool(name="ps4", bufs=4))
+        ps3 = ctx.enter_context(tc.psum_pool(name="ps3", bufs=3))
         ctx.enter_context(tc.manual_schedule())
 
         def ok(c):
@@ -57,7 +59,7 @@ def tile_staticgraphmodule_t_kernel(tc, x, Wp, b, out):
         xt = []
         for c in range(NCH):
             xt.append(const.tile([P, PACK, PIX + (2 * W_IMG if on_pe(c) else 0)], BF16, name="xt%d" % c))
-        w_sb = const.tile([P, PACK * 1024], BF16, name="w_sb")
+        w_sb = tri.tile([P, PACK * 1024], BF16, name="tt", align_bytes=64)
         b16 = const.tile([P, PACK], BF16, name="b16")
 
         def planar(c, p0, p1):
@@ -79,8 +81,9 @@ def tile_staticgraphmodule_t_kernel(tc, x, Wp, b, out):
         load_x(1, 0, PIX)
         nc.sync.dma_start(out=b16[:], in_=b.rearrange("(p j) -> p j", j=PACK))
         load_x(2, 0, PIX)
+        load_x(3, 0, PIX)
         nc.sync.dma_start(out=w_sb[:], in_=Wp.rearrange("(m j) k -> m (j k)", j=PACK))
-        for c in range(3, NCH):
+        for c in range(4, NCH):
             load_x(c, 0, PIX)
 
         ident = const.tile([P, P], F32, name="ident")
@@ -91,7 +94,7 @@ def tile_staticgraphmodule_t_kernel(tc, x, Wp, b, out):
         xgi = const.tile([P, (H_IMG + 2) * RL], BF16, name="xgi", align_bytes=64)
         b32 = const.tile([P, PACK], F32, name="b32")
         nb32 = const.tile([P, PACK], F32, name="nb32")
-        wg = const.tile([P, 8 * P * PACK], BF16, name="wg", align_bytes=64)
+        wg = tri.tile([P, 8 * P * PACK], BF16, name="tt", align_bytes=64)
         wcodes = const.tile([P, 8 * P], U32, name="wcodes", align_bytes=64)
         wscales = const.tile([P, 8 * P], U8, name="wscales", align_bytes=64)
         jt = const.tile([P, 2, W_IMG + 2], BF16, name="jt")
@@ -118,9 +121,10 @@ def tile_staticgraphmodule_t_kernel(tc, x, Wp, b, out):
         tt = {}
         hrow = {}
         pv = {}
-        xtp = {}
+        stg = {}
         xts = {}
-        mo = {}
+        xtr = {}
+        xps = {}
 
         def base_of(c):
             return (1 + (c % CPI) * ROWS) * RL
@@ -138,56 +142,75 @@ def tile_staticgraphmodule_t_kernel(tc, x, Wp, b, out):
                                planar_view(planar(c, PIX - W_IMG, PIX)))
 
         def s_xb(c):
-            tt[c] = tri.tile([P, PACK, PIX], F32, name="tt")
+            tt[c] = tri.tile([P, PACK, PIX], F32, name="tt", align_bytes=64)
             for j in range(PACK):
                 nc.scalar.activation(out=tt[c][:, j, :], in_=planar(c, 0, PIX)[:, j, :], func=ACT.Identity,
                                      bias=b32[:, j:j + 1], scale=1.0)
 
         def s_xt(c, g):
             q0, q1 = 2 * g, min(2 * g + 2, KT)
-            nc.scalar.copy(xts[c][:, q0:q1, :, :], xtp[(c, g)][:, 0:q1 - q0, :, :])
+            nc.scalar.copy(xts[c][:, q0:q1, :, :], stg[(c, "t", g)][:, 0:q1 - q0, :, :])
 
         def s_mean(c, t):
             nc.scalar.copy(mean[c][:, t * 2 * RL:(t + 1) * 2 * RL].rearrange("p (n j) -> p n j", j=PACK),
-                           mo[(c, t)][:].rearrange("p j n -> p n j"))
+                           stg[(c, "m", t)][:].rearrange("p j n -> p n j"))
+
+        def s_b1(c, g):
+            r0, r1 = 4 * g, min(4 * g + 4, NB)
+            nc.scalar.copy(xtr[c][:, r0:r1, :], stg[(c, "b", g)][:, 0:r1 - r0, :])
 
         def rows2(c, first):
             r0 = (c % CPI) * ROWS + first
             return xgi[:, r0 * RL:(r0 + ROWS) * RL].rearrange("p (k t c) -> p k t c", t=2, c=RL)
 
+        def pe_b1(c, g):
+            if g == 0:
+                xtr[c] = tri.tile([P, NB, P], F32, name="xtr")
+            stg[(c, "b", g)] = ps3.tile([P, 4, P], F32, name="stg")
+            for r in range(4 * g, min(4 * g + 4, NB)):
+                row = (c % CPI) * ROWS + r
+                nc.tensor.transpose(stg[(c, "b", g)][:, r - 4 * g, :], xgi[:, row * RL:(row + 1) * RL].bitcast(F32), ident[:])
+
+        def pe_b2(c, key, slots):
+            xps[(c, key)] = ps2.tile([P, 4, P], F32, name="xps")
+            for q in range(4):
+                nc.tensor.transpose(xps[(c, key)][:, q, :], xtr[c][:, slots[q], :], ident[:])
+
+        def bank(c, key):
+            return xps[(c, key)][:].rearrange("p q m -> p (q m)").bitcast(BF16)
+
         def pe_t1(c, g):
             if g == 0:
                 xts[c] = dbl.tile([P, KT, PACK, P], BF16, name="xts")
-            xtp[(c, g)] = ps2.tile([P, 2, PACK, P], BF16, name="xtp")
+            stg[(c, "t", g)] = ps3.tile([P, 2, PACK, P], BF16, name="stg")
             for q in range(2 * g, min(2 * g + 2, KT)):
                 for j in range(PACK):
-                    nc.tensor.transpose(xtp[(c, g)][:, q - 2 * g, j, :], xt[c][:, j, q * P:(q + 1) * P], identb[:])
+                    nc.tensor.transpose(stg[(c, "t", g)][:, q - 2 * g, j, :], xt[c][:, j, q * P:(q + 1) * P], identb[:])
 
         def pe_mm(c, t):
             if t == 0:
                 mean[c] = tri.tile([P, CL], BF16, name="mean", align_bytes=64)
-            mo[(c, t)] = ps2.tile([P, PACK, P], F32, name="mo")
+            stg[(c, "m", t)] = ps3.tile([P, PACK, P], F32, name="stg")
             for j in range(PACK):
-                nc.tensor.matmul(out=mo[(c, t)][:, j, :], lhsT=xts[c][:, t, j, :],
+                nc.tensor.matmul(out=stg[(c, "m", t)][:, j, :], lhsT=xts[c][:, t, j, :],
                                  rhs=sa[:].rearrange("p a w -> p (a w)"), start=True, stop=False)
-                nc.tensor.matmul(out=mo[(c, t)][:, j, :], lhsT=xts[c][:, t + 1, j, :],
+                nc.tensor.matmul(out=stg[(c, "m", t)][:, j, :], lhsT=xts[c][:, t + 1, j, :],
                                  rhs=sb[:].rearrange("p a w -> p (a w)"), start=False, stop=True)
 
-        def pe_mx(c, js):
-            for j in js:
-                acc[(c, j)] = ps4.tile([P, PIX], F32, name="acc")
-                for s, codes, scales in ((0, xc, xs), (1, mc, ms)):
-                    cols = slice((s * PACK + j) * P, (s * PACK + j + 1) * P)
-                    nc.tensor.matmul_mx(out=acc[(c, j)][:],
-                                        lhsT=wcodes[:, cols].bitcast(FP8X4), lhsT_scale=wscales[:, cols],
-                                        rhs=codes[c][:].bitcast(FP8X4), rhs_scale=scales[c][:],
-                                        start=(s == 0), stop=(s == 1))
+        def pe_mx(c, j):
+            acc[(c, j)] = ps3.tile([P, PIX], F32, name="acc")
+            for s, codes, scales in ((0, xc, xs), (1, mc, ms)):
+                cols = slice((s * PACK + j) * P, (s * PACK + j + 1) * P)
+                nc.tensor.matmul_mx(out=acc[(c, j)][:],
+                                    lhsT=wcodes[:, cols].bitcast(FP8X4), lhsT_scale=wscales[:, cols],
+                                    rhs=codes[c][:].bitcast(FP8X4), rhs_scale=scales[c][:],
+                                    start=(s == 0), stop=(s == 1))
 
         def w_transposes():
             wf = w_sb[:].bitcast(F32).rearrange("p (j s q u) -> p j s q u", j=PACK, s=2, u=2)
             wgf = wg[:].bitcast(F32).rearrange("p (g m u) -> p g m u", m=P, u=2)
             for half in range(4):
-                pw = ps4.tile([P, 2, 2, P], F32, name="acc")
+                pw = ps3.tile([P, 2, 2, P], F32, name="acc")
                 for gi in range(2):
                     s, j = divmod(half * 2 + gi, PACK)
                     for u in range(2):
@@ -198,18 +221,23 @@ def tile_staticgraphmodule_t_kernel(tc, x, Wp, b, out):
             hrow[c] = tmp.tile([P, ROWS // 2, RL], BF16, name="hrow")
             nc.vector.tensor_scalar_mul(hrow[c][:], rows2(c, 1)[:, :, 1, :], 0.125)
 
+        def rows_of(c, key, direct_view):
+            if (c, key) in xps:
+                return bank(c, key).rearrange("p (k c) -> p k c", c=RL)
+            return direct_view
+
         def v_pv(c):
             pv[c] = tmp.tile([P, ROWS // 2, RL], F32, name="pv")
-            nc.vector.scalar_tensor_tensor(out=pv[c][:], in0=rows2(c, 1)[:, :, 0, :], scalar=0.125,
+            nc.vector.scalar_tensor_tensor(out=pv[c][:], in0=rows_of(c, "C", rows2(c, 1)[:, :, 0, :]), scalar=0.125,
                                            in1=hrow[c][:], op0=MULT, op1=ADD)
 
-        def v_cv(c):
-            cv[c] = dbl.tile([P, ROWS, PRL], F32, name="cv")
+        def v_cv(c, par):
+            if par == 0:
+                cv[c] = dbl.tile([P, ROWS, PRL], F32, name="cv")
             cvk = cv[c][:].rearrange("p (k t) c -> p k t c", t=2)
-            others = (rows2(c, 0)[:, :, 0, :], rows2(c, 2)[:, :, 1, :])
-            for par in range(2):
-                nc.vector.scalar_tensor_tensor(out=cvk[:, :, par, PACK:PACK + RL], in0=others[par], scalar=0.125,
-                                               in1=pv[c][:], op0=MULT, op1=ADD)
+            other = rows_of(c, "A", rows2(c, 0)[:, :, 0, :]) if par == 0 else rows_of(c, "B", rows2(c, 2)[:, :, 1, :])
+            nc.vector.scalar_tensor_tensor(out=cvk[:, :, par, PACK:PACK + RL], in0=other, scalar=0.125,
+                                           in1=pv[c][:], op0=MULT, op1=ADD)
 
         def v_pad(c):
             cvw = cv[c][:].rearrange("p r (w j) -> p r w j", j=PACK)
@@ -227,24 +255,24 @@ def tile_staticgraphmodule_t_kernel(tc, x, Wp, b, out):
             eng.tensor_tensor(out=b4[:, r0:r1, :, 0, :], in0=pairs(c, 0)[:, r0:r1, :, 0, :], in1=ph[c][:, r0:r1], op=ADD)
             eng.tensor_tensor(out=b4[:, r0:r1, :, 1, :], in0=ph[c][:, r0:r1], in1=pairs(c, 2)[:, r0:r1, :, 1, :], op=ADD)
 
-        def v_fin(c):
-            mean[c] = tri.tile([P, CL], BF16, name="mean", align_bytes=64)
-            nc.vector.scalar_tensor_tensor(out=mean[c][:], in0=xgi[:, base_of(c):base_of(c) + CL],
-                                           scalar=-0.125, in1=box[c][:], op0=MULT, op1=ADD)
+        def v_fin(c, h):
+            if h == 0:
+                mean[c] = tri.tile([P, CL], BF16, name="mean", align_bytes=64)
+            nc.vector.scalar_tensor_tensor(out=mean[c][:, h * HL:(h + 1) * HL], in0=bank(c, "DE"[h]),
+                                           scalar=-0.125, in1=box[c][:, h * HL:(h + 1) * HL], op0=MULT, op1=ADD)
 
         def v_q(src, codes, scales, c, nm):
             codes[c] = tri.tile([P, PIX], U32, name=nm + "c", align_bytes=64)
             scales[c] = tri.tile([P, PIX], U8, name=nm + "s", align_bytes=64)
             nc.vector.quantize_mx(out=codes[c][:].bitcast(FP8X4), scales=scales[c][:], in_=src)
 
-        def v_res_store(c):
+        def v_res(c, j, last):
             n, cc = divmod(c, CPI)
-            for j in range(PACK):
-                nc.vector.scalar_tensor_tensor(out=tt[c][:, j, :], in0=acc[(c, j)][:], scalar=nb32[:, j:j + 1],
-                                               in1=tt[c][:, j, :], op0=MAX, op1=ADD)
-                if c == NCH - 1:
-                    nc.sync.dma_start(out=ov[n, :, j, cc * PIX:(cc + 1) * PIX], in_=tt[c][:, j, :])
-            if c < NCH - 1:
+            nc.vector.scalar_tensor_tensor(out=tt[c][:, j, :], in0=acc[(c, j)][:], scalar=nb32[:, j:j + 1],
+                                           in1=tt[c][:, j, :], op0=MAX, op1=ADD)
+            if last:
+                nc.sync.dma_start(out=ov[n, :, j, cc * PIX:(cc + 1) * PIX], in_=tt[c][:, j, :])
+            elif j == PACK - 1:
                 nc.sync.dma_start(out=ov[n, :, :, cc * PIX:(cc + 1) * PIX], in_=tt[c][:])
 
         nc.vector.tensor_copy(out=b32[:], in_=b16[:])
@@ -258,56 +286,109 @@ def tile_staticgraphmodule_t_kernel(tc, x, Wp, b, out):
         nc.vector.tensor_copy(out=sb[:, 0, :], in_=h3[:, 0, :])
         nc.vector.tensor_tensor(out=sb[:, 1, :], in0=h8[:, 0, :], in1=h3[:, 1, :], op=ADD)
 
-        s_xg(0)
-        s_xg(1)
-        for s in range(NCH + 3):
-            if on_pe(s):
-                pe_t1(s, 0)
-            if ok(s + 2):
-                s_xg(s + 2)
-            if s == 1:
-                w_transposes()
-            if on_pe(s - 1):
-                pe_mm(s - 1, 0)
-                pe_mm(s - 1, 1)
-            if on_pe(s):
-                s_xt(s, 0)
-                pe_t1(s, 1)
-            if on_pe(s - 1):
-                s_mean(s - 1, 0)
-                s_mean(s - 1, 1)
-                pe_mm(s - 1, 2)
-                pe_mm(s - 1, 3)
-            if ok(s - 2):
-                s_xb(s - 2)
-            if on_pe(s):
-                s_xt(s, 1)
-                pe_t1(s, 2)
-            if on_pe(s - 1):
-                s_mean(s - 1, 2)
-                s_mean(s - 1, 3)
-            if on_pe(s):
-                s_xt(s, 2)
+        vlist = [c for c in range(NCH) if vg(c)]
+        nv = len(vlist)
+        nper = nv + 2
 
-            if vg(s):
-                v_hrow(s)
-            if ok(s - 1):
-                v_q(xgi[:, base_of(s - 1):base_of(s - 1) + CL], xc, xs, s - 1, "x")
-            if s == 2:
+        def vch(k):
+            return vlist[k] if 0 <= k < nv else -1
+
+        fin_of = [[] for k in range(nper + 1)]
+        for k in range(nv):
+            v = vlist[k]
+            fin_of[k + 2].append(v)
+            if on_pe(v + 1):
+                fin_of[k + 2 if v + 1 < NCH - 1 else k + 1].append(v + 1)
+        mm_of = {}
+        t1_of = {}
+        for k in range(nper):
+            for c in fin_of[k]:
+                if on_pe(c):
+                    mm_of[k - 1] = c
+                    t1_of[k - 2] = c
+        a_of = {}
+        done = 0
+        for k in range(-2, nper):
+            lim = min(vch(k + 2) + 1, NCH - 1) if k + 2 < nv else NCH - 1
+            a_of[k] = list(range(done, lim + 1))
+            done = max(done, lim + 1)
+
+        def bounced(k):
+            if k == 0:
+                return [vlist[0], vlist[1]]
+            return [vch(k + 1)] if k > 0 and vch(k + 1) >= 0 else []
+
+        for k in range(-2, nper):
+            v0, v1 = vch(k), vch(k - 1)
+            fl = fin_of[k] if k >= 0 else []
+            nfl = fin_of[k + 1] if k + 1 >= 0 else []
+            aj = a_of[k]
+            pm = mm_of.get(k, -1)
+            pt = t1_of.get(k, -1)
+            last = k == nper - 1
+            units = [(c, j) for c in fl for j in range(PACK)]
+
+            if v0 >= 0 and k > 0:
+                pe_b2(v0, "C", (1, 3, 5, 7))
+                pe_b2(v0, "A", (0, 2, 4, 6))
+            if v0 >= 0:
+                v_hrow(v0)
+            if len(aj) > 0:
+                s_xg(aj[0])
+            for c in bounced(k):
+                for g in range(3):
+                    pe_b1(c, g)
+                    s_b1(c, g)
+            if k == 0:
+                w_transposes()
+            for c in fl:
+                v_q(xgi[:, base_of(c):base_of(c) + CL], xc, xs, c, "x")
+                v_q(mean[c][:], mc, ms, c, "m")
+            if k == 1:
                 nc.vector.quantize_mx(out=wcodes[:].bitcast(FP8X4), scales=wscales[:], in_=wg[:])
-            if vg(s):
-                v_pv(s)
-            if ok(s - 3):
-                v_q(mean[s - 3][:], mc, ms, s - 3, "m")
-                pe_mx(s - 3, (0, 1, 2, 3))
-            if vg(s - 1):
-                v_pad(s - 1)
-                box[s - 1] = dbl.tile([P, CL], F32, name="box")
-                box_sums(nc.gpsimd, s - 1, 0, ROWS)
-            if vg(s):
-                v_cv(s)
-                ph_sums(nc.gpsimd, s)
-            if vg(s - 2):
-                v_fin(s - 2)
-            if ok(s - 3):
-                v_res_store(s - 3)
+            if v1 >= 0:
+                v_pad(v1)
+                box[v1] = dbl.tile([P, CL], F32, name="box")
+                box_sums(nc.gpsimd, v1, 0, ROWS)
+            for c, j in units[0:3]:
+                pe_mx(c, j)
+            if v0 >= 0:
+                v_pv(v0)
+            if v0 >= 0 and k > 0:
+                pe_b2(v0, "B", (3, 5, 7, 9))
+            if v0 >= 0:
+                v_cv(v0, 0)
+            if len(fl) > 1:
+                s_xb(fl[1])
+            if pm >= 0:
+                pe_mm(pm, 0)
+                s_mean(pm, 0)
+            if v1 >= 0:
+                pe_b2(v1, "D", (1, 2, 3, 4))
+            if v0 >= 0:
+                v_cv(v0, 1)
+                ph_sums(nc.gpsimd, v0)
+            if pm >= 0:
+                pe_mm(pm, 1)
+                s_mean(pm, 1)
+            if v1 >= 0:
+                pe_b2(v1, "E", (5, 6, 7, 8))
+            for i in range(max(len(units), 2)):
+                if i < len(units):
+                    v_res(units[i][0], units[i][1], last)
+                if i + 3 < len(units):
+                    pe_mx(units[i + 3][0], units[i + 3][1])
+                if pm >= 0 and i < 2:
+                    pe_mm(pm, 2 + i)
+                    s_mean(pm, 2 + i)
+            if len(aj) > 1:
+                s_xg(aj[1])
+            if pt >= 0:
+                for g in range(3):
+                    pe_t1(pt, g)
+                    s_xt(pt, g)
+            if len(nfl) > 0:
+                s_xb(nfl[0])
+            if v1 >= 0:
+                v_fin(v1, 0)
+                v_fin(v1, 1)

@@ -129,6 +129,15 @@ def tile_staticgraphmodule_t_kernel(tc, x, Wp, b, out):
         def base_of(c):
             return (1 + (c % CPI) * ROWS) * RL
 
+        def v_xg(c):
+            nc.vector.tensor_copy(out=grouped_view(xgi[:, base_of(c):base_of(c) + CL]), in_=planar_view(planar(c, 0, PIX)))
+
+        def g_xb(c):
+            tt[c] = tri.tile([P, PACK, PIX], F32, name="tt", align_bytes=64)
+            for j in range(PACK):
+                nc.gpsimd.tensor_scalar(out=tt[c][:, j, :], in0=planar(c, 0, PIX)[:, j, :], scalar1=1.0,
+                                        scalar2=b32[:, j:j + 1], op0=MULT, op1=ADD)
+
         def s_xg(c):
             cc = c % CPI
             parts = 2 if c == 0 else 1
@@ -313,10 +322,13 @@ def tile_staticgraphmodule_t_kernel(tc, x, Wp, b, out):
             a_of[k] = list(range(done, lim + 1))
             done = max(done, lim + 1)
 
-        def bounced(k):
-            if k == 0:
-                return [vlist[0], vlist[1]]
-            return [vch(k + 1)] if k > 0 and vch(k + 1) >= 0 else []
+        def bounce(c):
+            for g in range(3):
+                pe_b1(c, g)
+                s_b1(c, g)
+
+        def q_x(c):
+            v_q(xgi[:, base_of(c):base_of(c) + CL], xc, xs, c, "x")
 
         for k in range(-2, nper):
             v0, v1 = vch(k), vch(k - 1)
@@ -333,19 +345,20 @@ def tile_staticgraphmodule_t_kernel(tc, x, Wp, b, out):
                 pe_b2(v0, "A", (0, 2, 4, 6))
             if v0 >= 0:
                 v_hrow(v0)
-            if len(aj) > 0:
+            if len(aj) > 0 and k != 0:
                 s_xg(aj[0])
-            for c in bounced(k):
-                for g in range(3):
-                    pe_b1(c, g)
-                    s_b1(c, g)
-            if k == 0:
-                w_transposes()
-            for c in fl:
-                v_q(xgi[:, base_of(c):base_of(c) + CL], xc, xs, c, "x")
-                v_q(mean[c][:], mc, ms, c, "m")
-            if k == 1:
+            if k == -2:
+                v_xg(aj[1])
+            if k > 0 and vch(k + 1) >= 0:
+                bounce(vch(k + 1))
+            if k == 2:
                 nc.vector.quantize_mx(out=wcodes[:].bitcast(FP8X4), scales=wscales[:], in_=wg[:])
+            for i in range(len(fl)):
+                if i > 0:
+                    q_x(fl[i])
+                v_q(mean[fl[i]][:], mc, ms, fl[i], "m")
+            if len(nfl) > 0:
+                q_x(nfl[0])
             if v1 >= 0:
                 v_pad(v1)
                 box[v1] = dbl.tile([P, CL], F32, name="box")
@@ -354,6 +367,9 @@ def tile_staticgraphmodule_t_kernel(tc, x, Wp, b, out):
                 pe_mx(c, j)
             if v0 >= 0:
                 v_pv(v0)
+            if k == 0:
+                v_xg(a_of[-1][1])
+                bounce(vlist[1])
             if v0 >= 0 and k > 0:
                 pe_b2(v0, "B", (3, 5, 7, 9))
             if v0 >= 0:
@@ -381,14 +397,21 @@ def tile_staticgraphmodule_t_kernel(tc, x, Wp, b, out):
                 if pm >= 0 and i < 2:
                     pe_mm(pm, 2 + i)
                     s_mean(pm, 2 + i)
-            if len(aj) > 1:
+            if k == 0:
+                bounce(vlist[0])
+                w_transposes()
+                s_xg(aj[0])
+            if len(aj) > 1 and k >= 0:
                 s_xg(aj[1])
             if pt >= 0:
                 for g in range(3):
                     pe_t1(pt, g)
                     s_xt(pt, g)
             if len(nfl) > 0:
-                s_xb(nfl[0])
+                if len(fl) > 1:
+                    g_xb(nfl[0])
+                else:
+                    s_xb(nfl[0])
             if v1 >= 0:
                 v_fin(v1, 0)
                 v_fin(v1, 1)

@@ -26,7 +26,7 @@ HL = CL // 2
 PRL = (W_IMG + 2) * PACK
 CPI = H_IMG // ROWS
 NCH = 2 * CPI
-PE_CHUNKS = (1, 4, 7)
+PE_CHUNKS = (1, 4, 7, 9, 12, 15)
 KT = ROWS // 2 + 1
 NB = ROWS + 2
 
@@ -51,7 +51,7 @@ def tile_staticgraphmodule_t_kernel(tc, x, Wp, b, out):
             return 0 <= c < NCH
 
         def on_pe(c):
-            return ok(c) and (c % CPI) in PE_CHUNKS
+            return ok(c) and c in PE_CHUNKS
 
         def vg(c):
             return ok(c) and not on_pe(c)
@@ -131,12 +131,6 @@ def tile_staticgraphmodule_t_kernel(tc, x, Wp, b, out):
 
         def v_xg(c):
             nc.vector.tensor_copy(out=grouped_view(xgi[:, base_of(c):base_of(c) + CL]), in_=planar_view(planar(c, 0, PIX)))
-
-        def g_xb(c):
-            tt[c] = tri.tile([P, PACK, PIX], F32, name="tt", align_bytes=64)
-            for j in range(PACK):
-                nc.gpsimd.tensor_scalar(out=tt[c][:, j, :], in0=planar(c, 0, PIX)[:, j, :], scalar1=1.0,
-                                        scalar2=b32[:, j:j + 1], op0=MULT, op1=ADD)
 
         def s_xg(c):
             cc = c % CPI
@@ -224,7 +218,7 @@ def tile_staticgraphmodule_t_kernel(tc, x, Wp, b, out):
                     s, j = divmod(half * 2 + gi, PACK)
                     for u in range(2):
                         nc.tensor.transpose(pw[:, gi, u, :], wf[:, j, s, :, u], ident[:])
-                nc.scalar.copy(wgf[:, half * 2:half * 2 + 2, :, :], pw[:].rearrange("p g u m -> p g m u"))
+                nc.vector.tensor_copy(out=wgf[:, half * 2:half * 2 + 2, :, :], in_=pw[:].rearrange("p g u m -> p g m u"))
 
         def v_hrow(c):
             hrow[c] = tmp.tile([P, ROWS // 2, RL], BF16, name="hrow")
@@ -348,7 +342,8 @@ def tile_staticgraphmodule_t_kernel(tc, x, Wp, b, out):
             if len(aj) > 0 and k != 0:
                 s_xg(aj[0])
             if k == -2:
-                v_xg(aj[1])
+                for c in aj[1:]:
+                    v_xg(c)
             if k > 0 and vch(k + 1) >= 0:
                 bounce(vch(k + 1))
             if k == 2:
@@ -368,7 +363,8 @@ def tile_staticgraphmodule_t_kernel(tc, x, Wp, b, out):
             if v0 >= 0:
                 v_pv(v0)
             if k == 0:
-                v_xg(a_of[-1][1])
+                for c in a_of[-1][1:]:
+                    v_xg(c)
                 bounce(vlist[1])
             if v0 >= 0 and k > 0:
                 pe_b2(v0, "B", (3, 5, 7, 9))
@@ -408,10 +404,7 @@ def tile_staticgraphmodule_t_kernel(tc, x, Wp, b, out):
                     pe_t1(pt, g)
                     s_xt(pt, g)
             if len(nfl) > 0:
-                if len(fl) > 1:
-                    g_xb(nfl[0])
-                else:
-                    s_xb(nfl[0])
+                s_xb(nfl[0])
             if v1 >= 0:
                 v_fin(v1, 0)
                 v_fin(v1, 1)

@@ -26,7 +26,7 @@ HL = CL // 2
 PRL = (W_IMG + 2) * PACK
 CPI = H_IMG // ROWS
 NCH = 2 * CPI
-PE_CHUNKS = (1, 4, 7, 9, 12, 15)
+PE_CHUNKS = (2, 5, 7, 10, 12, 15)
 KT = ROWS // 2 + 1
 NB = ROWS + 2
 
@@ -296,16 +296,38 @@ def tile_staticgraphmodule_t_kernel(tc, x, Wp, b, out):
         def vch(k):
             return vlist[k] if 0 <= k < nv else -1
 
-        fin_of = [[] for k in range(nper + 1)]
+        order = []
+        avail = []
         for k in range(nv):
             v = vlist[k]
-            fin_of[k + 2].append(v)
-            if on_pe(v + 1):
-                fin_of[k + 2 if v + 1 < NCH - 1 else k + 1].append(v + 1)
+            if on_pe(v + 1) and v + 1 == NCH - 1:
+                order.append(v + 1)
+                avail.append(k + 1)
+            order.append(v)
+            avail.append(k + 2)
+            if on_pe(v + 1) and v + 1 < NCH - 1:
+                order.append(v + 1)
+                avail.append(k + 2)
+        allunits = [(c, j) for c in order for j in range(PACK)]
+        upto = {}
+        for k in range(-2, nper):
+            quota = (len(allunits) * (k - 1) + nv // 2) // nv if k >= 2 else 0
+            there = PACK * len([a for a in avail if a <= k])
+            for i in range(len(order)):
+                if avail[i] > k:
+                    there = min(there, PACK * i)
+            upto[k] = min(quota, there) if k < nper - 1 else len(allunits)
+        start_of = {}
+        for k in range(-2, nper + 1):
+            start_of[k] = []
+        for i in range(len(order)):
+            for k in range(2, nper):
+                if upto[k - 1] <= PACK * i < upto[k]:
+                    start_of[k].append(order[i])
         mm_of = {}
         t1_of = {}
         for k in range(nper):
-            for c in fin_of[k]:
+            for c in start_of[k]:
                 if on_pe(c):
                     mm_of[k - 1] = c
                     t1_of[k - 2] = c
@@ -322,17 +344,33 @@ def tile_staticgraphmodule_t_kernel(tc, x, Wp, b, out):
                 s_b1(c, g)
 
         def q_x(c):
-            v_q(xgi[:, base_of(c):base_of(c) + CL], xc, xs, c, "x")
+            if c not in xc:
+                v_q(xgi[:, base_of(c):base_of(c) + CL], xc, xs, c, "x")
+
+        st = {"issued": 0, "done": 0, "ready": 0}
+
+        def issue():
+            while st["issued"] < min(st["done"] + 3, st["ready"]):
+                pe_mx(allunits[st["issued"]][0], allunits[st["issued"]][1])
+                st["issued"] += 1
+
+        def finish(m, lim):
+            for i in range(m):
+                if st["done"] < lim:
+                    c, j = allunits[st["done"]]
+                    v_res(c, j, c == order[-1])
+                    st["done"] += 1
+                    issue()
 
         for k in range(-2, nper):
             v0, v1 = vch(k), vch(k - 1)
-            fl = fin_of[k] if k >= 0 else []
-            nfl = fin_of[k + 1] if k + 1 >= 0 else []
+            fl = start_of[k]
+            nfl = start_of[k + 1]
             aj = a_of[k]
             pm = mm_of.get(k, -1)
             pt = t1_of.get(k, -1)
-            last = k == nper - 1
-            units = [(c, j) for c in fl for j in range(PACK)]
+            lim = upto[k]
+            n = lim - st["done"]
 
             if v0 >= 0 and k > 0:
                 pe_b2(v0, "C", (1, 3, 5, 7))
@@ -348,18 +386,17 @@ def tile_staticgraphmodule_t_kernel(tc, x, Wp, b, out):
                 bounce(vch(k + 1))
             if k == 2:
                 nc.vector.quantize_mx(out=wcodes[:].bitcast(FP8X4), scales=wscales[:], in_=wg[:])
-            for i in range(len(fl)):
-                if i > 0:
-                    q_x(fl[i])
-                v_q(mean[fl[i]][:], mc, ms, fl[i], "m")
+            for c in fl:
+                q_x(c)
+                v_q(mean[c][:], mc, ms, c, "m")
+                st["ready"] += PACK
             if len(nfl) > 0:
                 q_x(nfl[0])
             if v1 >= 0:
                 v_pad(v1)
                 box[v1] = dbl.tile([P, CL], F32, name="box")
                 box_sums(nc.gpsimd, v1, 0, ROWS)
-            for c, j in units[0:3]:
-                pe_mx(c, j)
+            issue()
             if v0 >= 0:
                 v_pv(v0)
             if k == 0:
@@ -368,6 +405,7 @@ def tile_staticgraphmodule_t_kernel(tc, x, Wp, b, out):
                 bounce(vlist[1])
             if v0 >= 0 and k > 0:
                 pe_b2(v0, "B", (3, 5, 7, 9))
+            finish(1, lim)
             if v0 >= 0:
                 v_cv(v0, 0)
             if len(fl) > 1:
@@ -377,6 +415,7 @@ def tile_staticgraphmodule_t_kernel(tc, x, Wp, b, out):
                 s_mean(pm, 0)
             if v1 >= 0:
                 pe_b2(v1, "D", (1, 2, 3, 4))
+            finish(1, lim)
             if v0 >= 0:
                 v_cv(v0, 1)
                 ph_sums(nc.gpsimd, v0)
@@ -385,14 +424,15 @@ def tile_staticgraphmodule_t_kernel(tc, x, Wp, b, out):
                 s_mean(pm, 1)
             if v1 >= 0:
                 pe_b2(v1, "E", (5, 6, 7, 8))
-            for i in range(max(len(units), 2)):
-                if i < len(units):
-                    v_res(units[i][0], units[i][1], last)
-                if i + 3 < len(units):
-                    pe_mx(units[i + 3][0], units[i + 3][1])
-                if pm >= 0 and i < 2:
-                    pe_mm(pm, 2 + i)
-                    s_mean(pm, 2 + i)
+            finish(1, lim)
+            if pm >= 0:
+                pe_mm(pm, 2)
+                s_mean(pm, 2)
+            finish(1, lim)
+            if pm >= 0:
+                pe_mm(pm, 3)
+                s_mean(pm, 3)
+            finish(n - 5, lim)
             if k == 0:
                 bounce(vlist[0])
                 w_transposes()
@@ -407,4 +447,7 @@ def tile_staticgraphmodule_t_kernel(tc, x, Wp, b, out):
                 s_xb(nfl[0])
             if v1 >= 0:
                 v_fin(v1, 0)
+            finish(1, lim)
+            if v1 >= 0:
                 v_fin(v1, 1)
+            finish(n, lim)

@@ -76,10 +76,10 @@ def tile_staticgraphmodule_t_kernel(tc, x, Wp, b, out):
                     p1 = p1 + W_IMG
             nc.sync.dma_start(out=planar(c, p0, p1), in_=xv[n, :, :, cc * PIX + p0:cc * PIX + p1])
 
+        nc.sync.dma_start(out=b16[:], in_=b.rearrange("(p j) -> p j", j=PACK))
         load_x(0, 0, PIX // 2)
         load_x(0, PIX // 2, PIX)
         load_x(1, 0, PIX)
-        nc.sync.dma_start(out=b16[:], in_=b.rearrange("(p j) -> p j", j=PACK))
         load_x(2, 0, PIX)
         load_x(3, 0, PIX)
         nc.sync.dma_start(out=w_sb[:], in_=Wp.rearrange("(m j) k -> m (j k)", j=PACK))
@@ -278,8 +278,6 @@ def tile_staticgraphmodule_t_kernel(tc, x, Wp, b, out):
             elif j == PACK - 1:
                 nc.sync.dma_start(out=ov[n, :, :, cc * PIX:(cc + 1) * PIX], in_=tt[c][:])
 
-        nc.vector.tensor_copy(out=b32[:], in_=b16[:])
-        nc.vector.tensor_scalar_mul(nb32[:], b16[:], -1.0)
         nc.vector.tensor_scalar_mul(jt[:, :, 1:W_IMG + 1], identb[:].rearrange("p (a w) -> p a w", a=2), 0.125)
         nc.vector.tensor_copy(out=jt[:, :, 0:W_IMG + 2:W_IMG + 1], in_=jt[:, :, 1:W_IMG + 1:W_IMG - 1])
         nc.vector.tensor_tensor(out=h8[:], in0=jt[:, :, 0:W_IMG], in1=jt[:, :, 2:W_IMG + 2], op=ADD)
@@ -288,6 +286,8 @@ def tile_staticgraphmodule_t_kernel(tc, x, Wp, b, out):
         nc.vector.tensor_copy(out=sa[:, 1, :], in_=h3[:, 1, :])
         nc.vector.tensor_copy(out=sb[:, 0, :], in_=h3[:, 0, :])
         nc.vector.tensor_tensor(out=sb[:, 1, :], in0=h8[:, 0, :], in1=h3[:, 1, :], op=ADD)
+        nc.vector.tensor_copy(out=b32[:], in_=b16[:])
+        nc.vector.tensor_scalar_mul(nb32[:], b16[:], -1.0)
 
         vlist = [c for c in range(NCH) if vg(c)]
         nv = len(vlist)

@@ -11,6 +11,7 @@ FP8X4 = mybir.dt.float8_e4m3fn_x4
 ADD = mybir.AluOpType.add
 MAX = mybir.AluOpType.max
 MULT = mybir.AluOpType.mult
+SUB = mybir.AluOpType.subtract
 ACT = mybir.ActivationFunctionType
 
 P = 128
@@ -176,7 +177,7 @@ def tile_staticgraphmodule_t_kernel(tc, x, Wp, b, out):
 
         def pe_b2(c, key, slots):
             xps[(c, key)] = ps2.tile([P, 4, P], F32, name="xps")
-            for q in range(4):
+            for q in range(len(slots)):
                 nc.tensor.transpose(xps[(c, key)][:, q, :], xtr[c][:, slots[q], :], ident[:])
 
         def bank(c, key):
@@ -221,7 +222,7 @@ def tile_staticgraphmodule_t_kernel(tc, x, Wp, b, out):
                 nc.vector.tensor_copy(out=wgf[:, half * 2:half * 2 + 2, :, :], in_=pw[:].rearrange("p g u m -> p g m u"))
 
         def v_hrow(c):
-            hrow[c] = tmp.tile([P, ROWS // 2, RL], BF16, name="hrow")
+            hrow[c] = dbl.tile([P, ROWS // 2, RL], BF16, name="hrow")
             nc.vector.tensor_scalar_mul(hrow[c][:], rows2(c, 1)[:, :, 1, :], 0.125)
 
         def rows_of(c, key, direct_view):
@@ -258,11 +259,23 @@ def tile_staticgraphmodule_t_kernel(tc, x, Wp, b, out):
             eng.tensor_tensor(out=b4[:, r0:r1, :, 0, :], in0=pairs(c, 0)[:, r0:r1, :, 0, :], in1=ph[c][:, r0:r1], op=ADD)
             eng.tensor_tensor(out=b4[:, r0:r1, :, 1, :], in0=ph[c][:, r0:r1], in1=pairs(c, 2)[:, r0:r1, :, 1, :], op=ADD)
 
-        def v_fin(c, h):
-            if h == 0:
-                mean[c] = tri.tile([P, CL], BF16, name="mean", align_bytes=64)
-            nc.vector.scalar_tensor_tensor(out=mean[c][:, h * HL:(h + 1) * HL], in0=bank(c, "DE"[h]),
-                                           scalar=-0.125, in1=box[c][:, h * HL:(h + 1) * HL], op0=MULT, op1=ADD)
+        def rowpairs(flat):
+            return flat.rearrange("p (k t c) -> p k t c", t=2, c=RL)
+
+        def g_fin(c):
+            mean[c] = tri.tile([P, CL], BF16, name="mean", align_bytes=64)
+            nc.gpsimd.tensor_tensor(out=rowpairs(mean[c][:])[:, 3:4, 1, :], in0=rowpairs(box[c][:])[:, 3:4, 1, :],
+                                    in1=hrow[c][:, 3:4, :], op=SUB)
+
+        def v_fin(c):
+            nc.vector.scalar_tensor_tensor(out=rowpairs(mean[c][:])[:, :, 0, :],
+                                           in0=bank(c, "D").rearrange("p (k c) -> p k c", c=RL),
+                                           scalar=-0.125, in1=rowpairs(box[c][:])[:, :, 0, :], op0=MULT, op1=ADD)
+
+        def v_fin2(c):
+            nc.vector.scalar_tensor_tensor(out=rowpairs(mean[c][:])[:, 0:3, 1, :],
+                                           in0=bank(c, "E")[:, 0:3 * RL].rearrange("p (k c) -> p k c", c=RL),
+                                           scalar=-0.125, in1=rowpairs(box[c][:])[:, 0:3, 1, :], op0=MULT, op1=ADD)
 
         def v_q(src, codes, scales, c, nm):
             codes[c] = tri.tile([P, PIX], U32, name=nm + "c", align_bytes=64)
@@ -396,6 +409,7 @@ def tile_staticgraphmodule_t_kernel(tc, x, Wp, b, out):
                 v_pad(v1)
                 box[v1] = dbl.tile([P, CL], F32, name="box")
                 box_sums(nc.gpsimd, v1, 0, ROWS)
+                g_fin(v1)
             issue()
             if v0 >= 0:
                 v_pv(v0)
@@ -414,7 +428,7 @@ def tile_staticgraphmodule_t_kernel(tc, x, Wp, b, out):
                 pe_mm(pm, 0)
                 s_mean(pm, 0)
             if v1 >= 0:
-                pe_b2(v1, "D", (1, 2, 3, 4))
+                pe_b2(v1, "D", (1, 3, 5, 7))
             finish(1, lim)
             if v0 >= 0:
                 v_cv(v0, 1)
@@ -423,7 +437,7 @@ def tile_staticgraphmodule_t_kernel(tc, x, Wp, b, out):
                 pe_mm(pm, 1)
                 s_mean(pm, 1)
             if v1 >= 0:
-                pe_b2(v1, "E", (5, 6, 7, 8))
+                pe_b2(v1, "E", (2, 4, 6))
             finish(1, lim)
             if pm >= 0:
                 pe_mm(pm, 2)
@@ -446,8 +460,8 @@ def tile_staticgraphmodule_t_kernel(tc, x, Wp, b, out):
             if len(nfl) > 0:
                 s_xb(nfl[0])
             if v1 >= 0:
-                v_fin(v1, 0)
+                v_fin(v1)
             finish(1, lim)
             if v1 >= 0:
-                v_fin(v1, 1)
+                v_fin2(v1)
             finish(n, lim)

@@ -17,19 +17,29 @@ ACT = mybir.ActivationFunctionType
 P = 128
 PACK = 4
 ROWS = 8
+NB = ROWS + 2
 W_IMG = 64
 H_IMG = 64
 PIX = ROWS * W_IMG
 IMG = H_IMG * W_IMG
 RL = W_IMG * PACK
 CL = PIX * PACK
-HL = CL // 2
 PRL = (W_IMG + 2) * PACK
 CPI = H_IMG // ROWS
 NCH = 2 * CPI
-PE_CHUNKS = (2, 5, 7, 10, 12, 15)
-KT = ROWS // 2 + 1
-NB = ROWS + 2
+
+HALO = NB * W_IMG
+XT = PACK * HALO
+HW = W_IMG // 2
+WR = P // HW
+NWR = ROWS // 2
+OV = HW + 2
+
+V_CHUNKS = (3, 7, 11, 14)
+NACC = 4
+NSTG = 4
+S_STRIP = ()
+GS = 4
 
 FLOPS = 2 * 512 * 1024 * 8192
 
@@ -44,202 +54,160 @@ def tile_staticgraphmodule_t_kernel(tc, x, Wp, b, out):
         tmp = ctx.enter_context(tc.tile_pool(name="tmp", bufs=1))
         dbl = ctx.enter_context(tc.tile_pool(name="dbl", bufs=2))
         tri = ctx.enter_context(tc.tile_pool(name="tri", bufs=3))
-        ps2 = ctx.enter_context(tc.psum_pool(name="ps2", bufs=2))
-        ps3 = ctx.enter_context(tc.psum_pool(name="ps3", bufs=3))
+        six = ctx.enter_context(tc.tile_pool(name="six", bufs=6))
+        many = ctx.enter_context(tc.tile_pool(name="many", bufs=NCH))
+        ps3 = ctx.enter_context(tc.psum_pool(name="ps3", bufs=NSTG))
+        ps4 = ctx.enter_context(tc.psum_pool(name="ps4", bufs=NACC))
         ctx.enter_context(tc.manual_schedule())
 
-        def ok(c):
-            return 0 <= c < NCH
+        pes = [c for c in range(NCH) if c not in V_CHUNKS]
+        vs = list(V_CHUNKS)
+        npe = len(pes)
 
-        def on_pe(c):
-            return ok(c) and c in PE_CHUNKS
-
-        def vg(c):
-            return ok(c) and not on_pe(c)
-
-        xt = []
-        for c in range(NCH):
-            xt.append(const.tile([P, PACK, PIX + (2 * W_IMG if on_pe(c) else 0)], BF16, name="xt%d" % c))
-        w_sb = tri.tile([P, PACK * 1024], BF16, name="tt", align_bytes=64)
+        xt = {}
         b16 = const.tile([P, PACK], BF16, name="b16")
-
-        def planar(c, p0, p1):
-            halo = W_IMG if on_pe(c) else 0
-            return xt[c][:, :, halo + p0:halo + p1]
-
-        def load_x(c, p0, p1):
-            n, cc = divmod(c, CPI)
-            if on_pe(c):
-                p0 = p0 - W_IMG
-                if cc == CPI - 1:
-                    nc.sync.dma_start(out=planar(c, PIX, PIX + W_IMG), in_=xv[n, :, :, IMG - W_IMG:IMG])
-                else:
-                    p1 = p1 + W_IMG
-            nc.sync.dma_start(out=planar(c, p0, p1), in_=xv[n, :, :, cc * PIX + p0:cc * PIX + p1])
-
         nc.sync.dma_start(out=b16[:], in_=b.rearrange("(p j) -> p j", j=PACK))
-        load_x(0, 0, PIX // 2)
-        load_x(0, PIX // 2, PIX)
-        load_x(1, 0, PIX)
-        load_x(2, 0, PIX)
-        load_x(3, 0, PIX)
-        nc.sync.dma_start(out=w_sb[:], in_=Wp.rearrange("(m j) k -> m (j k)", j=PACK))
-        for c in range(4, NCH):
-            load_x(c, 0, PIX)
+
+        def rows(c, r0, r1):
+            return xt[c][:].rearrange("p (j w) -> p j w", j=PACK)[:, :, r0 * W_IMG:r1 * W_IMG]
+
+        def load_x(c):
+            n, cc = divmod(c, CPI)
+            xt[c] = many.tile([P, XT], BF16, name="xt", align_bytes=64)
+            first = cc * ROWS - 1
+            lo = 1 if cc == 0 else 0
+            hi = NB - 1 if cc == CPI - 1 else NB
+            if cc == 0:
+                nc.sync.dma_start(out=rows(c, 0, 1), in_=xv[n, :, :, 0:W_IMG])
+            nc.sync.dma_start(out=rows(c, lo, hi), in_=xv[n, :, :, (first + lo) * W_IMG:(first + hi) * W_IMG])
+            if cc == CPI - 1:
+                nc.sync.dma_start(out=rows(c, NB - 1, NB), in_=xv[n, :, :, IMG - W_IMG:IMG])
+
+        w_sb = tri.tile([P, PACK * 1024], BF16, name="tt", align_bytes=64)
+        load_order = [pes[0], "w", vs[0], pes[1], pes[2], pes[3], pes[4], vs[1], pes[5], pes[6], pes[7], vs[2], pes[8], pes[9], pes[10], vs[3], pes[11]]
+        for c in load_order:
+            if c == "w":
+                nc.sync.dma_start(out=w_sb[:], in_=Wp.rearrange("(m j) k -> m (j k)", j=PACK))
+            else:
+                load_x(c)
 
         ident = const.tile([P, P], F32, name="ident")
         make_identity(nc, ident[:])
         identb = const.tile([P, P], BF16, name="identb")
         make_identity(nc, identb[:])
 
-        xgi = const.tile([P, (H_IMG + 2) * RL], BF16, name="xgi", align_bytes=64)
         b32 = const.tile([P, PACK], F32, name="b32")
         nb32 = const.tile([P, PACK], F32, name="nb32")
         wg = tri.tile([P, 8 * P * PACK], BF16, name="tt", align_bytes=64)
         wcodes = const.tile([P, 8 * P], U32, name="wcodes", align_bytes=64)
         wscales = const.tile([P, 8 * P], U8, name="wscales", align_bytes=64)
-        jt = const.tile([P, 2, W_IMG + 2], BF16, name="jt")
-        h8 = const.tile([P, 2, W_IMG], BF16, name="h8")
-        h3 = const.tile([P, 2, W_IMG], BF16, name="h3")
-        sa = const.tile([P, 2, W_IMG], BF16, name="sa")
-        sb = const.tile([P, 2, W_IMG], BF16, name="sb")
 
-        def grouped_view(flat):
-            return flat.rearrange("p (c i t) -> p c t i", i=4, t=PACK)
+        e = const.tile([P, 2, WR, OV + 2], BF16, name="e")
+        h2 = const.tile([P, 2, WR, OV], BF16, name="h2")
+        h3 = const.tile([P, 2, WR, OV], BF16, name="h3")
+        hs = const.tile([P, 2, 2, OV], BF16, name="hs")
+        band = const.tile([P, 2, 2, OV], BF16, name="band")
+        idq = identb[:].rearrange("p (r q) -> p r q", q=HW)
+        nc.vector.memset(e[:], 0.0)
+        nc.vector.tensor_scalar_mul(e[:, 0, :, 1:1 + HW], idq, 0.125)
+        nc.vector.tensor_scalar_mul(e[:, 1, :, 3:3 + HW], idq, 0.125)
+        nc.vector.tensor_copy(out=e[:, 0, :, 0:1], in_=e[:, 0, :, 1:2])
+        nc.vector.tensor_copy(out=e[:, 1, :, OV + 1:OV + 2], in_=e[:, 1, :, OV:OV + 1])
+        nc.vector.tensor_tensor(out=h2[:], in0=e[:, :, :, 0:OV], in1=e[:, :, :, 2:OV + 2], op=ADD)
+        nc.vector.tensor_tensor(out=h3[:], in0=h2[:], in1=e[:, :, :, 1:OV + 1], op=ADD)
+        nc.vector.tensor_tensor(out=hs[:], in0=h3[:, :, 0:2, :], in1=h3[:, :, 2:4, :], op=ADD)
+        nc.vector.tensor_tensor(out=band[:], in0=hs[:], in1=h2[:, :, 1:3, :], op=ADD)
 
-        def planar_view(pl):
-            return pl.rearrange("p t (c i) -> p c t i", i=4)
-
+        strip = {}
+        xg = {}
+        mean = {}
+        xts = {}
+        stg = {}
+        xps = {}
+        xtr = {}
+        hrow = {}
+        pv = {}
         cv = {}
         ph = {}
         box = {}
-        mean = {}
         xc = {}
         xs = {}
         mc = {}
         ms = {}
         acc = {}
         tt = {}
-        hrow = {}
-        pv = {}
-        stg = {}
-        xts = {}
-        xtr = {}
-        xps = {}
+        xb = {}
 
-        def base_of(c):
-            return (1 + (c % CPI) * ROWS) * RL
+        def new_xg(c):
+            if c in vs:
+                xg[c] = dbl.tile([P, NB * RL], BF16, name="xgv", align_bytes=64)
+            else:
+                xg[c] = tri.tile([P, CL], BF16, name="xg", align_bytes=64)
 
-        def v_xg(c):
-            nc.vector.tensor_copy(out=grouped_view(xgi[:, base_of(c):base_of(c) + CL]), in_=planar_view(planar(c, 0, PIX)))
+        def interleave(eng, c, part, parts):
+            r0, r1 = (0, NB) if c in vs else (1, NB - 1)
+            if part == 0:
+                new_xg(c)
+            h = (r1 - r0) // parts
+            dst = xg[c][:, part * h * RL:(part + 1) * h * RL].rearrange("p (c i t) -> p c t i", i=4, t=PACK)
+            src = rows(c, r0 + part * h, r0 + (part + 1) * h).rearrange("p t (c i) -> p c t i", i=4)
+            if eng == "v":
+                nc.vector.tensor_copy(out=dst, in_=src)
+            else:
+                nc.scalar.copy(dst, src)
 
-        def s_xg(c):
-            cc = c % CPI
-            parts = 2 if c == 0 else 1
-            for part in range(parts):
-                nc.scalar.copy(grouped_view(xgi[:, base_of(c) + part * CL // parts:base_of(c) + (part + 1) * CL // parts]),
-                               planar_view(planar(c, part * PIX // parts, (part + 1) * PIX // parts)))
-                if cc == 0 and part == 0:
-                    nc.scalar.copy(grouped_view(xgi[:, 0:RL]), planar_view(planar(c, 0, W_IMG)))
-            if cc == CPI - 1:
-                nc.scalar.copy(grouped_view(xgi[:, (H_IMG + 1) * RL:(H_IMG + 2) * RL]),
-                               planar_view(planar(c, PIX - W_IMG, PIX)))
+        def v_strip(c, eng="v"):
+            strip[c] = dbl.tile([P, XT], BF16, name="strip", align_bytes=64)
+            dst = strip[c][:].rearrange("p (s g w) -> p s g w", s=2, w=HW)
+            src = xt[c][:].rearrange("p (g s w) -> p s g w", s=2, w=HW)
+            if eng == "v":
+                nc.vector.tensor_copy(out=dst, in_=src)
+            else:
+                nc.scalar.copy(dst, src)
 
-        def s_xb(c):
-            tt[c] = tri.tile([P, PACK, PIX], F32, name="tt", align_bytes=64)
+        def pe_t(c, g):
+            if g == 0:
+                xts[c] = dbl.tile([P, NWR, 2, PACK, P], BF16, name="xts")
+            stg[(c, "t", g)] = ps3.tile([P, 2, PACK, P], BF16, name="stg")
+            for s in range(2):
+                for j in range(PACK):
+                    o = ((s * PACK + j) * NB + 2 * g) * HW
+                    nc.tensor.transpose(stg[(c, "t", g)][:, s, j, :], strip[c][:, o:o + P], identb[:])
+
+        def s_t(c, g):
+            nc.scalar.copy(xts[c][:, g], stg[(c, "t", g)][:])
+
+        def pe_m(c, g):
+            if g == 0:
+                mean[c] = tri.tile([P, CL], BF16, name="mean", align_bytes=64)
+            t = ps3.tile([P, PACK, 2, W_IMG], F32, name="stg")
+            stg[(c, "m", g)] = t
             for j in range(PACK):
-                nc.scalar.activation(out=tt[c][:, j, :], in_=planar(c, 0, PIX)[:, j, :], func=ACT.Identity,
-                                     bias=b32[:, j:j + 1], scale=1.0)
+                left, right = xts[c][:, g, 0, j, :], xts[c][:, g, 1, j, :]
+                nc.tensor.matmul(out=t[:, j, :, 0:OV], lhsT=left, rhs=band[:, 0], start=True, stop=False)
+                nc.tensor.matmul(out=t[:, j, :, HW - 2:OV], lhsT=right, rhs=band[:, 1, :, 0:4], start=False, stop=True)
+                nc.tensor.matmul(out=t[:, j, :, OV:W_IMG], lhsT=right, rhs=band[:, 1, :, 4:OV], start=True, stop=True)
 
-        def s_xt(c, g):
-            q0, q1 = 2 * g, min(2 * g + 2, KT)
-            nc.scalar.copy(xts[c][:, q0:q1, :, :], stg[(c, "t", g)][:, 0:q1 - q0, :, :])
-
-        def s_mean(c, t):
-            nc.scalar.copy(mean[c][:, t * 2 * RL:(t + 1) * 2 * RL].rearrange("p (n j) -> p n j", j=PACK),
-                           stg[(c, "m", t)][:].rearrange("p j n -> p n j"))
-
-        def s_b1(c, g):
-            r0, r1 = 4 * g, min(4 * g + 4, NB)
-            nc.scalar.copy(xtr[c][:, r0:r1, :], stg[(c, "b", g)][:, 0:r1 - r0, :])
+        def s_m(c, g):
+            dst = mean[c][:, g * 2 * RL:(g + 1) * 2 * RL].rearrange("p (n j) -> p n j", j=PACK)
+            nc.scalar.copy(dst, stg[(c, "m", g)][:].rearrange("p j r w -> p (r w) j"))
 
         def rows2(c, first):
-            r0 = (c % CPI) * ROWS + first
-            return xgi[:, r0 * RL:(r0 + ROWS) * RL].rearrange("p (k t c) -> p k t c", t=2, c=RL)
-
-        def pe_b1(c, g):
-            if g == 0:
-                xtr[c] = tri.tile([P, NB, P], F32, name="xtr")
-            stg[(c, "b", g)] = ps3.tile([P, 4, P], F32, name="stg")
-            for r in range(4 * g, min(4 * g + 4, NB)):
-                row = (c % CPI) * ROWS + r
-                nc.tensor.transpose(stg[(c, "b", g)][:, r - 4 * g, :], xgi[:, row * RL:(row + 1) * RL].bitcast(F32), ident[:])
-
-        def pe_b2(c, key, slots):
-            xps[(c, key)] = ps2.tile([P, 4, P], F32, name="xps")
-            for q in range(len(slots)):
-                nc.tensor.transpose(xps[(c, key)][:, q, :], xtr[c][:, slots[q], :], ident[:])
-
-        def bank(c, key):
-            return xps[(c, key)][:].rearrange("p q m -> p (q m)").bitcast(BF16)
-
-        def pe_t1(c, g):
-            if g == 0:
-                xts[c] = dbl.tile([P, KT, PACK, P], BF16, name="xts")
-            stg[(c, "t", g)] = ps3.tile([P, 2, PACK, P], BF16, name="stg")
-            for q in range(2 * g, min(2 * g + 2, KT)):
-                for j in range(PACK):
-                    nc.tensor.transpose(stg[(c, "t", g)][:, q - 2 * g, j, :], xt[c][:, j, q * P:(q + 1) * P], identb[:])
-
-        def pe_mm(c, t):
-            if t == 0:
-                mean[c] = tri.tile([P, CL], BF16, name="mean", align_bytes=64)
-            stg[(c, "m", t)] = ps3.tile([P, PACK, P], F32, name="stg")
-            for j in range(PACK):
-                nc.tensor.matmul(out=stg[(c, "m", t)][:, j, :], lhsT=xts[c][:, t, j, :],
-                                 rhs=sa[:].rearrange("p a w -> p (a w)"), start=True, stop=False)
-                nc.tensor.matmul(out=stg[(c, "m", t)][:, j, :], lhsT=xts[c][:, t + 1, j, :],
-                                 rhs=sb[:].rearrange("p a w -> p (a w)"), start=False, stop=True)
-
-        def pe_mx(c, j):
-            acc[(c, j)] = ps3.tile([P, PIX], F32, name="acc")
-            for s, codes, scales in ((0, xc, xs), (1, mc, ms)):
-                cols = slice((s * PACK + j) * P, (s * PACK + j + 1) * P)
-                nc.tensor.matmul_mx(out=acc[(c, j)][:],
-                                    lhsT=wcodes[:, cols].bitcast(FP8X4), lhsT_scale=wscales[:, cols],
-                                    rhs=codes[c][:].bitcast(FP8X4), rhs_scale=scales[c][:],
-                                    start=(s == 0), stop=(s == 1))
-
-        def w_transposes():
-            wf = w_sb[:].bitcast(F32).rearrange("p (j s q u) -> p j s q u", j=PACK, s=2, u=2)
-            wgf = wg[:].bitcast(F32).rearrange("p (g m u) -> p g m u", m=P, u=2)
-            for half in range(4):
-                pw = ps3.tile([P, 2, 2, P], F32, name="acc")
-                for gi in range(2):
-                    s, j = divmod(half * 2 + gi, PACK)
-                    for u in range(2):
-                        nc.tensor.transpose(pw[:, gi, u, :], wf[:, j, s, :, u], ident[:])
-                nc.vector.tensor_copy(out=wgf[:, half * 2:half * 2 + 2, :, :], in_=pw[:].rearrange("p g u m -> p g m u"))
+            return xg[c][:, first * RL:(first + ROWS) * RL].rearrange("p (k t c) -> p k t c", t=2, c=RL)
 
         def v_hrow(c):
             hrow[c] = dbl.tile([P, ROWS // 2, RL], BF16, name="hrow")
             nc.vector.tensor_scalar_mul(hrow[c][:], rows2(c, 1)[:, :, 1, :], 0.125)
 
-        def rows_of(c, key, direct_view):
-            if (c, key) in xps:
-                return bank(c, key).rearrange("p (k c) -> p k c", c=RL)
-            return direct_view
-
         def v_pv(c):
             pv[c] = tmp.tile([P, ROWS // 2, RL], F32, name="pv")
-            nc.vector.scalar_tensor_tensor(out=pv[c][:], in0=rows_of(c, "C", rows2(c, 1)[:, :, 0, :]), scalar=0.125,
-                                           in1=hrow[c][:], op0=MULT, op1=ADD)
+            nc.vector.scalar_tensor_tensor(out=pv[c][:], in0=rows2(c, 1)[:, :, 0, :], scalar=0.125, in1=hrow[c][:], op0=MULT, op1=ADD)
 
         def v_cv(c, par):
             if par == 0:
-                cv[c] = dbl.tile([P, ROWS, PRL], F32, name="cv")
+                cv[c] = tmp.tile([P, ROWS, PRL], F32, name="cv")
             cvk = cv[c][:].rearrange("p (k t) c -> p k t c", t=2)
-            other = rows_of(c, "A", rows2(c, 0)[:, :, 0, :]) if par == 0 else rows_of(c, "B", rows2(c, 2)[:, :, 1, :])
+            other = rows2(c, 0)[:, :, 0, :] if par == 0 else rows2(c, 2)[:, :, 1, :]
             nc.vector.scalar_tensor_tensor(out=cvk[:, :, par, PACK:PACK + RL], in0=other, scalar=0.125,
                                            in1=pv[c][:], op0=MULT, op1=ADD)
 
@@ -250,218 +218,228 @@ def tile_staticgraphmodule_t_kernel(tc, x, Wp, b, out):
         def pairs(c, first):
             return cv[c][:, :, first * PACK:first * PACK + RL].rearrange("p r (i t j) -> p r i t j", t=2, j=PACK)
 
-        def ph_sums(eng, c):
+        def v_ph(c):
             ph[c] = tmp.tile([P, ROWS, W_IMG // 2, PACK], F32, name="ph")
-            eng.tensor_tensor(out=ph[c][:], in0=pairs(c, 1)[:, :, :, 0, :], in1=pairs(c, 1)[:, :, :, 1, :], op=ADD)
+            nc.vector.tensor_tensor(out=ph[c][:], in0=pairs(c, 1)[:, :, :, 0, :], in1=pairs(c, 1)[:, :, :, 1, :], op=ADD)
 
-        def box_sums(eng, c, r0, r1):
+        def v_box(c, half):
+            if half == 0:
+                box[c] = tmp.tile([P, CL], F32, name="box")
             b4 = box[c][:].rearrange("p (r i t j) -> p r i t j", i=W_IMG // 2, t=2, j=PACK)
-            eng.tensor_tensor(out=b4[:, r0:r1, :, 0, :], in0=pairs(c, 0)[:, r0:r1, :, 0, :], in1=ph[c][:, r0:r1], op=ADD)
-            eng.tensor_tensor(out=b4[:, r0:r1, :, 1, :], in0=ph[c][:, r0:r1], in1=pairs(c, 2)[:, r0:r1, :, 1, :], op=ADD)
+            if half == 0:
+                nc.vector.tensor_tensor(out=b4[:, :, :, 0, :], in0=pairs(c, 0)[:, :, :, 0, :], in1=ph[c][:], op=ADD)
+            else:
+                nc.vector.tensor_tensor(out=b4[:, :, :, 1, :], in0=ph[c][:], in1=pairs(c, 2)[:, :, :, 1, :], op=ADD)
 
         def rowpairs(flat):
             return flat.rearrange("p (k t c) -> p k t c", t=2, c=RL)
 
-        def g_fin(c):
-            mean[c] = tri.tile([P, CL], BF16, name="mean", align_bytes=64)
-            nc.gpsimd.tensor_tensor(out=rowpairs(mean[c][:])[:, 3:4, 1, :], in0=rowpairs(box[c][:])[:, 3:4, 1, :],
-                                    in1=hrow[c][:, 3:4, :], op=SUB)
+        def v_fin(c, par):
+            if par == 0:
+                mean[c] = tri.tile([P, CL], BF16, name="mean", align_bytes=64)
+            nc.vector.scalar_tensor_tensor(out=rowpairs(mean[c][:])[:, :, par, :], in0=rows2(c, 1)[:, :, par, :],
+                                           scalar=-0.125, in1=rowpairs(box[c][:])[:, :, par, :], op0=MULT, op1=ADD)
 
-        def v_fin(c):
-            nc.vector.scalar_tensor_tensor(out=rowpairs(mean[c][:])[:, :, 0, :],
-                                           in0=bank(c, "D").rearrange("p (k c) -> p k c", c=RL),
-                                           scalar=-0.125, in1=rowpairs(box[c][:])[:, :, 0, :], op0=MULT, op1=ADD)
-
-        def v_fin2(c):
-            nc.vector.scalar_tensor_tensor(out=rowpairs(mean[c][:])[:, 0:3, 1, :],
-                                           in0=bank(c, "E")[:, 0:3 * RL].rearrange("p (k c) -> p k c", c=RL),
-                                           scalar=-0.125, in1=rowpairs(box[c][:])[:, 0:3, 1, :], op0=MULT, op1=ADD)
-
-        def v_q(src, codes, scales, c, nm):
+        def quant(src, codes, scales, c, nm):
             codes[c] = tri.tile([P, PIX], U32, name=nm + "c", align_bytes=64)
             scales[c] = tri.tile([P, PIX], U8, name=nm + "s", align_bytes=64)
             nc.vector.quantize_mx(out=codes[c][:].bitcast(FP8X4), scales=scales[c][:], in_=src)
 
+        def q_x(c):
+            quant(xg[c][:, RL:RL + CL] if c in vs else xg[c][:], xc, xs, c, "x")
+
+        def q_m(c):
+            quant(mean[c][:], mc, ms, c, "m")
+            pass
+
+        def pe_mx(c, j):
+            acc[(c, j)] = ps4.tile([P, PIX], F32, name="acc")
+            for s, codes, scales in ((0, xc, xs), (1, mc, ms)):
+                cols = slice((s * PACK + j) * P, (s * PACK + j + 1) * P)
+                nc.tensor.matmul_mx(out=acc[(c, j)][:],
+                                    lhsT=wcodes[:, cols].bitcast(FP8X4), lhsT_scale=wscales[:, cols],
+                                    rhs=codes[c][:].bitcast(FP8X4), rhs_scale=scales[c][:],
+                                    start=(s == 0), stop=(s == 1))
+
+        gate = {}
+
+        def v_gate():
+            gate["b"] = dbl.tile([P, PACK], F32, name="bk")
+            nc.vector.tensor_copy(out=gate["b"][:], in_=b16[:])
+
+        def x_b(c, j):
+            xb[(c, j)] = six.tile([P, PIX], F32, name="xb")
+            nc.gpsimd.tensor_scalar(out=xb[(c, j)][:], in0=rows(c, 1, NB - 1)[:, j, :], scalar1=1.0, scalar2=gate["b"][:, j:j + 1], op0=MULT, op1=ADD)
+
         def v_res(c, j, last):
             n, cc = divmod(c, CPI)
+            if j == 0:
+                tt[c] = tri.tile([P, PACK, PIX], F32, name="tt", align_bytes=64)
             nc.vector.scalar_tensor_tensor(out=tt[c][:, j, :], in0=acc[(c, j)][:], scalar=nb32[:, j:j + 1],
-                                           in1=tt[c][:, j, :], op0=MAX, op1=ADD)
+                                           in1=xb[(c, j)][:], op0=MAX, op1=ADD)
             if last:
                 nc.sync.dma_start(out=ov[n, :, j, cc * PIX:(cc + 1) * PIX], in_=tt[c][:, j, :])
             elif j == PACK - 1:
                 nc.sync.dma_start(out=ov[n, :, :, cc * PIX:(cc + 1) * PIX], in_=tt[c][:])
 
-        nc.vector.tensor_scalar_mul(jt[:, :, 1:W_IMG + 1], identb[:].rearrange("p (a w) -> p a w", a=2), 0.125)
-        nc.vector.tensor_copy(out=jt[:, :, 0:W_IMG + 2:W_IMG + 1], in_=jt[:, :, 1:W_IMG + 1:W_IMG - 1])
-        nc.vector.tensor_tensor(out=h8[:], in0=jt[:, :, 0:W_IMG], in1=jt[:, :, 2:W_IMG + 2], op=ADD)
-        nc.vector.tensor_tensor(out=h3[:], in0=h8[:], in1=jt[:, :, 1:W_IMG + 1], op=ADD)
-        nc.vector.tensor_tensor(out=sa[:, 0, :], in0=h3[:, 0, :], in1=h8[:, 1, :], op=ADD)
-        nc.vector.tensor_copy(out=sa[:, 1, :], in_=h3[:, 1, :])
-        nc.vector.tensor_copy(out=sb[:, 0, :], in_=h3[:, 0, :])
-        nc.vector.tensor_tensor(out=sb[:, 1, :], in0=h8[:, 0, :], in1=h3[:, 1, :], op=ADD)
+        def w_group(eng, h):
+            wf = w_sb[:].bitcast(F32).rearrange("p (j s q u) -> p j s q u", j=PACK, s=2, u=2)
+            wgf = wg[:].bitcast(F32).rearrange("p (g m u) -> p g m u", m=P, u=2)
+            pw = ps4.tile([P, 2, 2, P], F32, name="acc")
+            for gi in range(2):
+                s, j = divmod(h * 2 + gi, PACK)
+                for u in range(2):
+                    nc.tensor.transpose(pw[:, gi, u, :], wf[:, j, s, :, u], ident[:])
+            dst, src = wgf[:, h * 2:h * 2 + 2, :, :], pw[:].rearrange("p g u m -> p g m u")
+            if eng == "v":
+                nc.vector.tensor_copy(out=dst, in_=src)
+            else:
+                nc.scalar.copy(dst, src)
+
+        order = [pes[0], pes[1]]
+        for m in range(4):
+            order += [c for c in (pes[3 * m + 2], vs[m])]
+            if m < 3:
+                order += [pes[3 * m + 3], pes[3 * m + 4]]
+        units = [(c, j) for c in order for j in range(PACK)]
+        st = {"done": 0, "mx": 0, "x_b": 0, "ready": 0}
+
+        def xb_to(n):
+            while st["x_b"] < min(n, len(units)):
+                x_b(units[st["x_b"]][0], units[st["x_b"]][1])
+                st["x_b"] += 1
+
+        def mx_to(n):
+            while st["mx"] < min(n, st["ready"], st["done"] + NACC):
+                pe_mx(units[st["mx"]][0], units[st["mx"]][1])
+                st["mx"] += 1
+
+        def fin():
+            if st["done"] < st["mx"]:
+                c, j = units[st["done"]]
+                v_res(c, j, c == order[-1])
+                st["done"] += 1
+
+        def qx(k):
+            if 0 <= k < npe:
+                q_x(pes[k])
+
+        def qm(k):
+            if 0 <= k < npe:
+                q_m(pes[k])
+                st["ready"] += PACK
+
+        def strip_of(k):
+            if 0 <= k < npe:
+                v_strip(pes[k], "s" if k in S_STRIP else "v")
+
+        def qv(m):
+            if 0 <= m < 4:
+                q_x(vs[m])
+                v_gate()
+                q_m(vs[m])
+                st["ready"] += PACK
+
+        def vop(m, i):
+            if m >= 4:
+                return
+            c = vs[m]
+            if i == 0:
+                v_pv(c)
+            elif i < 3:
+                v_cv(c, i - 1)
+            elif i == 3:
+                v_pad(c)
+                v_gate()
+                v_ph(c)
+            elif i < 6:
+                v_box(c, i - 4)
+            else:
+                v_fin(c, i - 6)
+
+        SEQ = (("t", 0), ("t", 1), ("m", 0), ("t", 2), ("m", 1), ("t", 3), ("m", 2), ("m", 3))
+
+        def group(k, i):
+            if 0 <= k < npe:
+                kind, g = SEQ[i]
+                if kind == "t":
+                    pe_t(pes[k], g)
+                    s_t(pes[k], g)
+                else:
+                    pe_m(pes[k], g)
+                    s_m(pes[k], g)
+
+        def s_xg(k, part):
+            if 0 <= k < npe:
+                interleave("s", pes[k], part, 2)
+
+        v_strip(pes[0])
+        interleave("v", pes[0], 0, 1)
         nc.vector.tensor_copy(out=b32[:], in_=b16[:])
         nc.vector.tensor_scalar_mul(nb32[:], b16[:], -1.0)
+        q_x(pes[0])
+        group(0, 0)
+        group(0, 1)
+        group(0, 3)
+        w_group("v", 0)
+        group(0, 2)
+        group(0, 5)
+        w_group("s", 1)
+        group(0, 4)
+        interleave("v", vs[0], 0, 2)
+        interleave("v", vs[0], 1, 2)
+        v_strip(pes[1])
+        w_group("v", 2)
+        group(0, 6)
+        w_group("v", 3)
+        group(0, 7)
+        v_gate()
+        xb_to(2)
+        s_xg(1, 0)
+        s_xg(1, 1)
+        nc.vector.quantize_mx(out=wcodes[:].bitcast(FP8X4), scales=wscales[:], in_=wg[:])
+        qm(0)
+        v_gate()
 
-        vlist = [c for c in range(NCH) if vg(c)]
-        nv = len(vlist)
-        nper = nv + 2
-
-        def vch(k):
-            return vlist[k] if 0 <= k < nv else -1
-
-        order = []
-        avail = []
-        for k in range(nv):
-            v = vlist[k]
-            if on_pe(v + 1) and v + 1 == NCH - 1:
-                order.append(v + 1)
-                avail.append(k + 1)
-            order.append(v)
-            avail.append(k + 2)
-            if on_pe(v + 1) and v + 1 < NCH - 1:
-                order.append(v + 1)
-                avail.append(k + 2)
-        allunits = [(c, j) for c in order for j in range(PACK)]
-        upto = {}
-        for k in range(-2, nper):
-            quota = (len(allunits) * (k - 1) + nv // 2) // nv if k >= 2 else 0
-            there = PACK * len([a for a in avail if a <= k])
-            for i in range(len(order)):
-                if avail[i] > k:
-                    there = min(there, PACK * i)
-            upto[k] = min(quota, there) if k < nper - 1 else len(allunits)
-        start_of = {}
-        for k in range(-2, nper + 1):
-            start_of[k] = []
-        for i in range(len(order)):
-            for k in range(2, nper):
-                if upto[k - 1] <= PACK * i < upto[k]:
-                    start_of[k].append(order[i])
-        mm_of = {}
-        t1_of = {}
-        for k in range(nper):
-            for c in start_of[k]:
-                if on_pe(c):
-                    mm_of[k - 1] = c
-                    t1_of[k - 2] = c
-        a_of = {}
-        done = 0
-        for k in range(-2, nper):
-            lim = min(vch(k + 2) + 1, NCH - 1) if k + 2 < nv else NCH - 1
-            a_of[k] = list(range(done, lim + 1))
-            done = max(done, lim + 1)
-
-        def bounce(c):
-            for g in range(3):
-                pe_b1(c, g)
-                s_b1(c, g)
-
-        def q_x(c):
-            if c not in xc:
-                v_q(xgi[:, base_of(c):base_of(c) + CL], xc, xs, c, "x")
-
-        st = {"issued": 0, "done": 0, "ready": 0}
-
-        def issue():
-            while st["issued"] < min(st["done"] + 3, st["ready"]):
-                pe_mx(allunits[st["issued"]][0], allunits[st["issued"]][1])
-                st["issued"] += 1
-
-        def finish(m, lim):
-            for i in range(m):
-                if st["done"] < lim:
-                    c, j = allunits[st["done"]]
-                    v_res(c, j, c == order[-1])
-                    st["done"] += 1
-                    issue()
-
-        for k in range(-2, nper):
-            v0, v1 = vch(k), vch(k - 1)
-            fl = start_of[k]
-            nfl = start_of[k + 1]
-            aj = a_of[k]
-            pm = mm_of.get(k, -1)
-            pt = t1_of.get(k, -1)
-            lim = upto[k]
-            n = lim - st["done"]
-
-            if v0 >= 0 and k > 0:
-                pe_b2(v0, "C", (1, 3, 5, 7))
-                pe_b2(v0, "A", (0, 2, 4, 6))
-            if v0 >= 0:
-                v_hrow(v0)
-            if len(aj) > 0 and k != 0:
-                s_xg(aj[0])
-            if k == -2:
-                for c in aj[1:]:
-                    v_xg(c)
-            if k > 0 and vch(k + 1) >= 0:
-                bounce(vch(k + 1))
-            if k == 2:
-                nc.vector.quantize_mx(out=wcodes[:].bitcast(FP8X4), scales=wscales[:], in_=wg[:])
-            for c in fl:
-                q_x(c)
-                v_q(mean[c][:], mc, ms, c, "m")
-                st["ready"] += PACK
-            if len(nfl) > 0:
-                q_x(nfl[0])
-            if v1 >= 0:
-                v_pad(v1)
-                box[v1] = dbl.tile([P, CL], F32, name="box")
-                box_sums(nc.gpsimd, v1, 0, ROWS)
-                g_fin(v1)
-            issue()
-            if v0 >= 0:
-                v_pv(v0)
-            if k == 0:
-                for c in a_of[-1][1:]:
-                    v_xg(c)
-                bounce(vlist[1])
-            if v0 >= 0 and k > 0:
-                pe_b2(v0, "B", (3, 5, 7, 9))
-            finish(1, lim)
-            if v0 >= 0:
-                v_cv(v0, 0)
-            if len(fl) > 1:
-                s_xb(fl[1])
-            if pm >= 0:
-                pe_mm(pm, 0)
-                s_mean(pm, 0)
-            if v1 >= 0:
-                pe_b2(v1, "D", (1, 3, 5, 7))
-            finish(1, lim)
-            if v0 >= 0:
-                v_cv(v0, 1)
-                ph_sums(nc.gpsimd, v0)
-            if pm >= 0:
-                pe_mm(pm, 1)
-                s_mean(pm, 1)
-            if v1 >= 0:
-                pe_b2(v1, "E", (2, 4, 6))
-            finish(1, lim)
-            if pm >= 0:
-                pe_mm(pm, 2)
-                s_mean(pm, 2)
-            finish(1, lim)
-            if pm >= 0:
-                pe_mm(pm, 3)
-                s_mean(pm, 3)
-            finish(n - 5, lim)
-            if k == 0:
-                bounce(vlist[0])
-                w_transposes()
-                s_xg(aj[0])
-            if len(aj) > 1 and k >= 0:
-                s_xg(aj[1])
-            if pt >= 0:
-                for g in range(3):
-                    pe_t1(pt, g)
-                    s_xt(pt, g)
-            if len(nfl) > 0:
-                s_xb(nfl[0])
-            if v1 >= 0:
-                v_fin(v1)
-            finish(1, lim)
-            if v1 >= 0:
-                v_fin2(v1)
-            finish(n, lim)
+        for m in range(5):
+            b = 3 * m
+            for s in range(16):
+                for i in range(24):
+                    if 2 * i // 3 == s:
+                        group(b + 1 + i // 8, i % 8)
+                if s in (1, 4):
+                    s_xg(b + 2, (1, 4).index(s))
+                if s in (7, 10):
+                    s_xg(b + 3, (7, 10).index(s))
+                if s in (12, 15):
+                    s_xg(b + 4, (12, 15).index(s))
+                if s in (3, 9) and m < 3:
+                    interleave("s", vs[m + 1], (3, 9).index(s), 2)
+                if s % 2 == 1:
+                    vop(m, s // 2)
+                elif s == 0:
+                    if m < 4:
+                        v_hrow(vs[m])
+                    qv(m - 1)
+                elif s == 2:
+                    strip_of(b + 2)
+                elif s == 4:
+                    if m > 0:
+                        qx(b)
+                        v_gate()
+                        qm(b)
+                elif s == 6:
+                    qx(b + 1)
+                elif s == 8:
+                    strip_of(b + 3)
+                elif s == 10:
+                    qm(b + 1)
+                elif s == 12:
+                    qx(b + 2)
+                elif s == 14:
+                    qm(b + 2)
+                    v_gate()
+                    strip_of(b + 4)
+                xb_to(st["done"] + 6)
+                fin()
+                mx_to(st["done"] + 3)

@@ -33,7 +33,11 @@ XT = PACK * HALO
 HW = W_IMG // 2
 WR = P // HW
 NWR = ROWS // 2
-OV = HW + 2
+OV = HW + 1
+WM = 2
+AHEAD = 8
+S_LAST = 12
+XB = 4
 
 V_CHUNKS = (3, 7, 11, 14)
 NACC = 4
@@ -54,7 +58,8 @@ def tile_staticgraphmodule_t_kernel(tc, x, Wp, b, out):
         tmp = ctx.enter_context(tc.tile_pool(name="tmp", bufs=1))
         dbl = ctx.enter_context(tc.tile_pool(name="dbl", bufs=2))
         tri = ctx.enter_context(tc.tile_pool(name="tri", bufs=3))
-        six = ctx.enter_context(tc.tile_pool(name="six", bufs=6))
+        four = ctx.enter_context(tc.tile_pool(name="four", bufs=5))
+        six = ctx.enter_context(tc.tile_pool(name="six", bufs=XB))
         many = ctx.enter_context(tc.tile_pool(name="many", bufs=NCH))
         ps3 = ctx.enter_context(tc.psum_pool(name="ps3", bufs=NSTG))
         ps4 = ctx.enter_context(tc.psum_pool(name="ps4", bufs=NACC))
@@ -84,7 +89,7 @@ def tile_staticgraphmodule_t_kernel(tc, x, Wp, b, out):
                 nc.sync.dma_start(out=rows(c, NB - 1, NB), in_=xv[n, :, :, IMG - W_IMG:IMG])
 
         w_sb = tri.tile([P, PACK * 1024], BF16, name="tt", align_bytes=64)
-        load_order = [pes[0], "w", vs[0], pes[1], pes[2], pes[3], pes[4], vs[1], pes[5], pes[6], pes[7], vs[2], pes[8], pes[9], pes[10], vs[3], pes[11]]
+        load_order = [pes[0], vs[0], "w", pes[1], pes[2], pes[3], pes[4], vs[1], pes[5], pes[6], pes[7], vs[2], pes[8], pes[9], pes[10], vs[3], pes[11]]
         for c in load_order:
             if c == "w":
                 nc.sync.dma_start(out=w_sb[:], in_=Wp.rearrange("(m j) k -> m (j k)", j=PACK))
@@ -110,12 +115,14 @@ def tile_staticgraphmodule_t_kernel(tc, x, Wp, b, out):
         idq = identb[:].rearrange("p (r q) -> p r q", q=HW)
         nc.vector.memset(e[:], 0.0)
         nc.vector.tensor_scalar_mul(e[:, 0, :, 1:1 + HW], idq, 0.125)
-        nc.vector.tensor_scalar_mul(e[:, 1, :, 3:3 + HW], idq, 0.125)
+        nc.vector.tensor_scalar_mul(e[:, 1, :, 2:2 + HW], idq, 0.125)
         nc.vector.tensor_copy(out=e[:, 0, :, 0:1], in_=e[:, 0, :, 1:2])
         nc.vector.tensor_copy(out=e[:, 1, :, OV + 1:OV + 2], in_=e[:, 1, :, OV:OV + 1])
         nc.vector.tensor_tensor(out=h2[:], in0=e[:, :, :, 0:OV], in1=e[:, :, :, 2:OV + 2], op=ADD)
         nc.vector.tensor_tensor(out=h3[:], in0=h2[:], in1=e[:, :, :, 1:OV + 1], op=ADD)
         nc.vector.tensor_tensor(out=hs[:], in0=h3[:, :, 0:2, :], in1=h3[:, :, 2:4, :], op=ADD)
+        ident2 = const.tile([P, P], F32, name="ident2")
+        nc.vector.tensor_copy(out=ident2[:], in_=ident[:])
         nc.vector.tensor_tensor(out=band[:], in0=hs[:], in1=h2[:, :, 1:3, :], op=ADD)
 
         strip = {}
@@ -179,14 +186,14 @@ def tile_staticgraphmodule_t_kernel(tc, x, Wp, b, out):
 
         def pe_m(c, g):
             if g == 0:
-                mean[c] = tri.tile([P, CL], BF16, name="mean", align_bytes=64)
+                mean[c] = four.tile([P, CL], BF16, name="mean", align_bytes=64)
             t = ps3.tile([P, PACK, 2, W_IMG], F32, name="stg")
             stg[(c, "m", g)] = t
             for j in range(PACK):
                 left, right = xts[c][:, g, 0, j, :], xts[c][:, g, 1, j, :]
                 nc.tensor.matmul(out=t[:, j, :, 0:OV], lhsT=left, rhs=band[:, 0], start=True, stop=False)
-                nc.tensor.matmul(out=t[:, j, :, HW - 2:OV], lhsT=right, rhs=band[:, 1, :, 0:4], start=False, stop=True)
-                nc.tensor.matmul(out=t[:, j, :, OV:W_IMG], lhsT=right, rhs=band[:, 1, :, 4:OV], start=True, stop=True)
+                nc.tensor.matmul(out=t[:, j, :, HW - 1:OV], lhsT=right, rhs=band[:, 1, :, 0:2], start=False, stop=True)
+                nc.tensor.matmul(out=t[:, j, :, OV:W_IMG], lhsT=right, rhs=band[:, 1, :, 2:OV], start=True, stop=True)
 
         def s_m(c, g):
             dst = mean[c][:, g * 2 * RL:(g + 1) * 2 * RL].rearrange("p (n j) -> p n j", j=PACK)
@@ -236,7 +243,7 @@ def tile_staticgraphmodule_t_kernel(tc, x, Wp, b, out):
 
         def v_fin(c, par):
             if par == 0:
-                mean[c] = tri.tile([P, CL], BF16, name="mean", align_bytes=64)
+                mean[c] = four.tile([P, CL], BF16, name="mean", align_bytes=64)
             nc.vector.scalar_tensor_tensor(out=rowpairs(mean[c][:])[:, :, par, :], in0=rows2(c, 1)[:, :, par, :],
                                            scalar=-0.125, in1=rowpairs(box[c][:])[:, :, par, :], op0=MULT, op1=ADD)
 
@@ -269,6 +276,9 @@ def tile_staticgraphmodule_t_kernel(tc, x, Wp, b, out):
 
         def x_b(c, j):
             xb[(c, j)] = six.tile([P, PIX], F32, name="xb")
+            if (c, j) in units[:4] + units[-S_LAST:]:
+                nc.scalar.activation(out=xb[(c, j)][:], in_=rows(c, 1, NB - 1)[:, j, :], func=ACT.Identity, bias=b32[:, j:j + 1], scale=1.0)
+                return
             nc.gpsimd.tensor_scalar(out=xb[(c, j)][:], in0=rows(c, 1, NB - 1)[:, j, :], scalar1=1.0, scalar2=gate["b"][:, j:j + 1], op0=MULT, op1=ADD)
 
         def v_res(c, j, last):
@@ -296,11 +306,13 @@ def tile_staticgraphmodule_t_kernel(tc, x, Wp, b, out):
             else:
                 nc.scalar.copy(dst, src)
 
-        order = [pes[0], pes[1]]
+        order = []
         for m in range(4):
-            order += [c for c in (pes[3 * m + 2], vs[m])]
-            if m < 3:
-                order += [pes[3 * m + 3], pes[3 * m + 4]]
+            order += [pes[3 * m]]
+            if m > 0:
+                order += [vs[m - 1]]
+            order += [pes[3 * m + 1], pes[3 * m + 2]]
+        order += [vs[3]]
         units = [(c, j) for c in order for j in range(PACK)]
         st = {"done": 0, "mx": 0, "x_b": 0, "ready": 0}
 
@@ -373,73 +385,120 @@ def tile_staticgraphmodule_t_kernel(tc, x, Wp, b, out):
             if 0 <= k < npe:
                 interleave("s", pes[k], part, 2)
 
+        def warm_plain(n):
+            t = ps3.tile([P, P], F32, name="stg")
+            for i in range(n):
+                nc.tensor.matmul(out=t[:], lhsT=ident2[:], rhs=ident2[:], start=True, stop=True)
+
+        def warm_mx(n):
+            c = pes[0]
+            t = ps3.tile([P, PIX], F32, name="stg")
+            for i in range(n):
+                nc.tensor.matmul_mx(out=t[:], lhsT=xc[c][:, 0:P].bitcast(FP8X4), lhsT_scale=xs[c][:, 0:P],
+                                    rhs=xc[c][:].bitcast(FP8X4), rhs_scale=xs[c][:], start=True, stop=True)
+
+        warm_plain(3)
         v_strip(pes[0])
         interleave("v", pes[0], 0, 1)
+        q_x(pes[0])
         nc.vector.tensor_copy(out=b32[:], in_=b16[:])
         nc.vector.tensor_scalar_mul(nb32[:], b16[:], -1.0)
-        q_x(pes[0])
         group(0, 0)
+        warm_plain(1)
         group(0, 1)
+        warm_plain(1)
         group(0, 3)
-        w_group("v", 0)
-        group(0, 2)
+        warm_plain(1)
         group(0, 5)
-        w_group("s", 1)
-        group(0, 4)
         interleave("v", vs[0], 0, 2)
         interleave("v", vs[0], 1, 2)
-        v_strip(pes[1])
-        w_group("v", 2)
+        w_group("v", 0)
+        group(0, 2)
+        w_group("v", 1)
+        group(0, 4)
+        v_hrow(vs[0])
         group(0, 6)
-        w_group("v", 3)
+        w_group("s", 2)
         group(0, 7)
-        v_gate()
+        w_group("s", 3)
+        v_strip(pes[1])
+        v_pv(vs[0])
+        warm_mx(3)
         xb_to(2)
-        s_xg(1, 0)
-        s_xg(1, 1)
+        group(1, 0)
+        warm_mx(1)
+        group(1, 1)
+        warm_mx(1)
         nc.vector.quantize_mx(out=wcodes[:].bitcast(FP8X4), scales=wscales[:], in_=wg[:])
         qm(0)
+        v_strip(pes[2])
+        group(1, 3)
+        warm_mx(1)
+        group(1, 2)
+        group(1, 5)
+        xb_to(XB)
+        mx_to(2)
+        group(1, 4)
+        group(1, 6)
+        group(1, 7)
+        v_cv(vs[0], 0)
+        interleave("v", pes[1], 0, 1)
         v_gate()
 
+        V_EARLY = 2
         for m in range(5):
             b = 3 * m
             for s in range(16):
                 for i in range(24):
                     if 2 * i // 3 == s:
-                        group(b + 1 + i // 8, i % 8)
-                if s in (1, 4):
-                    s_xg(b + 2, (1, 4).index(s))
-                if s in (7, 10):
-                    s_xg(b + 3, (7, 10).index(s))
+                        group(b + 1 + (i + AHEAD) // 8, (i + AHEAD) % 8)
+                if s in (1, 3) and m > 0:
+                    s_xg(b + 2, (1, 3).index(s))
+                if s in (7, 9):
+                    s_xg(b + 3, (7, 9).index(s))
                 if s in (12, 15):
                     s_xg(b + 4, (12, 15).index(s))
-                if s in (3, 9) and m < 3:
-                    interleave("s", vs[m + 1], (3, 9).index(s), 2)
+                if s in (5, 11) and m < 3:
+                    interleave("s", vs[m + 1], (5, 11).index(s), 2)
+                start = m == 0 and s < 8
                 if s % 2 == 1:
-                    vop(m, s // 2)
+                    if start:
+                        v_gate()
+                    if m > 0 or s // 2 + V_EARLY < 8:
+                        vop(m, s // 2 + (V_EARLY if m == 0 else 0))
                 elif s == 0:
-                    if m < 4:
+                    if 0 < m < 4:
                         v_hrow(vs[m])
                     qv(m - 1)
                 elif s == 2:
-                    strip_of(b + 2)
-                elif s == 4:
-                    if m > 0:
-                        qx(b)
-                        v_gate()
-                        qm(b)
-                elif s == 6:
-                    qx(b + 1)
-                elif s == 8:
                     strip_of(b + 3)
-                elif s == 10:
-                    qm(b + 1)
-                elif s == 12:
-                    qx(b + 2)
-                elif s == 14:
-                    qm(b + 2)
+                elif s == 4:
+                    qx(b + 1)
                     v_gate()
+                    qm(b + 1)
+                elif s == 6:
+                    if m > 0:
+                        qx(b + 2)
+                    else:
+                        interleave("v", pes[2], 0, 1)
+                elif s == 8:
                     strip_of(b + 4)
-                xb_to(st["done"] + 6)
-                fin()
-                mx_to(st["done"] + 3)
+                elif s == 10:
+                    if m == 0:
+                        qx(b + 2)
+                        v_gate()
+                    qm(b + 2)
+                elif s == 12:
+                    qx(b + 3)
+                elif s == 14:
+                    qm(b + 3)
+                    v_gate()
+                    strip_of(b + 5)
+                xb_to(st["done"] + XB)
+                if not start or s % 2 == 1:
+                    fin()
+                mx_to(st["done"] + (3 if m < 3 else 4))
+                if m == 3 and s >= 6:
+                    t = ps3.tile([P, PIX], F32, name="stg")
+                    nc.tensor.matmul_mx(out=t[:], lhsT=wcodes[:, 0:P].bitcast(FP8X4), lhsT_scale=wscales[:, 0:P],
+                                        rhs=wcodes[:, 0:PIX].bitcast(FP8X4), rhs_scale=wscales[:, 0:PIX], start=True, stop=True)

@@ -36,8 +36,9 @@ NWR = ROWS // 2
 OV = HW + 1
 WM = 2
 AHEAD = 8
-S_LAST = 12
+S_LAST = 16
 XB = 4
+GCOL = 512
 
 V_CHUNKS = (3, 7, 11, 14)
 NACC = 4
@@ -107,6 +108,11 @@ def tile_staticgraphmodule_t_kernel(tc, x, Wp, b, out):
         wcodes = const.tile([P, 8 * P], U32, name="wcodes", align_bytes=64)
         wscales = const.tile([P, 8 * P], U8, name="wscales", align_bytes=64)
 
+        ones = four.tile([P, CL], BF16, name="mean", align_bytes=64)
+        ocodes = const.tile([P, PIX], U32, name="ocodes", align_bytes=64)
+        oscales = const.tile([P, PIX], U8, name="oscales", align_bytes=64)
+        nc.vector.memset(ones[:], 1.0)
+        nc.vector.quantize_mx(out=ocodes[:].bitcast(FP8X4), scales=oscales[:], in_=ones[:])
         e = const.tile([P, 2, WR, OV + 2], BF16, name="e")
         h2 = const.tile([P, 2, WR, OV], BF16, name="h2")
         h3 = const.tile([P, 2, WR, OV], BF16, name="h3")
@@ -121,8 +127,6 @@ def tile_staticgraphmodule_t_kernel(tc, x, Wp, b, out):
         nc.vector.tensor_tensor(out=h2[:], in0=e[:, :, :, 0:OV], in1=e[:, :, :, 2:OV + 2], op=ADD)
         nc.vector.tensor_tensor(out=h3[:], in0=h2[:], in1=e[:, :, :, 1:OV + 1], op=ADD)
         nc.vector.tensor_tensor(out=hs[:], in0=h3[:, :, 0:2, :], in1=h3[:, :, 2:4, :], op=ADD)
-        ident2 = const.tile([P, P], F32, name="ident2")
-        nc.vector.tensor_copy(out=ident2[:], in_=ident[:])
         nc.vector.tensor_tensor(out=band[:], in0=hs[:], in1=h2[:, :, 1:3, :], op=ADD)
 
         strip = {}
@@ -173,7 +177,7 @@ def tile_staticgraphmodule_t_kernel(tc, x, Wp, b, out):
                 nc.scalar.copy(dst, src)
 
         def pe_t(c, g):
-            if g == 0:
+            if c not in xts:
                 xts[c] = dbl.tile([P, NWR, 2, PACK, P], BF16, name="xts")
             stg[(c, "t", g)] = ps3.tile([P, 2, PACK, P], BF16, name="stg")
             for s in range(2):
@@ -185,7 +189,7 @@ def tile_staticgraphmodule_t_kernel(tc, x, Wp, b, out):
             nc.scalar.copy(xts[c][:, g], stg[(c, "t", g)][:])
 
         def pe_m(c, g):
-            if g == 0:
+            if c not in mean:
                 mean[c] = four.tile([P, CL], BF16, name="mean", align_bytes=64)
             t = ps3.tile([P, PACK, 2, W_IMG], F32, name="stg")
             stg[(c, "m", g)] = t
@@ -199,53 +203,74 @@ def tile_staticgraphmodule_t_kernel(tc, x, Wp, b, out):
             dst = mean[c][:, g * 2 * RL:(g + 1) * 2 * RL].rearrange("p (n j) -> p n j", j=PACK)
             nc.scalar.copy(dst, stg[(c, "m", g)][:].rearrange("p j r w -> p (r w) j"))
 
+        def rv(c):
+            return ROWS - 2 if c == vs[3] else ROWS
+
         def rows2(c, first):
-            return xg[c][:, first * RL:(first + ROWS) * RL].rearrange("p (k t c) -> p k t c", t=2, c=RL)
+            return xg[c][:, first * RL:(first + rv(c)) * RL].rearrange("p (k t c) -> p k t c", t=2, c=RL)
 
         def v_hrow(c):
             hrow[c] = dbl.tile([P, ROWS // 2, RL], BF16, name="hrow")
-            nc.vector.tensor_scalar_mul(hrow[c][:], rows2(c, 1)[:, :, 1, :], 0.125)
+            nc.vector.tensor_scalar_mul(hrow[c][:, 0:rv(c) // 2], rows2(c, 1)[:, :, 1, :], 0.125)
 
         def v_pv(c):
             pv[c] = tmp.tile([P, ROWS // 2, RL], F32, name="pv")
-            nc.vector.scalar_tensor_tensor(out=pv[c][:], in0=rows2(c, 1)[:, :, 0, :], scalar=0.125, in1=hrow[c][:], op0=MULT, op1=ADD)
+            nc.vector.scalar_tensor_tensor(out=pv[c][:, 0:rv(c) // 2], in0=rows2(c, 1)[:, :, 0, :], scalar=0.125, in1=hrow[c][:, 0:rv(c) // 2], op0=MULT, op1=ADD)
 
         def v_cv(c, par):
             if par == 0:
                 cv[c] = tmp.tile([P, ROWS, PRL], F32, name="cv")
-            cvk = cv[c][:].rearrange("p (k t) c -> p k t c", t=2)
+            cvk = cv[c][:, 0:rv(c)].rearrange("p (k t) c -> p k t c", t=2)
             other = rows2(c, 0)[:, :, 0, :] if par == 0 else rows2(c, 2)[:, :, 1, :]
             nc.vector.scalar_tensor_tensor(out=cvk[:, :, par, PACK:PACK + RL], in0=other, scalar=0.125,
-                                           in1=pv[c][:], op0=MULT, op1=ADD)
+                                           in1=pv[c][:, 0:rv(c) // 2], op0=MULT, op1=ADD)
 
         def v_pad(c):
-            cvw = cv[c][:].rearrange("p r (w j) -> p r w j", j=PACK)
+            cvw = cv[c][:, 0:rv(c)].rearrange("p r (w j) -> p r w j", j=PACK)
             nc.vector.tensor_copy(out=cvw[:, :, 0:W_IMG + 2:W_IMG + 1, :], in_=cvw[:, :, 1:W_IMG + 1:W_IMG - 1, :])
 
         def pairs(c, first):
-            return cv[c][:, :, first * PACK:first * PACK + RL].rearrange("p r (i t j) -> p r i t j", t=2, j=PACK)
+            return cv[c][:, 0:rv(c), first * PACK:first * PACK + RL].rearrange("p r (i t j) -> p r i t j", t=2, j=PACK)
 
         def v_ph(c):
             ph[c] = tmp.tile([P, ROWS, W_IMG // 2, PACK], F32, name="ph")
-            nc.vector.tensor_tensor(out=ph[c][:], in0=pairs(c, 1)[:, :, :, 0, :], in1=pairs(c, 1)[:, :, :, 1, :], op=ADD)
+            nc.vector.tensor_tensor(out=ph[c][:, 0:rv(c)], in0=pairs(c, 1)[:, :, :, 0, :], in1=pairs(c, 1)[:, :, :, 1, :], op=ADD)
 
         def v_box(c, half):
             if half == 0:
                 box[c] = tmp.tile([P, CL], F32, name="box")
-            b4 = box[c][:].rearrange("p (r i t j) -> p r i t j", i=W_IMG // 2, t=2, j=PACK)
+            b4 = box[c][:, 0:rv(c) * RL].rearrange("p (r i t j) -> p r i t j", i=W_IMG // 2, t=2, j=PACK)
             if half == 0:
-                nc.vector.tensor_tensor(out=b4[:, :, :, 0, :], in0=pairs(c, 0)[:, :, :, 0, :], in1=ph[c][:], op=ADD)
+                nc.vector.tensor_tensor(out=b4[:, :, :, 0, :], in0=pairs(c, 0)[:, :, :, 0, :], in1=ph[c][:, 0:rv(c)], op=ADD)
             else:
-                nc.vector.tensor_tensor(out=b4[:, :, :, 1, :], in0=ph[c][:], in1=pairs(c, 2)[:, :, :, 1, :], op=ADD)
+                nc.vector.tensor_tensor(out=b4[:, :, :, 1, :], in0=ph[c][:, 0:rv(c)], in1=pairs(c, 2)[:, :, :, 1, :], op=ADD)
+
+        def last_rows():
+            c = vs[3]
+            strip[c] = dbl.tile([P, XT], BF16, name="strip", align_bytes=64)
+            dst = strip[c][:].rearrange("p (s j r w) -> p s j r w", s=2, j=PACK, w=HW)[:, :, :, ROWS - 2:NB, :]
+            src = xt[c][:].rearrange("p (j r s w) -> p s j r w", j=PACK, s=2, w=HW)[:, :, :, ROWS - 2:NB, :]
+            for s in range(2):
+                nc.scalar.copy(dst[:, s], src[:, s])
+
+        def last_rows_t():
+            c = vs[3]
+            pe_t(c, NWR - 1)
+            s_t(c, NWR - 1)
+
+        def last_rows_m():
+            c = vs[3]
+            pe_m(c, NWR - 1)
+            s_m(c, NWR - 1)
 
         def rowpairs(flat):
             return flat.rearrange("p (k t c) -> p k t c", t=2, c=RL)
 
         def v_fin(c, par):
-            if par == 0:
+            if par == 0 and c not in mean:
                 mean[c] = four.tile([P, CL], BF16, name="mean", align_bytes=64)
-            nc.vector.scalar_tensor_tensor(out=rowpairs(mean[c][:])[:, :, par, :], in0=rows2(c, 1)[:, :, par, :],
-                                           scalar=-0.125, in1=rowpairs(box[c][:])[:, :, par, :], op0=MULT, op1=ADD)
+            nc.vector.scalar_tensor_tensor(out=rowpairs(mean[c][:, 0:rv(c) * RL])[:, :, par, :], in0=rows2(c, 1)[:, :, par, :],
+                                           scalar=-0.125, in1=rowpairs(box[c][:, 0:rv(c) * RL])[:, :, par, :], op0=MULT, op1=ADD)
 
         def quant(src, codes, scales, c, nm):
             codes[c] = tri.tile([P, PIX], U32, name=nm + "c", align_bytes=64)
@@ -279,7 +304,9 @@ def tile_staticgraphmodule_t_kernel(tc, x, Wp, b, out):
             if (c, j) in units[:4] + units[-S_LAST:]:
                 nc.scalar.activation(out=xb[(c, j)][:], in_=rows(c, 1, NB - 1)[:, j, :], func=ACT.Identity, bias=b32[:, j:j + 1], scale=1.0)
                 return
-            nc.gpsimd.tensor_scalar(out=xb[(c, j)][:], in0=rows(c, 1, NB - 1)[:, j, :], scalar1=1.0, scalar2=gate["b"][:, j:j + 1], op0=MULT, op1=ADD)
+            if GCOL < PIX:
+                nc.scalar.activation(out=xb[(c, j)][:, GCOL:], in_=rows(c, 1, NB - 1)[:, j, GCOL:], func=ACT.Identity, bias=b32[:, j:j + 1], scale=1.0)
+            nc.gpsimd.tensor_scalar(out=xb[(c, j)][:, 0:GCOL], in0=rows(c, 1, NB - 1)[:, j, 0:GCOL], scalar1=1.0, scalar2=gate["b"][:, j:j + 1], op0=MULT, op1=ADD)
 
         def v_res(c, j, last):
             n, cc = divmod(c, CPI)
@@ -385,10 +412,12 @@ def tile_staticgraphmodule_t_kernel(tc, x, Wp, b, out):
             if 0 <= k < npe:
                 interleave("s", pes[k], part, 2)
 
+
         def warm_plain(n):
-            t = ps3.tile([P, P], F32, name="stg")
+            t = ps3.tile([P, PIX], F32, name="stg")
             for i in range(n):
-                nc.tensor.matmul(out=t[:], lhsT=ident2[:], rhs=ident2[:], start=True, stop=True)
+                nc.tensor.matmul_mx(out=t[:], lhsT=ocodes[:, 0:P].bitcast(FP8X4), lhsT_scale=oscales[:, 0:P],
+                                    rhs=ocodes[:].bitcast(FP8X4), rhs_scale=oscales[:], start=True, stop=True)
 
         def warm_mx(n):
             c = pes[0]
@@ -397,32 +426,33 @@ def tile_staticgraphmodule_t_kernel(tc, x, Wp, b, out):
                 nc.tensor.matmul_mx(out=t[:], lhsT=xc[c][:, 0:P].bitcast(FP8X4), lhsT_scale=xs[c][:, 0:P],
                                     rhs=xc[c][:].bitcast(FP8X4), rhs_scale=xs[c][:], start=True, stop=True)
 
-        warm_plain(3)
+        warm_plain(6)
         v_strip(pes[0])
         interleave("v", pes[0], 0, 1)
         q_x(pes[0])
         nc.vector.tensor_copy(out=b32[:], in_=b16[:])
         nc.vector.tensor_scalar_mul(nb32[:], b16[:], -1.0)
         group(0, 0)
-        warm_plain(1)
+        warm_plain(2)
         group(0, 1)
-        warm_plain(1)
+        warm_plain(2)
         group(0, 3)
-        warm_plain(1)
+        warm_plain(2)
         group(0, 5)
         interleave("v", vs[0], 0, 2)
         interleave("v", vs[0], 1, 2)
+        v_hrow(vs[0])
         w_group("v", 0)
         group(0, 2)
+        v_strip(pes[1])
         w_group("v", 1)
         group(0, 4)
-        v_hrow(vs[0])
         group(0, 6)
         w_group("s", 2)
         group(0, 7)
         w_group("s", 3)
-        v_strip(pes[1])
         v_pv(vs[0])
+        v_strip(pes[2])
         warm_mx(3)
         xb_to(2)
         group(1, 0)
@@ -431,7 +461,6 @@ def tile_staticgraphmodule_t_kernel(tc, x, Wp, b, out):
         warm_mx(1)
         nc.vector.quantize_mx(out=wcodes[:].bitcast(FP8X4), scales=wscales[:], in_=wg[:])
         qm(0)
-        v_strip(pes[2])
         group(1, 3)
         warm_mx(1)
         group(1, 2)
@@ -460,6 +489,12 @@ def tile_staticgraphmodule_t_kernel(tc, x, Wp, b, out):
                     s_xg(b + 4, (12, 15).index(s))
                 if s in (5, 11) and m < 3:
                     interleave("s", vs[m + 1], (5, 11).index(s), 2)
+                if m == 3 and s == 4:
+                    last_rows()
+                if m == 3 and s == 6:
+                    last_rows_t()
+                if m == 3 and s == 8:
+                    last_rows_m()
                 start = m == 0 and s < 8
                 if s % 2 == 1:
                     if start:
@@ -494,11 +529,13 @@ def tile_staticgraphmodule_t_kernel(tc, x, Wp, b, out):
                     qm(b + 3)
                     v_gate()
                     strip_of(b + 5)
-                xb_to(st["done"] + XB)
+                if not start or s % 2 == 1:
+                    xb_to(st["done"] + XB)
                 if not start or s % 2 == 1:
                     fin()
-                mx_to(st["done"] + (3 if m < 3 else 4))
-                if m == 3 and s >= 6:
+                mx_to(st["done"] + (2 if m < 3 else 4))
+                if m == 3 and s >= 10 or m == 4 and s < 3:
                     t = ps3.tile([P, PIX], F32, name="stg")
-                    nc.tensor.matmul_mx(out=t[:], lhsT=wcodes[:, 0:P].bitcast(FP8X4), lhsT_scale=wscales[:, 0:P],
-                                        rhs=wcodes[:, 0:PIX].bitcast(FP8X4), rhs_scale=wscales[:, 0:PIX], start=True, stop=True)
+                    for i in range(2):
+                        nc.tensor.matmul_mx(out=t[:], lhsT=wcodes[:, 0:P].bitcast(FP8X4), lhsT_scale=wscales[:, 0:P],
+                                            rhs=wcodes[:, 0:PIX].bitcast(FP8X4), rhs_scale=wscales[:, 0:PIX], start=True, stop=True)

@@ -5,14 +5,14 @@ from concourse.masks import make_identity
 
 F32 = mybir.dt.float32
 BF16 = mybir.dt.bfloat16
+I32 = mybir.dt.int32
 U32 = mybir.dt.uint32
 U8 = mybir.dt.uint8
 FP8X4 = mybir.dt.float8_e4m3fn_x4
 ADD = mybir.AluOpType.add
 MAX = mybir.AluOpType.max
 MULT = mybir.AluOpType.mult
-SUB = mybir.AluOpType.subtract
-ACT = mybir.ActivationFunctionType
+IDENT = mybir.ActivationFunctionType.Identity
 
 P = 128
 PACK = 4
@@ -27,24 +27,18 @@ CL = PIX * PACK
 PRL = (W_IMG + 2) * PACK
 CPI = H_IMG // ROWS
 NCH = 2 * CPI
-
 HALO = NB * W_IMG
 XT = PACK * HALO
 HW = W_IMG // 2
-WR = P // HW
-NWR = ROWS // 2
 OV = HW + 1
-WM = 2
-AHEAD = 8
-S_LAST = 16
-XB = 4
-GCOL = 512
+NWR = ROWS // 2
 
 V_CHUNKS = (3, 7, 11, 14)
 NACC = 4
 NSTG = 4
-S_STRIP = ()
-GS = 4
+XB = 4
+S_LAST = 12
+TAIL_ROWS = 2
 
 FLOPS = 2 * 512 * 1024 * 8192
 
@@ -56,30 +50,25 @@ def tile_staticgraphmodule_t_kernel(tc, x, Wp, b, out):
 
     with ExitStack() as ctx:
         const = ctx.enter_context(tc.tile_pool(name="const", bufs=1))
-        tmp = ctx.enter_context(tc.tile_pool(name="tmp", bufs=1))
         dbl = ctx.enter_context(tc.tile_pool(name="dbl", bufs=2))
         tri = ctx.enter_context(tc.tile_pool(name="tri", bufs=3))
-        four = ctx.enter_context(tc.tile_pool(name="four", bufs=5))
-        six = ctx.enter_context(tc.tile_pool(name="six", bufs=XB))
-        many = ctx.enter_context(tc.tile_pool(name="many", bufs=NCH))
-        ps3 = ctx.enter_context(tc.psum_pool(name="ps3", bufs=NSTG))
-        ps4 = ctx.enter_context(tc.psum_pool(name="ps4", bufs=NACC))
+        four = ctx.enter_context(tc.tile_pool(name="four", bufs=4))
+        ps_s = ctx.enter_context(tc.psum_pool(name="ps_s", bufs=NSTG))
+        ps_a = ctx.enter_context(tc.psum_pool(name="ps_a", bufs=NACC))
         ctx.enter_context(tc.manual_schedule())
 
-        pes = [c for c in range(NCH) if c not in V_CHUNKS]
         vs = list(V_CHUNKS)
+        pes = [c for c in range(NCH) if c not in vs]
         npe = len(pes)
 
         xt = {}
-        b16 = const.tile([P, PACK], BF16, name="b16")
-        nc.sync.dma_start(out=b16[:], in_=b.rearrange("(p j) -> p j", j=PACK))
 
         def rows(c, r0, r1):
             return xt[c][:].rearrange("p (j w) -> p j w", j=PACK)[:, :, r0 * W_IMG:r1 * W_IMG]
 
         def load_x(c):
             n, cc = divmod(c, CPI)
-            xt[c] = many.tile([P, XT], BF16, name="xt", align_bytes=64)
+            xt[c] = const.tile([P, XT], BF16, name="xt%d" % c, align_bytes=64)
             first = cc * ROWS - 1
             lo = 1 if cc == 0 else 0
             hi = NB - 1 if cc == CPI - 1 else NB
@@ -89,39 +78,39 @@ def tile_staticgraphmodule_t_kernel(tc, x, Wp, b, out):
             if cc == CPI - 1:
                 nc.sync.dma_start(out=rows(c, NB - 1, NB), in_=xv[n, :, :, IMG - W_IMG:IMG])
 
+        b16 = const.tile([P, PACK], BF16, name="b16")
+        nc.sync.dma_start(out=b16[:], in_=b.rearrange("(p j) -> p j", j=PACK))
         w_sb = tri.tile([P, PACK * 1024], BF16, name="tt", align_bytes=64)
-        load_order = [pes[0], vs[0], "w", pes[1], pes[2], pes[3], pes[4], vs[1], pes[5], pes[6], pes[7], vs[2], pes[8], pes[9], pes[10], vs[3], pes[11]]
-        for c in load_order:
-            if c == "w":
-                nc.sync.dma_start(out=w_sb[:], in_=Wp.rearrange("(m j) k -> m (j k)", j=PACK))
-            else:
-                load_x(c)
+        load_x(pes[0])
+        load_x(vs[0])
+        nc.sync.dma_start(out=w_sb[:], in_=Wp.rearrange("(m j) k -> m (j k)", j=PACK))
+        load_x(pes[1])
+        load_x(pes[2])
+        for m in range(1, 4):
+            load_x(vs[m])
+            for k in range(3 * m, 3 * m + 3):
+                load_x(pes[k])
 
         ident = const.tile([P, P], F32, name="ident")
         make_identity(nc, ident[:])
         identb = const.tile([P, P], BF16, name="identb")
         make_identity(nc, identb[:])
 
-        b32 = const.tile([P, PACK], F32, name="b32")
-        nb32 = const.tile([P, PACK], F32, name="nb32")
-        wg = tri.tile([P, 8 * P * PACK], BF16, name="tt", align_bytes=64)
-        wcodes = const.tile([P, 8 * P], U32, name="wcodes", align_bytes=64)
-        wscales = const.tile([P, 8 * P], U8, name="wscales", align_bytes=64)
-
-        ones = four.tile([P, CL], BF16, name="mean", align_bytes=64)
+        ones = four.tile([P, 2, CL], BF16, name="xm", align_bytes=64)
         ocodes = const.tile([P, PIX], U32, name="ocodes", align_bytes=64)
         oscales = const.tile([P, PIX], U8, name="oscales", align_bytes=64)
-        nc.vector.memset(ones[:], 1.0)
-        nc.vector.quantize_mx(out=ocodes[:].bitcast(FP8X4), scales=oscales[:], in_=ones[:])
-        e = const.tile([P, 2, WR, OV + 2], BF16, name="e")
-        h2 = const.tile([P, 2, WR, OV], BF16, name="h2")
-        h3 = const.tile([P, 2, WR, OV], BF16, name="h3")
+        nc.vector.memset(ones[:, 0, :].bitcast(I32), 0x3F803F80)
+        nc.vector.quantize_mx(out=ocodes[:].bitcast(FP8X4), scales=oscales[:], in_=ones[:, 0, :])
+
+        e = const.tile([P, 2, PACK, OV + 2], BF16, name="e")
+        h2 = const.tile([P, 2, PACK, OV], BF16, name="h2")
+        h3 = const.tile([P, 2, PACK, OV], BF16, name="h3")
         hs = const.tile([P, 2, 2, OV], BF16, name="hs")
         band = const.tile([P, 2, 2, OV], BF16, name="band")
         idq = identb[:].rearrange("p (r q) -> p r q", q=HW)
         nc.vector.memset(e[:], 0.0)
-        nc.vector.tensor_scalar_mul(e[:, 0, :, 1:1 + HW], idq, 0.125)
-        nc.vector.tensor_scalar_mul(e[:, 1, :, 2:2 + HW], idq, 0.125)
+        nc.vector.tensor_copy(out=e[:, 0, :, 1:1 + HW], in_=idq)
+        nc.vector.tensor_copy(out=e[:, 1, :, 2:2 + HW], in_=idq)
         nc.vector.tensor_copy(out=e[:, 0, :, 0:1], in_=e[:, 0, :, 1:2])
         nc.vector.tensor_copy(out=e[:, 1, :, OV + 1:OV + 2], in_=e[:, 1, :, OV:OV + 1])
         nc.vector.tensor_tensor(out=h2[:], in0=e[:, :, :, 0:OV], in1=e[:, :, :, 2:OV + 2], op=ADD)
@@ -129,200 +118,156 @@ def tile_staticgraphmodule_t_kernel(tc, x, Wp, b, out):
         nc.vector.tensor_tensor(out=hs[:], in0=h3[:, :, 0:2, :], in1=h3[:, :, 2:4, :], op=ADD)
         nc.vector.tensor_tensor(out=band[:], in0=hs[:], in1=h2[:, :, 1:3, :], op=ADD)
 
+        b32 = const.tile([P, PACK], F32, name="b32")
+        nb32 = const.tile([P, PACK], F32, name="nb32")
+        wg = tri.tile([P, 8 * P * PACK], BF16, name="tt", align_bytes=64)
+        wcodes = const.tile([P, 8 * P], U32, name="wcodes", align_bytes=64)
+        wscales = const.tile([P, 8 * P], U8, name="wscales", align_bytes=64)
+
         strip = {}
-        xg = {}
-        mean = {}
+        xm = {}
+        xgv = {}
         xts = {}
-        stg = {}
-        xps = {}
-        xtr = {}
-        hrow = {}
         pv = {}
         cv = {}
         ph = {}
         box = {}
-        xc = {}
-        xs = {}
-        mc = {}
-        ms = {}
+        codes = {}
+        scales = {}
         acc = {}
-        tt = {}
         xb = {}
+        tt = {}
+        gate = {}
 
-        def new_xg(c):
-            if c in vs:
-                xg[c] = dbl.tile([P, NB * RL], BF16, name="xgv", align_bytes=64)
-            else:
-                xg[c] = tri.tile([P, CL], BF16, name="xg", align_bytes=64)
+        def side(c, s):
+            if c not in xm:
+                xm[c] = four.tile([P, 2, CL], BF16, name="xm", align_bytes=64)
+            return xm[c][:, s, :]
+
+        def mean(c):
+            return side(c, 1)
 
         def interleave(eng, c, part, parts):
-            r0, r1 = (0, NB) if c in vs else (1, NB - 1)
-            if part == 0:
-                new_xg(c)
+            if c in vs and c not in xgv:
+                xgv[c] = dbl.tile([P, NB * RL], BF16, name="xgv", align_bytes=64)
+            tile, r0, r1 = (xgv[c][:], 0, NB) if c in vs else (side(c, 0), 1, NB - 1)
             h = (r1 - r0) // parts
-            dst = xg[c][:, part * h * RL:(part + 1) * h * RL].rearrange("p (c i t) -> p c t i", i=4, t=PACK)
+            dst = tile[:, part * h * RL:(part + 1) * h * RL].rearrange("p (c i t) -> p c t i", i=4, t=PACK)
             src = rows(c, r0 + part * h, r0 + (part + 1) * h).rearrange("p t (c i) -> p c t i", i=4)
             if eng == "v":
                 nc.vector.tensor_copy(out=dst, in_=src)
             else:
                 nc.scalar.copy(dst, src)
 
-        def v_strip(c, eng="v"):
+        def v_strip(c):
             strip[c] = dbl.tile([P, XT], BF16, name="strip", align_bytes=64)
-            dst = strip[c][:].rearrange("p (s g w) -> p s g w", s=2, w=HW)
-            src = xt[c][:].rearrange("p (g s w) -> p s g w", s=2, w=HW)
-            if eng == "v":
-                nc.vector.tensor_copy(out=dst, in_=src)
-            else:
-                nc.scalar.copy(dst, src)
+            nc.vector.tensor_copy(out=strip[c][:].rearrange("p (s g w) -> p s g w", s=2, w=HW),
+                                  in_=xt[c][:].rearrange("p (g s w) -> p s g w", s=2, w=HW))
 
-        def pe_t(c, g):
+        def s_strip_tail(c):
+            strip[c] = dbl.tile([P, XT], BF16, name="strip", align_bytes=64)
+            dst = strip[c][:].rearrange("p (s j r w) -> p s j r w", s=2, j=PACK, w=HW)
+            src = xt[c][:].rearrange("p (j r s w) -> p s j r w", j=PACK, s=2, w=HW)
+            for s in range(2):
+                nc.scalar.copy(dst[:, s, :, ROWS - TAIL_ROWS:NB, :], src[:, s, :, ROWS - TAIL_ROWS:NB, :])
+
+        def turn(c, g):
             if c not in xts:
                 xts[c] = dbl.tile([P, NWR, 2, PACK, P], BF16, name="xts")
-            stg[(c, "t", g)] = ps3.tile([P, 2, PACK, P], BF16, name="stg")
+            t = ps_s.tile([P, 2, PACK, P], BF16, name="stg")
             for s in range(2):
                 for j in range(PACK):
                     o = ((s * PACK + j) * NB + 2 * g) * HW
-                    nc.tensor.transpose(stg[(c, "t", g)][:, s, j, :], strip[c][:, o:o + P], identb[:])
+                    nc.tensor.transpose(t[:, s, j, :], strip[c][:, o:o + P], identb[:])
+            nc.scalar.copy(xts[c][:, g], t[:])
 
-        def s_t(c, g):
-            nc.scalar.copy(xts[c][:, g], stg[(c, "t", g)][:])
-
-        def pe_m(c, g):
-            if c not in mean:
-                mean[c] = four.tile([P, CL], BF16, name="mean", align_bytes=64)
-            t = ps3.tile([P, PACK, 2, W_IMG], F32, name="stg")
-            stg[(c, "m", g)] = t
+        def add_up(c, g):
+            t = ps_s.tile([P, PACK, 2, W_IMG], F32, name="stg")
             for j in range(PACK):
                 left, right = xts[c][:, g, 0, j, :], xts[c][:, g, 1, j, :]
                 nc.tensor.matmul(out=t[:, j, :, 0:OV], lhsT=left, rhs=band[:, 0], start=True, stop=False)
                 nc.tensor.matmul(out=t[:, j, :, HW - 1:OV], lhsT=right, rhs=band[:, 1, :, 0:2], start=False, stop=True)
                 nc.tensor.matmul(out=t[:, j, :, OV:W_IMG], lhsT=right, rhs=band[:, 1, :, 2:OV], start=True, stop=True)
+            nc.scalar.copy(mean(c)[:, g * 2 * RL:(g + 1) * 2 * RL].rearrange("p (n j) -> p n j", j=PACK),
+                           t[:].rearrange("p j r w -> p (r w) j"))
 
-        def s_m(c, g):
-            dst = mean[c][:, g * 2 * RL:(g + 1) * 2 * RL].rearrange("p (n j) -> p n j", j=PACK)
-            nc.scalar.copy(dst, stg[(c, "m", g)][:].rearrange("p j r w -> p (r w) j"))
+        def nrow(c):
+            return ROWS - TAIL_ROWS if c == vs[-1] else ROWS
 
-        def rv(c):
-            return ROWS - 2 if c == vs[3] else ROWS
-
-        def rows2(c, first):
-            return xg[c][:, first * RL:(first + rv(c)) * RL].rearrange("p (k t c) -> p k t c", t=2, c=RL)
-
-        def v_hrow(c):
-            hrow[c] = dbl.tile([P, ROWS // 2, RL], BF16, name="hrow")
-            nc.vector.tensor_scalar_mul(hrow[c][:, 0:rv(c) // 2], rows2(c, 1)[:, :, 1, :], 0.125)
+        def every2(c, first):
+            n = nrow(c)
+            return xgv[c][:, first * RL:(first + n) * RL].rearrange("p (k t c) -> p k t c", t=2, c=RL)
 
         def v_pv(c):
-            pv[c] = tmp.tile([P, ROWS // 2, RL], F32, name="pv")
-            nc.vector.scalar_tensor_tensor(out=pv[c][:, 0:rv(c) // 2], in0=rows2(c, 1)[:, :, 0, :], scalar=0.125, in1=hrow[c][:, 0:rv(c) // 2], op0=MULT, op1=ADD)
+            pv[c] = const.tile([P, ROWS // 2, RL], F32, name="pv")
+            nc.vector.tensor_tensor(out=pv[c][:, 0:nrow(c) // 2], in0=every2(c, 1)[:, :, 0, :], in1=every2(c, 1)[:, :, 1, :], op=ADD)
 
         def v_cv(c, par):
             if par == 0:
-                cv[c] = tmp.tile([P, ROWS, PRL], F32, name="cv")
-            cvk = cv[c][:, 0:rv(c)].rearrange("p (k t) c -> p k t c", t=2)
-            other = rows2(c, 0)[:, :, 0, :] if par == 0 else rows2(c, 2)[:, :, 1, :]
-            nc.vector.scalar_tensor_tensor(out=cvk[:, :, par, PACK:PACK + RL], in0=other, scalar=0.125,
-                                           in1=pv[c][:, 0:rv(c) // 2], op0=MULT, op1=ADD)
+                cv[c] = const.tile([P, ROWS, PRL], F32, name="cv")
+            cvk = cv[c][:, 0:nrow(c)].rearrange("p (k t) c -> p k t c", t=2)
+            other = every2(c, 0)[:, :, 0, :] if par == 0 else every2(c, 2)[:, :, 1, :]
+            nc.vector.tensor_tensor(out=cvk[:, :, par, PACK:PACK + RL], in0=other, in1=pv[c][:, 0:nrow(c) // 2], op=ADD)
 
         def v_pad(c):
-            cvw = cv[c][:, 0:rv(c)].rearrange("p r (w j) -> p r w j", j=PACK)
+            cvw = cv[c][:, 0:nrow(c)].rearrange("p r (w j) -> p r w j", j=PACK)
             nc.vector.tensor_copy(out=cvw[:, :, 0:W_IMG + 2:W_IMG + 1, :], in_=cvw[:, :, 1:W_IMG + 1:W_IMG - 1, :])
 
         def pairs(c, first):
-            return cv[c][:, 0:rv(c), first * PACK:first * PACK + RL].rearrange("p r (i t j) -> p r i t j", t=2, j=PACK)
+            return cv[c][:, 0:nrow(c), first * PACK:first * PACK + RL].rearrange("p r (i t j) -> p r i t j", t=2, j=PACK)
 
         def v_ph(c):
-            ph[c] = tmp.tile([P, ROWS, W_IMG // 2, PACK], F32, name="ph")
-            nc.vector.tensor_tensor(out=ph[c][:, 0:rv(c)], in0=pairs(c, 1)[:, :, :, 0, :], in1=pairs(c, 1)[:, :, :, 1, :], op=ADD)
+            ph[c] = const.tile([P, ROWS, W_IMG // 2, PACK], F32, name="ph")
+            nc.vector.tensor_tensor(out=ph[c][:, 0:nrow(c)], in0=pairs(c, 1)[:, :, :, 0, :], in1=pairs(c, 1)[:, :, :, 1, :], op=ADD)
 
         def v_box(c, half):
             if half == 0:
-                box[c] = tmp.tile([P, CL], F32, name="box")
-            b4 = box[c][:, 0:rv(c) * RL].rearrange("p (r i t j) -> p r i t j", i=W_IMG // 2, t=2, j=PACK)
-            if half == 0:
-                nc.vector.tensor_tensor(out=b4[:, :, :, 0, :], in0=pairs(c, 0)[:, :, :, 0, :], in1=ph[c][:, 0:rv(c)], op=ADD)
-            else:
-                nc.vector.tensor_tensor(out=b4[:, :, :, 1, :], in0=ph[c][:, 0:rv(c)], in1=pairs(c, 2)[:, :, :, 1, :], op=ADD)
+                box[c] = const.tile([P, CL], F32, name="box")
+            b4 = box[c][:, 0:nrow(c) * RL].rearrange("p (r i t j) -> p r i t j", i=W_IMG // 2, t=2, j=PACK)
+            outer = pairs(c, 0)[:, :, :, 0, :] if half == 0 else pairs(c, 2)[:, :, :, 1, :]
+            nc.vector.tensor_tensor(out=b4[:, :, :, half, :], in0=outer, in1=ph[c][:, 0:nrow(c)], op=ADD)
 
-        def last_rows():
-            c = vs[3]
-            strip[c] = dbl.tile([P, XT], BF16, name="strip", align_bytes=64)
-            dst = strip[c][:].rearrange("p (s j r w) -> p s j r w", s=2, j=PACK, w=HW)[:, :, :, ROWS - 2:NB, :]
-            src = xt[c][:].rearrange("p (j r s w) -> p s j r w", j=PACK, s=2, w=HW)[:, :, :, ROWS - 2:NB, :]
+        def v_fin(c, half):
+            n = nrow(c) * RL // 2
+            lo, hi = half * n, (half + 1) * n
+            nc.vector.scalar_tensor_tensor(out=mean(c)[:, lo:hi], in0=xgv[c][:, RL + lo:RL + hi], scalar=-1.0,
+                                           in1=box[c][:, lo:hi], op0=MULT, op1=ADD)
+
+        def quant(c, parts):
+            if c not in codes:
+                codes[c] = tri.tile([P, 2, PIX], U32, name="codes", align_bytes=64)
+                scales[c] = tri.tile([P, 2, PIX], U8, name="scales", align_bytes=64)
+            if parts == 2:
+                nc.vector.quantize_mx(out=codes[c][:].rearrange("p s n -> p (s n)").bitcast(FP8X4),
+                                      scales=scales[c][:].rearrange("p s n -> p (s n)"), in_=xm[c][:].rearrange("p s n -> p (s n)"))
+
+        def quant1(c, s, src):
+            quant(c, 1)
+            nc.vector.quantize_mx(out=codes[c][:, s, :].bitcast(FP8X4), scales=scales[c][:, s, :], in_=src)
+
+        def mx(c, j):
+            acc[(c, j)] = ps_a.tile([P, PIX], F32, name="acc")
             for s in range(2):
-                nc.scalar.copy(dst[:, s], src[:, s])
-
-        def last_rows_t():
-            c = vs[3]
-            pe_t(c, NWR - 1)
-            s_t(c, NWR - 1)
-
-        def last_rows_m():
-            c = vs[3]
-            pe_m(c, NWR - 1)
-            s_m(c, NWR - 1)
-
-        def rowpairs(flat):
-            return flat.rearrange("p (k t c) -> p k t c", t=2, c=RL)
-
-        def v_fin(c, par):
-            if par == 0 and c not in mean:
-                mean[c] = four.tile([P, CL], BF16, name="mean", align_bytes=64)
-            nc.vector.scalar_tensor_tensor(out=rowpairs(mean[c][:, 0:rv(c) * RL])[:, :, par, :], in0=rows2(c, 1)[:, :, par, :],
-                                           scalar=-0.125, in1=rowpairs(box[c][:, 0:rv(c) * RL])[:, :, par, :], op0=MULT, op1=ADD)
-
-        def quant(src, codes, scales, c, nm):
-            codes[c] = tri.tile([P, PIX], U32, name=nm + "c", align_bytes=64)
-            scales[c] = tri.tile([P, PIX], U8, name=nm + "s", align_bytes=64)
-            nc.vector.quantize_mx(out=codes[c][:].bitcast(FP8X4), scales=scales[c][:], in_=src)
-
-        def q_x(c):
-            quant(xg[c][:, RL:RL + CL] if c in vs else xg[c][:], xc, xs, c, "x")
-
-        def q_m(c):
-            quant(mean[c][:], mc, ms, c, "m")
-            pass
-
-        def pe_mx(c, j):
-            acc[(c, j)] = ps4.tile([P, PIX], F32, name="acc")
-            for s, codes, scales in ((0, xc, xs), (1, mc, ms)):
                 cols = slice((s * PACK + j) * P, (s * PACK + j + 1) * P)
                 nc.tensor.matmul_mx(out=acc[(c, j)][:],
                                     lhsT=wcodes[:, cols].bitcast(FP8X4), lhsT_scale=wscales[:, cols],
-                                    rhs=codes[c][:].bitcast(FP8X4), rhs_scale=scales[c][:],
+                                    rhs=codes[c][:, s, :].bitcast(FP8X4), rhs_scale=scales[c][:, s, :],
                                     start=(s == 0), stop=(s == 1))
 
-        gate = {}
+        def warm(n):
+            t = ps_s.tile([P, PIX], F32, name="stg")
+            for i in range(n):
+                nc.tensor.matmul_mx(out=t[:], lhsT=ocodes[:, 0:P].bitcast(FP8X4), lhsT_scale=oscales[:, 0:P],
+                                    rhs=ocodes[:].bitcast(FP8X4), rhs_scale=oscales[:], start=True, stop=True)
 
         def v_gate():
             gate["b"] = dbl.tile([P, PACK], F32, name="bk")
             nc.vector.tensor_copy(out=gate["b"][:], in_=b16[:])
 
-        def x_b(c, j):
-            xb[(c, j)] = six.tile([P, PIX], F32, name="xb")
-            if (c, j) in units[:4] + units[-S_LAST:]:
-                nc.scalar.activation(out=xb[(c, j)][:], in_=rows(c, 1, NB - 1)[:, j, :], func=ACT.Identity, bias=b32[:, j:j + 1], scale=1.0)
-                return
-            if GCOL < PIX:
-                nc.scalar.activation(out=xb[(c, j)][:, GCOL:], in_=rows(c, 1, NB - 1)[:, j, GCOL:], func=ACT.Identity, bias=b32[:, j:j + 1], scale=1.0)
-            nc.gpsimd.tensor_scalar(out=xb[(c, j)][:, 0:GCOL], in0=rows(c, 1, NB - 1)[:, j, 0:GCOL], scalar1=1.0, scalar2=gate["b"][:, j:j + 1], op0=MULT, op1=ADD)
-
-        def v_res(c, j, last):
-            n, cc = divmod(c, CPI)
-            if j == 0:
-                tt[c] = tri.tile([P, PACK, PIX], F32, name="tt", align_bytes=64)
-            nc.vector.scalar_tensor_tensor(out=tt[c][:, j, :], in0=acc[(c, j)][:], scalar=nb32[:, j:j + 1],
-                                           in1=xb[(c, j)][:], op0=MAX, op1=ADD)
-            if last:
-                nc.sync.dma_start(out=ov[n, :, j, cc * PIX:(cc + 1) * PIX], in_=tt[c][:, j, :])
-            elif j == PACK - 1:
-                nc.sync.dma_start(out=ov[n, :, :, cc * PIX:(cc + 1) * PIX], in_=tt[c][:])
-
-        def w_group(eng, h):
+        def w_turn(eng, h):
             wf = w_sb[:].bitcast(F32).rearrange("p (j s q u) -> p j s q u", j=PACK, s=2, u=2)
             wgf = wg[:].bitcast(F32).rearrange("p (g m u) -> p g m u", m=P, u=2)
-            pw = ps4.tile([P, 2, 2, P], F32, name="acc")
+            pw = ps_a.tile([P, 2, 2, P], F32, name="acc")
             for gi in range(2):
                 s, j = divmod(h * 2 + gi, PACK)
                 for u in range(2):
@@ -335,134 +280,115 @@ def tile_staticgraphmodule_t_kernel(tc, x, Wp, b, out):
 
         order = []
         for m in range(4):
-            order += [pes[3 * m]]
-            if m > 0:
-                order += [vs[m - 1]]
-            order += [pes[3 * m + 1], pes[3 * m + 2]]
+            order += [pes[3 * m]] + vs[max(m - 1, 0):m] + [pes[3 * m + 1], pes[3 * m + 2]]
         order += [vs[3]]
         units = [(c, j) for c in order for j in range(PACK)]
-        st = {"done": 0, "mx": 0, "x_b": 0, "ready": 0}
+        s_units = units[:4] + units[len(units) - S_LAST:]
+        st = {"done": 0, "mx": 0, "xb": 0, "ready": 0}
 
         def xb_to(n):
-            while st["x_b"] < min(n, len(units)):
-                x_b(units[st["x_b"]][0], units[st["x_b"]][1])
-                st["x_b"] += 1
+            while st["xb"] < min(n, len(units)):
+                c, j = units[st["xb"]]
+                xb[(c, j)] = four.tile([P, PIX], F32, name="xb")
+                src = rows(c, 1, NB - 1)[:, j, :]
+                if (c, j) in s_units:
+                    nc.scalar.activation(out=xb[(c, j)][:], in_=src, func=IDENT, bias=b32[:, j:j + 1], scale=1.0)
+                else:
+                    nc.gpsimd.tensor_scalar(out=xb[(c, j)][:], in0=src, scalar1=1.0, scalar2=gate["b"][:, j:j + 1], op0=MULT, op1=ADD)
+                st["xb"] += 1
 
         def mx_to(n):
             while st["mx"] < min(n, st["ready"], st["done"] + NACC):
-                pe_mx(units[st["mx"]][0], units[st["mx"]][1])
+                mx(units[st["mx"]][0], units[st["mx"]][1])
                 st["mx"] += 1
 
-        def fin():
-            if st["done"] < st["mx"]:
-                c, j = units[st["done"]]
-                v_res(c, j, c == order[-1])
-                st["done"] += 1
+        def finish():
+            if st["done"] == st["mx"]:
+                return
+            c, j = units[st["done"]]
+            n, cc = divmod(c, CPI)
+            if j == 0:
+                tt[c] = tri.tile([P, PACK, PIX], F32, name="tt", align_bytes=64)
+            nc.vector.scalar_tensor_tensor(out=tt[c][:, j, :], in0=acc[(c, j)][:], scalar=nb32[:, j:j + 1],
+                                           in1=xb[(c, j)][:], op0=MAX, op1=ADD)
+            dst = ov[n, :, :, cc * PIX:(cc + 1) * PIX]
+            if c == order[-1]:
+                nc.sync.dma_start(out=dst[:, j, :], in_=tt[c][:, j, :])
+            elif j == PACK - 1:
+                nc.sync.dma_start(out=dst, in_=tt[c][:])
+            st["done"] += 1
 
-        def qx(k):
+        def q(k):
             if 0 <= k < npe:
-                q_x(pes[k])
-
-        def qm(k):
-            if 0 <= k < npe:
-                q_m(pes[k])
+                quant(pes[k], 2)
                 st["ready"] += PACK
-
-        def strip_of(k):
-            if 0 <= k < npe:
-                v_strip(pes[k], "s" if k in S_STRIP else "v")
 
         def qv(m):
             if 0 <= m < 4:
-                q_x(vs[m])
+                c = vs[m]
+                quant1(c, 0, xgv[c][:, RL:RL + CL])
                 v_gate()
-                q_m(vs[m])
+                quant1(c, 1, mean(c))
                 st["ready"] += PACK
 
-        def vop(m, i):
-            if m >= 4:
-                return
-            c = vs[m]
-            if i == 0:
-                v_pv(c)
-            elif i < 3:
-                v_cv(c, i - 1)
-            elif i == 3:
-                v_pad(c)
-                v_gate()
-                v_ph(c)
-            elif i < 6:
-                v_box(c, i - 4)
-            else:
-                v_fin(c, i - 6)
+        VOPS = (lambda c: v_pv(c), lambda c: v_cv(c, 0), lambda c: v_cv(c, 1), lambda c: v_ph(c),
+                lambda c: v_box(c, 0), lambda c: v_box(c, 1), lambda c: v_fin(c, 0), lambda c: v_fin(c, 1))
 
-        SEQ = (("t", 0), ("t", 1), ("m", 0), ("t", 2), ("m", 1), ("t", 3), ("m", 2), ("m", 3))
+        def vop(m, i):
+            if 0 <= m < 4 and i < len(VOPS):
+                VOPS[i](vs[m])
+
+        SEQ = ((turn, 0), (turn, 1), (add_up, 0), (turn, 2), (add_up, 1), (turn, 3), (add_up, 2), (add_up, 3))
 
         def group(k, i):
             if 0 <= k < npe:
-                kind, g = SEQ[i]
-                if kind == "t":
-                    pe_t(pes[k], g)
-                    s_t(pes[k], g)
-                else:
-                    pe_m(pes[k], g)
-                    s_m(pes[k], g)
+                SEQ[i][0](pes[k], SEQ[i][1])
 
-        def s_xg(k, part):
+        def s_x(k, part):
             if 0 <= k < npe:
                 interleave("s", pes[k], part, 2)
 
+        def strip_of(k):
+            if 0 <= k < npe:
+                v_strip(pes[k])
 
-        def warm_plain(n):
-            t = ps3.tile([P, PIX], F32, name="stg")
-            for i in range(n):
-                nc.tensor.matmul_mx(out=t[:], lhsT=ocodes[:, 0:P].bitcast(FP8X4), lhsT_scale=oscales[:, 0:P],
-                                    rhs=ocodes[:].bitcast(FP8X4), rhs_scale=oscales[:], start=True, stop=True)
-
-        def warm_mx(n):
-            c = pes[0]
-            t = ps3.tile([P, PIX], F32, name="stg")
-            for i in range(n):
-                nc.tensor.matmul_mx(out=t[:], lhsT=xc[c][:, 0:P].bitcast(FP8X4), lhsT_scale=xs[c][:, 0:P],
-                                    rhs=xc[c][:].bitcast(FP8X4), rhs_scale=xs[c][:], start=True, stop=True)
-
-        warm_plain(6)
+        warm(6)
         v_strip(pes[0])
         interleave("v", pes[0], 0, 1)
-        q_x(pes[0])
         nc.vector.tensor_copy(out=b32[:], in_=b16[:])
         nc.vector.tensor_scalar_mul(nb32[:], b16[:], -1.0)
         group(0, 0)
-        warm_plain(2)
+        warm(2)
         group(0, 1)
-        warm_plain(2)
+        warm(2)
         group(0, 3)
-        warm_plain(2)
+        warm(2)
         group(0, 5)
         interleave("v", vs[0], 0, 2)
         interleave("v", vs[0], 1, 2)
-        v_hrow(vs[0])
-        w_group("v", 0)
+        w2 = w_sb[:].rearrange("p (j s k) -> p j s k", j=PACK, s=2)[:, :, 1, :]
+        nc.vector.tensor_scalar_mul(w2, w2, 0.125)
+        w_turn("v", 0)
         group(0, 2)
         v_strip(pes[1])
-        w_group("v", 1)
+        w_turn("v", 1)
         group(0, 4)
         group(0, 6)
-        w_group("s", 2)
+        w_turn("s", 2)
         group(0, 7)
-        w_group("s", 3)
+        w_turn("s", 3)
         v_pv(vs[0])
         v_strip(pes[2])
-        warm_mx(3)
+        warm(3)
         xb_to(2)
         group(1, 0)
-        warm_mx(1)
+        warm(1)
         group(1, 1)
-        warm_mx(1)
+        warm(1)
         nc.vector.quantize_mx(out=wcodes[:].bitcast(FP8X4), scales=wscales[:], in_=wg[:])
-        qm(0)
+        q(0)
         group(1, 3)
-        warm_mx(1)
+        warm(1)
         group(1, 2)
         group(1, 5)
         xb_to(XB)
@@ -474,68 +400,56 @@ def tile_staticgraphmodule_t_kernel(tc, x, Wp, b, out):
         interleave("v", pes[1], 0, 1)
         v_gate()
 
-        V_EARLY = 2
+        early = 2
         for m in range(5):
-            b = 3 * m
+            a = 3 * m
             for s in range(16):
+                start = m == 0 and s < 8
                 for i in range(24):
                     if 2 * i // 3 == s:
-                        group(b + 1 + (i + AHEAD) // 8, (i + AHEAD) % 8)
+                        group(a + 2 + i // 8, i % 8)
                 if s in (1, 3) and m > 0:
-                    s_xg(b + 2, (1, 3).index(s))
+                    s_x(a + 2, s // 2)
                 if s in (7, 9):
-                    s_xg(b + 3, (7, 9).index(s))
+                    s_x(a + 3, (s - 7) // 2)
                 if s in (12, 15):
-                    s_xg(b + 4, (12, 15).index(s))
+                    s_x(a + 4, s // 15)
                 if s in (5, 11) and m < 3:
-                    interleave("s", vs[m + 1], (5, 11).index(s), 2)
+                    interleave("s", vs[m + 1], s // 11, 2)
                 if m == 3 and s == 4:
-                    last_rows()
+                    s_strip_tail(vs[-1])
                 if m == 3 and s == 6:
-                    last_rows_t()
+                    turn(vs[-1], NWR - 1)
                 if m == 3 and s == 8:
-                    last_rows_m()
-                start = m == 0 and s < 8
+                    add_up(vs[-1], NWR - 1)
                 if s % 2 == 1:
                     if start:
                         v_gate()
-                    if m > 0 or s // 2 + V_EARLY < 8:
-                        vop(m, s // 2 + (V_EARLY if m == 0 else 0))
+                    if m == 0 and s == 3:
+                        v_pad(vs[0])
+                    vop(m, s // 2 + (early if m == 0 else 0))
                 elif s == 0:
-                    if 0 < m < 4:
-                        v_hrow(vs[m])
                     qv(m - 1)
                 elif s == 2:
-                    strip_of(b + 3)
+                    strip_of(a + 3)
                 elif s == 4:
-                    qx(b + 1)
-                    v_gate()
-                    qm(b + 1)
+                    q(a + 1)
                 elif s == 6:
-                    if m > 0:
-                        qx(b + 2)
-                    else:
-                        interleave("v", pes[2], 0, 1)
-                elif s == 8:
-                    strip_of(b + 4)
-                elif s == 10:
                     if m == 0:
-                        qx(b + 2)
-                        v_gate()
-                    qm(b + 2)
+                        interleave("v", pes[2], 0, 1)
+                    elif m < 4:
+                        v_pad(vs[m])
+                elif s == 8:
+                    strip_of(a + 4)
+                elif s == 10:
+                    q(a + 2)
                 elif s == 12:
-                    qx(b + 3)
+                    strip_of(a + 5)
                 elif s == 14:
-                    qm(b + 3)
-                    v_gate()
-                    strip_of(b + 5)
+                    q(a + 3)
                 if not start or s % 2 == 1:
                     xb_to(st["done"] + XB)
-                if not start or s % 2 == 1:
-                    fin()
+                    finish()
                 mx_to(st["done"] + (2 if m < 3 else 4))
                 if m == 3 and s >= 10 or m == 4 and s < 3:
-                    t = ps3.tile([P, PIX], F32, name="stg")
-                    for i in range(2):
-                        nc.tensor.matmul_mx(out=t[:], lhsT=wcodes[:, 0:P].bitcast(FP8X4), lhsT_scale=wscales[:, 0:P],
-                                            rhs=wcodes[:, 0:PIX].bitcast(FP8X4), rhs_scale=wscales[:, 0:PIX], start=True, stop=True)
+                    warm(2)

@@ -283,7 +283,7 @@ def tile_staticgraphmodule_t_kernel(tc, x, Wp, b, out):
             order += [pes[3 * m]] + vs[max(m - 1, 0):m] + [pes[3 * m + 1], pes[3 * m + 2]]
         order += [vs[3]]
         units = [(c, j) for c in order for j in range(PACK)]
-        s_units = units[:4] + units[len(units) - S_LAST:]
+        s_units = units[len(units) - S_LAST:]
         st = {"done": 0, "mx": 0, "xb": 0, "ready": 0}
 
         def xb_to(n):
@@ -338,7 +338,7 @@ def tile_staticgraphmodule_t_kernel(tc, x, Wp, b, out):
             if 0 <= m < 4 and i < len(VOPS):
                 VOPS[i](vs[m])
 
-        SEQ = ((turn, 0), (turn, 1), (add_up, 0), (turn, 2), (add_up, 1), (turn, 3), (add_up, 2), (add_up, 3))
+        SEQ = ((turn, 0), (turn, 1), (turn, 2), (add_up, 0), (turn, 3), (add_up, 1), (add_up, 2), (add_up, 3))
 
         def group(k, i):
             if 0 <= k < npe:
@@ -352,50 +352,50 @@ def tile_staticgraphmodule_t_kernel(tc, x, Wp, b, out):
             if 0 <= k < npe:
                 v_strip(pes[k])
 
-        warm(6)
+        warm(7)
         v_strip(pes[0])
         interleave("v", pes[0], 0, 1)
         nc.vector.tensor_copy(out=b32[:], in_=b16[:])
         nc.vector.tensor_scalar_mul(nb32[:], b16[:], -1.0)
-        group(0, 0)
-        warm(2)
-        group(0, 1)
-        warm(2)
-        group(0, 3)
-        warm(2)
-        group(0, 5)
+        turn(pes[0], 0)
+        warm(1)
+        turn(pes[0], 1)
+        warm(1)
+        turn(pes[0], 2)
+        warm(1)
+        turn(pes[0], 3)
         interleave("v", vs[0], 0, 2)
         interleave("v", vs[0], 1, 2)
         w2 = w_sb[:].rearrange("p (j s k) -> p j s k", j=PACK, s=2)[:, :, 1, :]
         nc.vector.tensor_scalar_mul(w2, w2, 0.125)
+        v_gate()
+        xb_to(XB)
         w_turn("v", 0)
-        group(0, 2)
+        add_up(pes[0], 0)
         v_strip(pes[1])
         w_turn("v", 1)
-        group(0, 4)
-        group(0, 6)
+        add_up(pes[0], 1)
+        add_up(pes[0], 2)
         w_turn("s", 2)
-        group(0, 7)
+        add_up(pes[0], 3)
         w_turn("s", 3)
         v_pv(vs[0])
         v_strip(pes[2])
         warm(3)
-        xb_to(2)
-        group(1, 0)
+        turn(pes[1], 0)
         warm(1)
-        group(1, 1)
+        turn(pes[1], 1)
         warm(1)
         nc.vector.quantize_mx(out=wcodes[:].bitcast(FP8X4), scales=wscales[:], in_=wg[:])
         q(0)
-        group(1, 3)
+        turn(pes[1], 2)
         warm(1)
-        group(1, 2)
-        group(1, 5)
-        xb_to(XB)
+        add_up(pes[1], 0)
+        turn(pes[1], 3)
         mx_to(2)
-        group(1, 4)
-        group(1, 6)
-        group(1, 7)
+        add_up(pes[1], 1)
+        add_up(pes[1], 2)
+        add_up(pes[1], 3)
         v_cv(vs[0], 0)
         interleave("v", pes[1], 0, 1)
         v_gate()

@@ -159,10 +159,14 @@ def tile_staticgraphmodule_t_kernel(tc, x, Wp, b, out):
             else:
                 nc.scalar.copy(dst, src)
 
-        def v_strip(c):
+        def v_strip(c, eng="v"):
             strip[c] = dbl.tile([P, XT], BF16, name="strip", align_bytes=64)
-            nc.vector.tensor_copy(out=strip[c][:].rearrange("p (s g w) -> p s g w", s=2, w=HW),
-                                  in_=xt[c][:].rearrange("p (g s w) -> p s g w", s=2, w=HW))
+            dst = strip[c][:].rearrange("p (s g w) -> p s g w", s=2, w=HW)
+            src = xt[c][:].rearrange("p (g s w) -> p s g w", s=2, w=HW)
+            if eng == "v":
+                nc.vector.tensor_copy(out=dst, in_=src)
+            else:
+                nc.scalar.copy(dst, src)
 
         def s_strip_tail(c):
             strip[c] = dbl.tile([P, XT], BF16, name="strip", align_bytes=64)
@@ -348,9 +352,9 @@ def tile_staticgraphmodule_t_kernel(tc, x, Wp, b, out):
             if 0 <= k < npe:
                 interleave("s", pes[k], part, 2)
 
-        def strip_of(k):
+        def strip_of(k, eng="v"):
             if 0 <= k < npe:
-                v_strip(pes[k])
+                v_strip(pes[k], eng)
 
         warm(7)
         v_strip(pes[0])
@@ -422,6 +426,8 @@ def tile_staticgraphmodule_t_kernel(tc, x, Wp, b, out):
                     turn(vs[-1], NWR - 1)
                 if m == 3 and s == 8:
                     add_up(vs[-1], NWR - 1)
+                if s == 0 and m >= 2:
+                    strip_of(a + 3, "s")
                 if s % 2 == 1:
                     if start:
                         v_gate()
@@ -431,7 +437,8 @@ def tile_staticgraphmodule_t_kernel(tc, x, Wp, b, out):
                 elif s == 0:
                     qv(m - 1)
                 elif s == 2:
-                    strip_of(a + 3)
+                    if m < 2:
+                        strip_of(a + 3)
                 elif s == 4:
                     q(a + 1)
                 elif s == 6:

from contextlib import ExitStack

import concourse.mybir as mybir
from concourse.masks import make_identity

F32 = mybir.dt.float32
BF16 = mybir.dt.bfloat16
I32 = mybir.dt.int32
U32 = mybir.dt.uint32
U8 = mybir.dt.uint8
FP8X4 = mybir.dt.float8_e4m3fn_x4
ADD = mybir.AluOpType.add
MAX = mybir.AluOpType.max
MULT = mybir.AluOpType.mult
IDENT = mybir.ActivationFunctionType.Identity

P = 128
PACK = 4
ROWS = 8
NB = ROWS + 2
W_IMG = 64
H_IMG = 64
PIX = ROWS * W_IMG
IMG = H_IMG * W_IMG
RL = W_IMG * PACK
CL = PIX * PACK
PRL = (W_IMG + 2) * PACK
CPI = H_IMG // ROWS
NCH = 2 * CPI
HALO = NB * W_IMG
XT = PACK * HALO
HW = W_IMG // 2
OV = HW + 1
NWR = ROWS // 2

V_CHUNKS = (3, 7, 11, 14)
NACC = 4
NSTG = 4
XB = 4
S_LAST = 12
TAIL_ROWS = 2

FLOPS = 2 * 512 * 1024 * 8192


def tile_staticgraphmodule_t_kernel(tc, x, Wp, b, out):
    nc = tc.nc
    xv = x.rearrange("n (p j) h w -> n p j (h w)", j=PACK)
    ov = out.rearrange("n (p j) h w -> n p j (h w)", j=PACK)

    with ExitStack() as ctx:
        const = ctx.enter_context(tc.tile_pool(name="const", bufs=1))
        dbl = ctx.enter_context(tc.tile_pool(name="dbl", bufs=2))
        tri = ctx.enter_context(tc.tile_pool(name="tri", bufs=3))
        four = ctx.enter_context(tc.tile_pool(name="four", bufs=4))
        ps_s = ctx.enter_context(tc.psum_pool(name="ps_s", bufs=NSTG))
        ps_a = ctx.enter_context(tc.psum_pool(name="ps_a", bufs=NACC))
        ctx.enter_context(tc.manual_schedule())

        vs = list(V_CHUNKS)
        pes = [c for c in range(NCH) if c not in vs]
        npe = len(pes)

        xt = {}

        def rows(c, r0, r1):
            return xt[c][:].rearrange("p (j w) -> p j w", j=PACK)[:, :, r0 * W_IMG:r1 * W_IMG]

        def load_x(c):
            n, cc = divmod(c, CPI)
            xt[c] = const.tile([P, XT], BF16, name="xt%d" % c, align_bytes=64)
            first = cc * ROWS - 1
            lo = 1 if cc == 0 else 0
            hi = NB - 1 if cc == CPI - 1 else NB
            if cc == 0:
                nc.sync.dma_start(out=rows(c, 0, 1), in_=xv[n, :, :, 0:W_IMG])
            nc.sync.dma_start(out=rows(c, lo, hi), in_=xv[n, :, :, (first + lo) * W_IMG:(first + hi) * W_IMG])
            if cc == CPI - 1:
                nc.sync.dma_start(out=rows(c, NB - 1, NB), in_=xv[n, :, :, IMG - W_IMG:IMG])

        b16 = const.tile([P, PACK], BF16, name="b16")
        nc.sync.dma_start(out=b16[:], in_=b.rearrange("(p j) -> p j", j=PACK))
        w_sb = tri.tile([P, PACK * 1024], BF16, name="tt", align_bytes=64)
        load_x(pes[0])
        load_x(vs[0])
        nc.sync.dma_start(out=w_sb[:], in_=Wp.rearrange("(m j) k -> m (j k)", j=PACK))
        load_x(pes[1])
        load_x(pes[2])
        for m in range(1, 4):
            load_x(vs[m])
            for k in range(3 * m, 3 * m + 3):
                load_x(pes[k])

        ident = const.tile([P, P], F32, name="ident")
        make_identity(nc, ident[:])
        identb = const.tile([P, P], BF16, name="identb")
        make_identity(nc, identb[:])

        ones = four.tile([P, 2, CL], BF16, name="xm", align_bytes=64)
        ocodes = const.tile([P, PIX], U32, name="ocodes", align_bytes=64)
        oscales = const.tile([P, PIX], U8, name="oscales", align_bytes=64)
        nc.vector.memset(ones[:, 0, :].bitcast(I32), 0x3F803F80)
        nc.vector.quantize_mx(out=ocodes[:].bitcast(FP8X4), scales=oscales[:], in_=ones[:, 0, :])

        e = const.tile([P, 2, PACK, OV + 2], BF16, name="e")
        h2 = const.tile([P, 2, PACK, OV], BF16, name="h2")
        h3 = const.tile([P, 2, PACK, OV], BF16, name="h3")
        hs = const.tile([P, 2, 2, OV], BF16, name="hs")
        band = const.tile([P, 2, 2, OV], BF16, name="band")
        idq = identb[:].rearrange("p (r q) -> p r q", q=HW)
        nc.vector.memset(e[:], 0.0)
        nc.vector.tensor_copy(out=e[:, 0, :, 1:1 + HW], in_=idq)
        nc.vector.tensor_copy(out=e[:, 1, :, 2:2 + HW], in_=idq)
        nc.vector.tensor_copy(out=e[:, 0, :, 0:1], in_=e[:, 0, :, 1:2])
        nc.vector.tensor_copy(out=e[:, 1, :, OV + 1:OV + 2], in_=e[:, 1, :, OV:OV + 1])
        nc.vector.tensor_tensor(out=h2[:], in0=e[:, :, :, 0:OV], in1=e[:, :, :, 2:OV + 2], op=ADD)
        nc.vector.tensor_tensor(out=h3[:], in0=h2[:], in1=e[:, :, :, 1:OV + 1], op=ADD)
        nc.vector.tensor_tensor(out=hs[:], in0=h3[:, :, 0:2, :], in1=h3[:, :, 2:4, :], op=ADD)
        nc.vector.tensor_tensor(out=band[:], in0=hs[:], in1=h2[:, :, 1:3, :], op=ADD)

        b32 = const.tile([P, PACK], F32, name="b32")
        nb32 = const.tile([P, PACK], F32, name="nb32")
        wg = tri.tile([P, 8 * P * PACK], BF16, name="tt", align_bytes=64)
        wcodes = const.tile([P, 8 * P], U32, name="wcodes", align_bytes=64)
        wscales = const.tile([P, 8 * P], U8, name="wscales", align_bytes=64)

        strip = {}
        xm = {}
        xgv = {}
        xts = {}
        pv = {}
        cv = {}
        ph = {}
        box = {}
        codes = {}
        scales = {}
        acc = {}
        xb = {}
        tt = {}
        gate = {}

        def side(c, s):
            if c not in xm:
                xm[c] = four.tile([P, 2, CL], BF16, name="xm", align_bytes=64)
            return xm[c][:, s, :]

        def mean(c):
            return side(c, 1)

        def interleave(eng, c, part, parts):
            if c in vs and c not in xgv:
                xgv[c] = dbl.tile([P, NB * RL], BF16, name="xgv", align_bytes=64)
            tile, r0, r1 = (xgv[c][:], 0, NB) if c in vs else (side(c, 0), 1, NB - 1)
            h = (r1 - r0) // parts
            dst = tile[:, part * h * RL:(part + 1) * h * RL].rearrange("p (c i t) -> p c t i", i=4, t=PACK)
            src = rows(c, r0 + part * h, r0 + (part + 1) * h).rearrange("p t (c i) -> p c t i", i=4)
            if eng == "v":
                nc.vector.tensor_copy(out=dst, in_=src)
            else:
                nc.scalar.copy(dst, src)

        def v_strip(c, eng="v"):
            strip[c] = dbl.tile([P, XT], BF16, name="strip", align_bytes=64)
            dst = strip[c][:].rearrange("p (s g w) -> p s g w", s=2, w=HW)
            src = xt[c][:].rearrange("p (g s w) -> p s g w", s=2, w=HW)
            if eng == "v":
                nc.vector.tensor_copy(out=dst, in_=src)
            else:
                nc.scalar.copy(dst, src)

        def s_strip_tail(c):
            strip[c] = dbl.tile([P, XT], BF16, name="strip", align_bytes=64)
            dst = strip[c][:].rearrange("p (s j r w) -> p s j r w", s=2, j=PACK, w=HW)
            src = xt[c][:].rearrange("p (j r s w) -> p s j r w", j=PACK, s=2, w=HW)
            for s in range(2):
                nc.scalar.copy(dst[:, s, :, ROWS - TAIL_ROWS:NB, :], src[:, s, :, ROWS - TAIL_ROWS:NB, :])

        def turn(c, g):
            if c not in xts:
                xts[c] = dbl.tile([P, NWR, 2, PACK, P], BF16, name="xts")
            t = ps_s.tile([P, 2, PACK, P], BF16, name="stg")
            for s in range(2):
                for j in range(PACK):
                    o = ((s * PACK + j) * NB + 2 * g) * HW
                    nc.tensor.transpose(t[:, s, j, :], strip[c][:, o:o + P], identb[:])
            nc.scalar.copy(xts[c][:, g], t[:])

        def add_up(c, g):
            t = ps_s.tile([P, PACK, 2, W_IMG], F32, name="stg")
            for j in range(PACK):
                left, right = xts[c][:, g, 0, j, :], xts[c][:, g, 1, j, :]
                nc.tensor.matmul(out=t[:, j, :, 0:OV], lhsT=left, rhs=band[:, 0], start=True, stop=False)
                nc.tensor.matmul(out=t[:, j, :, HW - 1:OV], lhsT=right, rhs=band[:, 1, :, 0:2], start=False, stop=True)
                nc.tensor.matmul(out=t[:, j, :, OV:W_IMG], lhsT=right, rhs=band[:, 1, :, 2:OV], start=True, stop=True)
            nc.scalar.copy(mean(c)[:, g * 2 * RL:(g + 1) * 2 * RL].rearrange("p (n j) -> p n j", j=PACK),
                           t[:].rearrange("p j r w -> p (r w) j"))

        def nrow(c):
            return ROWS - TAIL_ROWS if c == vs[-1] else ROWS

        def every2(c, first):
            n = nrow(c)
            return xgv[c][:, first * RL:(first + n) * RL].rearrange("p (k t c) -> p k t c", t=2, c=RL)

        def v_pv(c):
            pv[c] = const.tile([P, ROWS // 2, RL], F32, name="pv")
            nc.vector.tensor_tensor(out=pv[c][:, 0:nrow(c) // 2], in0=every2(c, 1)[:, :, 0, :], in1=every2(c, 1)[:, :, 1, :], op=ADD)

        def v_cv(c, par):
            if par == 0:
                cv[c] = const.tile([P, ROWS, PRL], F32, name="cv")
            cvk = cv[c][:, 0:nrow(c)].rearrange("p (k t) c -> p k t c", t=2)
            other = every2(c, 0)[:, :, 0, :] if par == 0 else every2(c, 2)[:, :, 1, :]
            nc.vector.tensor_tensor(out=cvk[:, :, par, PACK:PACK + RL], in0=other, in1=pv[c][:, 0:nrow(c) // 2], op=ADD)

        def v_pad(c):
            cvw = cv[c][:, 0:nrow(c)].rearrange("p r (w j) -> p r w j", j=PACK)
            nc.vector.tensor_copy(out=cvw[:, :, 0:W_IMG + 2:W_IMG + 1, :], in_=cvw[:, :, 1:W_IMG + 1:W_IMG - 1, :])

        def pairs(c, first):
            return cv[c][:, 0:nrow(c), first * PACK:first * PACK + RL].rearrange("p r (i t j) -> p r i t j", t=2, j=PACK)

        def v_ph(c):
            ph[c] = const.tile([P, ROWS, W_IMG // 2, PACK], F32, name="ph")
            nc.vector.tensor_tensor(out=ph[c][:, 0:nrow(c)], in0=pairs(c, 1)[:, :, :, 0, :], in1=pairs(c, 1)[:, :, :, 1, :], op=ADD)

        def v_box(c, half):
            if half == 0:
                box[c] = const.tile([P, CL], F32, name="box")
            b4 = box[c][:, 0:nrow(c) * RL].rearrange("p (r i t j) -> p r i t j", i=W_IMG // 2, t=2, j=PACK)
            outer = pairs(c, 0)[:, :, :, 0, :] if half == 0 else pairs(c, 2)[:, :, :, 1, :]
            nc.vector.tensor_tensor(out=b4[:, :, :, half, :], in0=outer, in1=ph[c][:, 0:nrow(c)], op=ADD)

        def v_fin(c, half):
            n = nrow(c) * RL // 2
            lo, hi = half * n, (half + 1) * n
            nc.vector.scalar_tensor_tensor(out=mean(c)[:, lo:hi], in0=xgv[c][:, RL + lo:RL + hi], scalar=-1.0,
                                           in1=box[c][:, lo:hi], op0=MULT, op1=ADD)

        def quant(c, parts):
            if c not in codes:
                codes[c] = tri.tile([P, 2, PIX], U32, name="codes", align_bytes=64)
                scales[c] = tri.tile([P, 2, PIX], U8, name="scales", align_bytes=64)
            if parts == 2:
                nc.vector.quantize_mx(out=codes[c][:].rearrange("p s n -> p (s n)").bitcast(FP8X4),
                                      scales=scales[c][:].rearrange("p s n -> p (s n)"), in_=xm[c][:].rearrange("p s n -> p (s n)"))

        def quant1(c, s, src):
            quant(c, 1)
            nc.vector.quantize_mx(out=codes[c][:, s, :].bitcast(FP8X4), scales=scales[c][:, s, :], in_=src)

        def mx(c, j):
            acc[(c, j)] = ps_a.tile([P, PIX], F32, name="acc")
            for s in range(2):
                cols = slice((s * PACK + j) * P, (s * PACK + j + 1) * P)
                nc.tensor.matmul_mx(out=acc[(c, j)][:],
                                    lhsT=wcodes[:, cols].bitcast(FP8X4), lhsT_scale=wscales[:, cols],
                                    rhs=codes[c][:, s, :].bitcast(FP8X4), rhs_scale=scales[c][:, s, :],
                                    start=(s == 0), stop=(s == 1))

        def warm(n):
            t = ps_s.tile([P, PIX], F32, name="stg")
            for i in range(n):
                nc.tensor.matmul_mx(out=t[:], lhsT=ocodes[:, 0:P].bitcast(FP8X4), lhsT_scale=oscales[:, 0:P],
                                    rhs=ocodes[:].bitcast(FP8X4), rhs_scale=oscales[:], start=True, stop=True)

        def v_gate():
            gate["b"] = dbl.tile([P, PACK], F32, name="bk")
            nc.vector.tensor_copy(out=gate["b"][:], in_=b16[:])

        def w_turn(eng, h):
            wf = w_sb[:].bitcast(F32).rearrange("p (j s q u) -> p j s q u", j=PACK, s=2, u=2)
            wgf = wg[:].bitcast(F32).rearrange("p (g m u) -> p g m u", m=P, u=2)
            pw = ps_a.tile([P, 2, 2, P], F32, name="acc")
            for gi in range(2):
                s, j = divmod(h * 2 + gi, PACK)
                for u in range(2):
                    nc.tensor.transpose(pw[:, gi, u, :], wf[:, j, s, :, u], ident[:])
            dst, src = wgf[:, h * 2:h * 2 + 2, :, :], pw[:].rearrange("p g u m -> p g m u")
            if eng == "v":
                nc.vector.tensor_copy(out=dst, in_=src)
            else:
                nc.scalar.copy(dst, src)

        order = []
        for m in range(4):
            order += [pes[3 * m]] + vs[max(m - 1, 0):m] + [pes[3 * m + 1], pes[3 * m + 2]]
        order += [vs[3]]
        units = [(c, j) for c in order for j in range(PACK)]
        s_units = units[len(units) - S_LAST:]
        st = {"done": 0, "mx": 0, "xb": 0, "ready": 0}

        def xb_to(n):
            while st["xb"] < min(n, len(units)):
                c, j = units[st["xb"]]
                xb[(c, j)] = four.tile([P, PIX], F32, name="xb")
                src = rows(c, 1, NB - 1)[:, j, :]
                if (c, j) in s_units:
                    nc.scalar.activation(out=xb[(c, j)][:], in_=src, func=IDENT, bias=b32[:, j:j + 1], scale=1.0)
                else:
                    nc.gpsimd.tensor_scalar(out=xb[(c, j)][:], in0=src, scalar1=1.0, scalar2=gate["b"][:, j:j + 1], op0=MULT, op1=ADD)
                st["xb"] += 1

        def mx_to(n):
            while st["mx"] < min(n, st["ready"], st["done"] + NACC):
                mx(units[st["mx"]][0], units[st["mx"]][1])
                st["mx"] += 1

        def finish():
            if st["done"] == st["mx"]:
                return
            c, j = units[st["done"]]
            n, cc = divmod(c, CPI)
            if j == 0:
                tt[c] = tri.tile([P, PACK, PIX], F32, name="tt", align_bytes=64)
            nc.vector.scalar_tensor_tensor(out=tt[c][:, j, :], in0=acc[(c, j)][:], scalar=nb32[:, j:j + 1],
                                           in1=xb[(c, j)][:], op0=MAX, op1=ADD)
            dst = ov[n, :, :, cc * PIX:(cc + 1) * PIX]
            if c == order[-1]:
                nc.sync.dma_start(out=dst[:, j, :], in_=tt[c][:, j, :])
            elif j == PACK - 1:
                nc.sync.dma_start(out=dst, in_=tt[c][:])
            st["done"] += 1

        def q(k):
            if 0 <= k < npe:
                quant(pes[k], 2)
                st["ready"] += PACK

        def qv(m):
            if 0 <= m < 4:
                c = vs[m]
                quant1(c, 0, xgv[c][:, RL:RL + CL])
                v_gate()
                quant1(c, 1, mean(c))
                st["ready"] += PACK

        VOPS = (lambda c: v_pv(c), lambda c: v_cv(c, 0), lambda c: v_cv(c, 1), lambda c: v_ph(c),
                lambda c: v_box(c, 0), lambda c: v_box(c, 1), lambda c: v_fin(c, 0), lambda c: v_fin(c, 1))

        def vop(m, i):
            if 0 <= m < 4 and i < len(VOPS):
                VOPS[i](vs[m])

        SEQ = ((turn, 0), (turn, 1), (turn, 2), (add_up, 0), (turn, 3), (add_up, 1), (add_up, 2), (add_up, 3))

        def group(k, i):
            if 0 <= k < npe:
                SEQ[i][0](pes[k], SEQ[i][1])

        def s_x(k, part):
            if 0 <= k < npe:
                interleave("s", pes[k], part, 2)

        def strip_of(k, eng="v"):
            if 0 <= k < npe:
                v_strip(pes[k], eng)

        warm(7)
        v_strip(pes[0])
        interleave("v", pes[0], 0, 1)
        nc.vector.tensor_copy(out=b32[:], in_=b16[:])
        nc.vector.tensor_scalar_mul(nb32[:], b16[:], -1.0)
        turn(pes[0], 0)
        warm(1)
        turn(pes[0], 1)
        warm(1)
        turn(pes[0], 2)
        warm(1)
        turn(pes[0], 3)
        interleave("v", vs[0], 0, 2)
        interleave("v", vs[0], 1, 2)
        w2 = w_sb[:].rearrange("p (j s k) -> p j s k", j=PACK, s=2)[:, :, 1, :]
        nc.vector.tensor_scalar_mul(w2, w2, 0.125)
        v_gate()
        xb_to(XB)
        w_turn("v", 0)
        add_up(pes[0], 0)
        v_strip(pes[1])
        w_turn("v", 1)
        add_up(pes[0], 1)
        add_up(pes[0], 2)
        w_turn("s", 2)
        add_up(pes[0], 3)
        w_turn("s", 3)
        v_pv(vs[0])
        v_strip(pes[2])
        warm(3)
        turn(pes[1], 0)
        warm(1)
        turn(pes[1], 1)
        warm(1)
        nc.vector.quantize_mx(out=wcodes[:].bitcast(FP8X4), scales=wscales[:], in_=wg[:])
        q(0)
        turn(pes[1], 2)
        warm(1)
        add_up(pes[1], 0)
        turn(pes[1], 3)
        mx_to(2)
        add_up(pes[1], 1)
        add_up(pes[1], 2)
        add_up(pes[1], 3)
        v_cv(vs[0], 0)
        interleave("v", pes[1], 0, 1)
        v_gate()

        early = 2
        for m in range(5):
            a = 3 * m
            for s in range(16):
                start = m == 0 and s < 8
                for i in range(24):
                    if 2 * i // 3 == s:
                        group(a + 2 + i // 8, i % 8)
                if s in (1, 3) and m > 0:
                    s_x(a + 2, s // 2)
                if s in (7, 9):
                    s_x(a + 3, (s - 7) // 2)
                if s in (12, 15):
                    s_x(a + 4, s // 15)
                if s in (5, 11) and m < 3:
                    interleave("s", vs[m + 1], s // 11, 2)
                if m == 3 and s == 4:
                    s_strip_tail(vs[-1])
                if m == 3 and s == 6:
                    turn(vs[-1], NWR - 1)
                if m == 3 and s == 8:
                    add_up(vs[-1], NWR - 1)
                if s == 0 and m >= 2:
                    strip_of(a + 3, "s")
                if s % 2 == 1:
                    if start:
                        v_gate()
                    if m == 0 and s == 3:
                        v_pad(vs[0])
                    vop(m, s // 2 + (early if m == 0 else 0))
                elif s == 0:
                    qv(m - 1)
                elif s == 2:
                    if m < 2:
                        strip_of(a + 3)
                elif s == 4:
                    q(a + 1)
                elif s == 6:
                    if m == 0:
                        interleave("v", pes[2], 0, 1)
                    elif m < 4:
                        v_pad(vs[m])
                elif s == 8:
                    strip_of(a + 4)
                elif s == 10:
                    q(a + 2)
                elif s == 12:
                    strip_of(a + 5)
                elif s == 14:
                    q(a + 3)
                if not start or s % 2 == 1:
                    xb_to(st["done"] + XB)
                    finish()
                mx_to(st["done"] + (2 if m < 3 else 4))
                if m == 3 and s >= 10 or m == 4 and s < 3:
                    warm(2)
